import numpy as np
import ml_dtypes


def mxq(x, axis, fmt="e4m3"):
    dtype, down = {"e4m3": (ml_dtypes.float8_e4m3fn, 7), "e5m2": (ml_dtypes.float8_e5m2, 14)}[fmt]
    v = np.moveaxis(np.asarray(x, np.float32).astype(ml_dtypes.bfloat16).astype(np.float64), axis, -1)
    blocks = v.reshape(v.shape[:-1] + (-1, 32))
    amax = np.abs(blocks).max(-1, keepdims=True)
    byte = np.maximum(np.where(amax > 0, np.frexp(amax)[1] - 1 + 127, 0) - down, 1)
    scale = np.exp2(byte - 127.0)
    codes = (blocks / scale).astype(np.float32).astype(dtype).astype(np.float64)
    return np.moveaxis((codes * scale).reshape(v.shape), -1, axis)


WIDE = False


def mx_kscale(k):
    if not WIDE:
        return np.ones(k)
    levels = np.array([10, -10, 5, -5, 0])
    a = np.random.permutation(np.resize(levels, k // 512 * 4)).reshape(k // 512, 4)
    idx = np.arange(k)
    return np.exp2(a[idx // 512, idx % 128 // 32])


BF16 = ml_dtypes.bfloat16


def bf(x):
    return np.asarray(x, np.float32).astype(BF16)


def f64(x):
    return np.asarray(x).astype(np.float64)


B, Q, S, D = 4, 128, 2048, 1024
EPS = 1e-8
SLOPE = 0.1
SMOOTH = 9.0


def l2norm(v, axis):
    return v / (np.sqrt(np.sum(v * v, axis=axis, keepdims=True) + EPS) + EPS)


def setup_inputs():
    s = mx_kscale(D)
    return {"query": bf(np.random.standard_normal((B, Q, D)) * 0.25 * s),
            "context": bf(np.random.standard_normal((B, S, D)) * 2.0 / s)}


def reference(query, context):
    q, c = f64(query), f64(context)
    attn = mxq(c, 2, "e4m3") @ mxq(q, 2, "e4m3").transpose(0, 2, 1)
    attn = np.where(attn >= 0.0, attn, SLOPE * attn)
    attn = l2norm(attn, 2)
    z = attn.transpose(0, 2, 1) * SMOOTH
    e = np.exp(z - z.max(2, keepdims=True))
    a = e / e.sum(2, keepdims=True)
    return mxq(a, 2, "e4m3") @ mxq(c, 1, "e4m3")

@@ -1,0 +1,214 @@
+from contextlib import ExitStack
+
+import concourse.mybir as mybir
+from concourse.masks import make_identity
+
+F32 = mybir.dt.float32
+BF16 = mybir.dt.bfloat16
+U32 = mybir.dt.uint32
+U8 = mybir.dt.uint8
+FP8X4 = mybir.dt.float8_e4m3fn_x4
+ALU = mybir.AluOpType
+ACT = mybir.ActivationFunctionType
+
+B, Q, S, D = 4, 128, 2048, 1024
+EPS = 1e-8
+SLOPE = 0.1
+SMOOTH = 9.0
+
+P = 128
+PACK = 4
+K_PASS = P * PACK
+GROUPS = S // K_PASS
+D_PASSES = D // K_PASS
+BANK = 512
+D_BANKS = D // BANK
+
+SCALAR_COLS = 128
+
+FLOPS = 2 * 2 * B * Q * S * D
+
+
+def turn_features_onto_partitions(nc, psum_turn, rows_words, identity, grouped_words):
+    turned = psum_turn.tile([P, D_PASSES, 2, P], F32)
+    for c in range(D_PASSES):
+        for u in range(2):
+            first = (2 * c + u) * P
+            nc.tensor.transpose(turned[:, c, u, :], rows_words[:, first : first + P], identity[:])
+    nc.scalar.copy(out=grouped_words, in_=turned[:].rearrange("p c u r -> p c r u"))
+
+
+def tile_smcmr_pa_t_kernel(tc, query, context, out):
+    nc = tc.nc
+    with ExitStack() as stack:
+        const = stack.enter_context(tc.tile_pool(name="const", bufs=1))
+        token_pool = stack.enter_context(tc.tile_pool(name="tokens", bufs=9))
+        query_pool = stack.enter_context(tc.tile_pool(name="query", bufs=2))
+        stage = stack.enter_context(tc.tile_pool(name="stage", bufs=2))
+        keep = stack.enter_context(tc.tile_pool(name="keep", bufs=2))
+        soft = stack.enter_context(tc.tile_pool(name="soft", bufs=3))
+        small = stack.enter_context(tc.tile_pool(name="small", bufs=4))
+        results = stack.enter_context(tc.tile_pool(name="results", bufs=4))
+        psum_turn = stack.enter_context(tc.psum_pool(name="psum_turn", bufs=3))
+        psum_score = stack.enter_context(tc.psum_pool(name="psum_score", bufs=2))
+        psum_sum = stack.enter_context(tc.psum_pool(name="psum_sum", bufs=1))
+        psum_out = stack.enter_context(tc.psum_pool(name="psum_out", bufs=2))
+
+        identity = const.tile([P, P], F32)
+        make_identity(nc, identity[:])
+        ones = const.tile([P, P], F32)
+        nc.vector.memset(ones[:], 1.0)
+        half = const.tile([P, PACK], F32)
+        nc.vector.memset(half[:], 0.5)
+        minus_one = const.tile([P, PACK], F32)
+        nc.vector.memset(minus_one[:], -1.0)
+
+        for b in range(B):
+            q_rows = query_pool.tile([P, D], BF16)
+            nc.sync.dma_start(out=q_rows[:], in_=query[b])
+            q_grouped = query_pool.tile([P, D_PASSES, Q, PACK], BF16, align_bytes=64)
+            turn_features_onto_partitions(
+                nc, psum_turn, q_rows[:].bitcast(F32), identity, q_grouped[:].bitcast(F32)
+            )
+            q_codes = query_pool.tile([P, D_PASSES, Q], U32, align_bytes=64)
+            q_scales = query_pool.tile([P, D_PASSES, Q], U8, align_bytes=64)
+            nc.vector.quantize_mx(
+                out=q_codes[:].rearrange("p c q -> p (c q)").bitcast(FP8X4),
+                scales=q_scales[:].rearrange("p c q -> p (c q)"),
+                in_=q_grouped[:].rearrange("p c q t -> p (c q t)"),
+            )
+
+            expo = keep.tile([P, GROUPS, PACK, Q], F32)
+            sums = psum_sum.tile([P, Q], F32)
+            c_codes = keep.tile([P, GROUPS, D], U32, align_bytes=64)
+            c_scales = keep.tile([P, GROUPS, D], U8, align_bytes=64)
+
+            group_rows = []
+            for g in range(GROUPS):
+                rows = token_pool.tile([P, PACK, D], BF16)
+                nc.sync.dma_start(
+                    out=rows[:],
+                    in_=context[b, g * K_PASS : (g + 1) * K_PASS, :].rearrange("(p j) d -> p j d", j=PACK),
+                )
+                group_rows.append(rows)
+
+                t_grouped = stage.tile([P, PACK, D_PASSES, P, PACK], BF16, align_bytes=64)
+                for j in range(PACK):
+                    turn_features_onto_partitions(
+                        nc, psum_turn, rows[:, j, :].bitcast(F32), identity, t_grouped[:, j].bitcast(F32)
+                    )
+                t_codes = stage.tile([P, PACK, D_PASSES, P], U32, align_bytes=64)
+                t_scales = stage.tile([P, PACK, D_PASSES, P], U8, align_bytes=64)
+                nc.vector.quantize_mx(
+                    out=t_codes[:].rearrange("p j c r -> p (j c r)").bitcast(FP8X4),
+                    scales=t_scales[:].rearrange("p j c r -> p (j c r)"),
+                    in_=t_grouped[:].rearrange("p j c r t -> p (j c r t)"),
+                )
+                scores = psum_score.tile([P, PACK, Q], F32)
+                for j in range(PACK):
+                    for c in range(D_PASSES):
+                        nc.tensor.matmul_mx(
+                            out=scores[:, j, :],
+                            lhsT=t_codes[:, j, c, :].bitcast(FP8X4),
+                            lhsT_scale=t_scales[:, j, c, :],
+                            rhs=q_codes[:, c, :].bitcast(FP8X4),
+                            rhs_scale=q_scales[:, c, :],
+                            start=(c == 0),
+                            stop=(c == D_PASSES - 1),
+                        )
+
+                damped = soft.tile([P, PACK, Q], F32)
+                nc.scalar.mul(out=damped[:], in_=scores[:], mul=SLOPE)
+                leaky = soft.tile([P, PACK, Q], F32)
+                nc.vector.tensor_tensor(out=leaky[:], in0=scores[:], in1=damped[:], op=ALU.max)
+
+                squares = small.tile([P, PACK], F32)
+                for j in range(PACK):
+                    unused = soft.tile([P, Q], F32)
+                    nc.scalar.activation(
+                        out=unused[:], in_=leaky[:, j, :], func=ACT.Square, accum_out=squares[:, j : j + 1]
+                    )
+                norm = small.tile([P, PACK], F32)
+                nc.gpsimd.tensor_scalar(
+                    out=norm[:], in0=squares[:], scalar1=1.0, scalar2=EPS, op0=ALU.mult, op1=ALU.add
+                )
+                root = small.tile([P, PACK], F32)
+                nc.gpsimd.tensor_tensor(out=root[:], in0=norm[:], in1=half[:], op=ALU.pow)
+                ninth = small.tile([P, PACK], F32)
+                nc.gpsimd.tensor_scalar(
+                    out=ninth[:], in0=root[:], scalar1=EPS, scalar2=1.0 / SMOOTH, op0=ALU.add, op1=ALU.mult
+                )
+                steep = small.tile([P, PACK], F32)
+                nc.gpsimd.tensor_tensor(out=steep[:], in0=ninth[:], in1=minus_one[:], op=ALU.pow)
+
+                for j in range(PACK):
+                    nc.scalar.activation(
+                        out=expo[:, g, j, :],
+                        in_=leaky[:, j, :],
+                        func=ACT.Exp,
+                        scale=steep[:, j : j + 1],
+                        bias=-SMOOTH,
+                    )
+                    nc.tensor.matmul(
+                        out=sums[:],
+                        lhsT=ones[:],
+                        rhs=expo[:, g, j, :],
+                        start=(g == 0 and j == 0),
+                        stop=(g == GROUPS - 1 and j == PACK - 1),
+                    )
+
+            for g in range(GROUPS):
+                rows = group_rows[g]
+                regrouped = stage.tile([P, D, PACK], BF16, align_bytes=64)
+                split = D - SCALAR_COLS
+                nc.vector.tensor_copy(
+                    out=regrouped[:, :split, :].rearrange("p (n i) j -> p n j i", i=4),
+                    in_=rows[:, :, :split].rearrange("p j (n i) -> p n j i", i=4),
+                )
+                nc.scalar.copy(
+                    out=regrouped[:, split:, :].rearrange("p (n i) j -> p n j i", i=4),
+                    in_=rows[:, :, split:].rearrange("p j (n i) -> p n j i", i=4),
+                )
+                nc.vector.quantize_mx(
+                    out=c_codes[:, g, :].bitcast(FP8X4),
+                    scales=c_scales[:, g, :],
+                    in_=regrouped[:].rearrange("p d j -> p (d j)"),
+                )
+
+            inverse = small.tile([P, Q], F32)
+            nc.vector.reciprocal(out=inverse[:], in_=sums[:])
+            weights = stage.tile([P, GROUPS, Q, PACK], BF16, align_bytes=64)
+            for g in range(GROUPS):
+                nc.vector.tensor_tensor(
+                    out=weights[:, g],
+                    in0=expo[:, g].rearrange("p j q -> p q j"),
+                    in1=inverse[:].unsqueeze(2).to_broadcast([P, Q, PACK]),
+                    op=ALU.mult,
+                )
+            w_codes = stage.tile([P, GROUPS, Q], U32, align_bytes=64)
+            w_scales = stage.tile([P, GROUPS, Q], U8, align_bytes=64)
+            nc.vector.quantize_mx(
+                out=w_codes[:].rearrange("p g q -> p (g q)").bitcast(FP8X4),
+                scales=w_scales[:].rearrange("p g q -> p (g q)"),
+                in_=weights[:].rearrange("p g q j -> p (g q j)"),
+            )
+
+            for h in range(D_BANKS):
+                columns = slice(h * BANK, (h + 1) * BANK)
+                acc = psum_out.tile([P, BANK], F32)
+                for g in range(GROUPS):
+                    nc.tensor.matmul_mx(
+                        out=acc[:],
+                        lhsT=w_codes[:, g, :].bitcast(FP8X4),
+                        lhsT_scale=w_scales[:, g, :],
+                        rhs=c_codes[:, g, columns].bitcast(FP8X4),
+                        rhs_scale=c_scales[:, g, columns],
+                        start=(g == 0),
+                        stop=(g == GROUPS - 1),
+                    )
+                result = results.tile([P, BANK], F32)
+                if h % 2 == 0:
+                    nc.scalar.copy(out=result[:], in_=acc[:])
+                else:
+                    nc.vector.tensor_copy(out=result[:], in_=acc[:])
+                nc.sync.dma_start(out=out[b, :, columns], in_=result[:])

@@ -20,39 +20,41 @@ P = 128
 PACK = 4
 K_PASS = P * PACK
 GROUPS = S // K_PASS
+ALL_GROUPS = B * GROUPS
 D_PASSES = D // K_PASS
 BANK = 512
 D_BANKS = D // BANK
 
-SCALAR_COLS = 128
+SCALAR_COLS = 192
+
+PREFETCH = 3
+TURN_LEAD = 4
+NORM_LAG = 1
+EXP_LAG = 5
+SUM_LAG = EXP_LAG + 1
+WEIGHT_LAG = SUM_LAG + GROUPS - 1
+OUT_LAG = WEIGHT_LAG + 1
+STORE_LAG = OUT_LAG + 1
+REGROUP_LAG = 5
+CODE_LAG = REGROUP_LAG + 1
 
 FLOPS = 2 * 2 * B * Q * S * D
-
-
-def turn_features_onto_partitions(nc, psum_turn, rows_words, identity, grouped_words):
-    turned = psum_turn.tile([P, D_PASSES, 2, P], F32)
-    for c in range(D_PASSES):
-        for u in range(2):
-            first = (2 * c + u) * P
-            nc.tensor.transpose(turned[:, c, u, :], rows_words[:, first : first + P], identity[:])
-    nc.scalar.copy(out=grouped_words, in_=turned[:].rearrange("p c u r -> p c r u"))
 
 
 def tile_smcmr_pa_t_kernel(tc, query, context, out):
     nc = tc.nc
     with ExitStack() as stack:
+        stack.enter_context(tc.manual_schedule())
         const = stack.enter_context(tc.tile_pool(name="const", bufs=1))
-        token_pool = stack.enter_context(tc.tile_pool(name="tokens", bufs=9))
-        query_pool = stack.enter_context(tc.tile_pool(name="query", bufs=2))
+        token_pool = stack.enter_context(tc.tile_pool(name="tokens", bufs=PREFETCH + REGROUP_LAG + 2))
         stage = stack.enter_context(tc.tile_pool(name="stage", bufs=2))
         keep = stack.enter_context(tc.tile_pool(name="keep", bufs=2))
-        soft = stack.enter_context(tc.tile_pool(name="soft", bufs=3))
-        small = stack.enter_context(tc.tile_pool(name="small", bufs=4))
-        results = stack.enter_context(tc.tile_pool(name="results", bufs=4))
-        psum_turn = stack.enter_context(tc.psum_pool(name="psum_turn", bufs=3))
-        psum_score = stack.enter_context(tc.psum_pool(name="psum_score", bufs=2))
+        soft = stack.enter_context(tc.tile_pool(name="soft", bufs=EXP_LAG + 1))
+        results = stack.enter_context(tc.tile_pool(name="results", bufs=2 * D_BANKS))
+        psum_turn = stack.enter_context(tc.psum_pool(name="psum_turn", bufs=TURN_LEAD))
+        psum_score = stack.enter_context(tc.psum_pool(name="psum_score", bufs=1))
         psum_sum = stack.enter_context(tc.psum_pool(name="psum_sum", bufs=1))
-        psum_out = stack.enter_context(tc.psum_pool(name="psum_out", bufs=2))
+        psum_out = stack.enter_context(tc.psum_pool(name="psum_out", bufs=D_BANKS))
 
         identity = const.tile([P, P], F32)
         make_identity(nc, identity[:])
@@ -63,152 +65,271 @@ def tile_smcmr_pa_t_kernel(tc, query, context, out):
         minus_one = const.tile([P, PACK], F32)
         nc.vector.memset(minus_one[:], -1.0)
 
-        for b in range(B):
-            q_rows = query_pool.tile([P, D], BF16)
-            nc.sync.dma_start(out=q_rows[:], in_=query[b])
-            q_grouped = query_pool.tile([P, D_PASSES, Q, PACK], BF16, align_bytes=64)
-            turn_features_onto_partitions(
-                nc, psum_turn, q_rows[:].bitcast(F32), identity, q_grouped[:].bitcast(F32)
-            )
-            q_codes = query_pool.tile([P, D_PASSES, Q], U32, align_bytes=64)
-            q_scales = query_pool.tile([P, D_PASSES, Q], U8, align_bytes=64)
-            nc.vector.quantize_mx(
-                out=q_codes[:].rearrange("p c q -> p (c q)").bitcast(FP8X4),
-                scales=q_scales[:].rearrange("p c q -> p (c q)"),
-                in_=q_grouped[:].rearrange("p c q t -> p (c q t)"),
-            )
+        rows_of, turned_of, grouped_of, token_codes_of, scores_of = {}, {}, {}, {}, {}
+        damped_of, leaky_of, steep_of, regrouped_of, weight_codes_of = {}, {}, {}, {}, {}
+        expo_of, sums_of, inverse_of, context_codes_of, acc_of = {}, {}, {}, {}, {}
 
-            expo = keep.tile([P, GROUPS, PACK, Q], F32)
-            sums = psum_sum.tile([P, Q], F32)
-            c_codes = keep.tile([P, GROUPS, D], U32, align_bytes=64)
-            c_scales = keep.tile([P, GROUPS, D], U8, align_bytes=64)
+        def is_group(i):
+            return 0 <= i < ALL_GROUPS
 
-            group_rows = []
-            for g in range(GROUPS):
-                rows = token_pool.tile([P, PACK, D], BF16)
-                nc.sync.dma_start(
-                    out=rows[:],
-                    in_=context[b, g * K_PASS : (g + 1) * K_PASS, :].rearrange("(p j) d -> p j d", j=PACK),
-                )
-                group_rows.append(rows)
+        def turn(key, rows_words):
+            turned = psum_turn.tile([P, D_PASSES, 2, P], F32)
+            for c in range(D_PASSES):
+                for u in range(2):
+                    first = (2 * c + u) * P
+                    nc.tensor.transpose(turned[:, c, u, :], rows_words[:, first : first + P], identity[:])
+            turned_of[key] = turned
 
+        def copy_turned(key, grouped_words):
+            nc.scalar.copy(out=grouped_words, in_=turned_of[key][:].rearrange("p c u r -> p c r u"))
+
+        def turn_tokens(tile_number):
+            i, j = divmod(tile_number, PACK)
+            if is_group(i):
+                turn(tile_number, rows_of[i][:, j, :].bitcast(F32))
+
+        def copy_turned_tokens(i, j):
+            if not is_group(i):
+                return
+            if j == 0:
                 t_grouped = stage.tile([P, PACK, D_PASSES, P, PACK], BF16, align_bytes=64)
-                for j in range(PACK):
-                    turn_features_onto_partitions(
-                        nc, psum_turn, rows[:, j, :].bitcast(F32), identity, t_grouped[:, j].bitcast(F32)
-                    )
-                t_codes = stage.tile([P, PACK, D_PASSES, P], U32, align_bytes=64)
-                t_scales = stage.tile([P, PACK, D_PASSES, P], U8, align_bytes=64)
-                nc.vector.quantize_mx(
-                    out=t_codes[:].rearrange("p j c r -> p (j c r)").bitcast(FP8X4),
-                    scales=t_scales[:].rearrange("p j c r -> p (j c r)"),
-                    in_=t_grouped[:].rearrange("p j c r t -> p (j c r t)"),
-                )
-                scores = psum_score.tile([P, PACK, Q], F32)
-                for j in range(PACK):
-                    for c in range(D_PASSES):
-                        nc.tensor.matmul_mx(
-                            out=scores[:, j, :],
-                            lhsT=t_codes[:, j, c, :].bitcast(FP8X4),
-                            lhsT_scale=t_scales[:, j, c, :],
-                            rhs=q_codes[:, c, :].bitcast(FP8X4),
-                            rhs_scale=q_scales[:, c, :],
-                            start=(c == 0),
-                            stop=(c == D_PASSES - 1),
-                        )
+                grouped_of[i] = t_grouped
+            copy_turned(PACK * i + j, grouped_of[i][:, j].bitcast(F32))
 
-                damped = soft.tile([P, PACK, Q], F32)
-                nc.scalar.mul(out=damped[:], in_=scores[:], mul=SLOPE)
-                leaky = soft.tile([P, PACK, Q], F32)
-                nc.vector.tensor_tensor(out=leaky[:], in0=scores[:], in1=damped[:], op=ALU.max)
+        def load(i):
+            if not is_group(i):
+                return
+            b, g = divmod(i, GROUPS)
+            rows = token_pool.tile([P, PACK, D], BF16)
+            nc.sync.dma_start(
+                out=rows[:], in_=context[b, g * K_PASS : (g + 1) * K_PASS, :].rearrange("(p j) d -> p j d", j=PACK)
+            )
+            rows_of[i] = rows
 
-                squares = small.tile([P, PACK], F32)
-                for j in range(PACK):
-                    unused = soft.tile([P, Q], F32)
-                    nc.scalar.activation(
-                        out=unused[:], in_=leaky[:, j, :], func=ACT.Square, accum_out=squares[:, j : j + 1]
-                    )
-                norm = small.tile([P, PACK], F32)
-                nc.gpsimd.tensor_scalar(
-                    out=norm[:], in0=squares[:], scalar1=1.0, scalar2=EPS, op0=ALU.mult, op1=ALU.add
-                )
-                root = small.tile([P, PACK], F32)
-                nc.gpsimd.tensor_tensor(out=root[:], in0=norm[:], in1=half[:], op=ALU.pow)
-                ninth = small.tile([P, PACK], F32)
-                nc.gpsimd.tensor_scalar(
-                    out=ninth[:], in0=root[:], scalar1=EPS, scalar2=1.0 / SMOOTH, op0=ALU.add, op1=ALU.mult
-                )
-                steep = small.tile([P, PACK], F32)
-                nc.gpsimd.tensor_tensor(out=steep[:], in0=ninth[:], in1=minus_one[:], op=ALU.pow)
-
-                for j in range(PACK):
-                    nc.scalar.activation(
-                        out=expo[:, g, j, :],
-                        in_=leaky[:, j, :],
-                        func=ACT.Exp,
-                        scale=steep[:, j : j + 1],
-                        bias=-SMOOTH,
-                    )
-                    nc.tensor.matmul(
-                        out=sums[:],
-                        lhsT=ones[:],
-                        rhs=expo[:, g, j, :],
-                        start=(g == 0 and j == 0),
-                        stop=(g == GROUPS - 1 and j == PACK - 1),
-                    )
-
-            for g in range(GROUPS):
-                rows = group_rows[g]
-                regrouped = stage.tile([P, D, PACK], BF16, align_bytes=64)
-                split = D - SCALAR_COLS
-                nc.vector.tensor_copy(
-                    out=regrouped[:, :split, :].rearrange("p (n i) j -> p n j i", i=4),
-                    in_=rows[:, :, :split].rearrange("p j (n i) -> p n j i", i=4),
-                )
-                nc.scalar.copy(
-                    out=regrouped[:, split:, :].rearrange("p (n i) j -> p n j i", i=4),
-                    in_=rows[:, :, split:].rearrange("p j (n i) -> p n j i", i=4),
-                )
-                nc.vector.quantize_mx(
-                    out=c_codes[:, g, :].bitcast(FP8X4),
-                    scales=c_scales[:, g, :],
-                    in_=regrouped[:].rearrange("p d j -> p (d j)"),
-                )
-
-            inverse = small.tile([P, Q], F32)
-            nc.vector.reciprocal(out=inverse[:], in_=sums[:])
-            weights = stage.tile([P, GROUPS, Q, PACK], BF16, align_bytes=64)
-            for g in range(GROUPS):
-                nc.vector.tensor_tensor(
-                    out=weights[:, g],
-                    in0=expo[:, g].rearrange("p j q -> p q j"),
-                    in1=inverse[:].unsqueeze(2).to_broadcast([P, Q, PACK]),
-                    op=ALU.mult,
-                )
-            w_codes = stage.tile([P, GROUPS, Q], U32, align_bytes=64)
-            w_scales = stage.tile([P, GROUPS, Q], U8, align_bytes=64)
+        def quantise_tokens(i):
+            if not is_group(i):
+                return
+            t_codes = stage.tile([P, PACK, D_PASSES, P], U32, align_bytes=64)
+            t_scales = stage.tile([P, PACK, D_PASSES, P], U8, align_bytes=64)
             nc.vector.quantize_mx(
-                out=w_codes[:].rearrange("p g q -> p (g q)").bitcast(FP8X4),
-                scales=w_scales[:].rearrange("p g q -> p (g q)"),
-                in_=weights[:].rearrange("p g q j -> p (g q j)"),
+                out=t_codes[:].rearrange("p j c r -> p (j c r)").bitcast(FP8X4),
+                scales=t_scales[:].rearrange("p j c r -> p (j c r)"),
+                in_=grouped_of[i][:].rearrange("p j c r t -> p (j c r t)"),
+            )
+            token_codes_of[i] = (t_codes, t_scales)
+
+        def first_matmul(i):
+            if not is_group(i):
+                return
+            b = i // GROUPS
+            t_codes, t_scales = token_codes_of[i]
+            scores = psum_score.tile([P, PACK, Q], F32)
+            for j in range(PACK):
+                for c in range(D_PASSES):
+                    nc.tensor.matmul_mx(
+                        out=scores[:, j, :],
+                        lhsT=t_codes[:, j, c, :].bitcast(FP8X4),
+                        lhsT_scale=t_scales[:, j, c, :],
+                        rhs=q_codes[:, b, c, :].bitcast(FP8X4),
+                        rhs_scale=q_scales[:, b, c, :],
+                        start=(c == 0),
+                        stop=(c == D_PASSES - 1),
+                    )
+            scores_of[i] = scores
+
+        def damp(i):
+            if not is_group(i):
+                return
+            damped = stage.tile([P, PACK, Q], F32)
+            nc.scalar.mul(out=damped[:], in_=scores_of[i][:], mul=SLOPE)
+            damped_of[i] = damped
+
+        def leaky_relu(i):
+            if not is_group(i):
+                return
+            leaky = soft.tile([P, PACK, Q], F32)
+            nc.vector.tensor_tensor(out=leaky[:], in0=scores_of[i][:], in1=damped_of[i][:], op=ALU.max)
+            leaky_of[i] = leaky
+
+        def norm_factor(i):
+            if not is_group(i):
+                return
+            squares = soft.tile([P, PACK], F32)
+            for j in range(PACK):
+                unused = stage.tile([P, Q], F32)
+                nc.scalar.activation(
+                    out=unused[:], in_=leaky_of[i][:, j, :], func=ACT.Square, accum_out=squares[:, j : j + 1]
+                )
+            norm = soft.tile([P, PACK], F32)
+            nc.gpsimd.tensor_scalar(out=norm[:], in0=squares[:], scalar1=1.0, scalar2=EPS, op0=ALU.mult, op1=ALU.add)
+            root = soft.tile([P, PACK], F32)
+            nc.gpsimd.tensor_tensor(out=root[:], in0=norm[:], in1=half[:], op=ALU.pow)
+            ninth = soft.tile([P, PACK], F32)
+            nc.gpsimd.tensor_scalar(
+                out=ninth[:], in0=root[:], scalar1=EPS, scalar2=1.0 / SMOOTH, op0=ALU.add, op1=ALU.mult
+            )
+            steep = soft.tile([P, PACK], F32)
+            nc.gpsimd.tensor_tensor(out=steep[:], in0=ninth[:], in1=minus_one[:], op=ALU.pow)
+            steep_of[i] = steep
+
+        def exponentials(i):
+            if not is_group(i):
+                return
+            b, g = divmod(i, GROUPS)
+            if g == 0:
+                expo = keep.tile([P, GROUPS, PACK, Q], F32)
+                expo_of[b] = expo
+            leaky, steep = leaky_of[i], steep_of[i]
+            for j in range(PACK):
+                nc.scalar.activation(
+                    out=expo_of[b][:, g, j, :],
+                    in_=leaky[:, j, :],
+                    func=ACT.Exp,
+                    scale=steep[:, j : j + 1],
+                    bias=-SMOOTH,
+                )
+
+        def add_to_sums(i, j):
+            if not is_group(i):
+                return
+            b, g = divmod(i, GROUPS)
+            if g == 0 and j == 0:
+                sums = psum_sum.tile([P, Q], F32)
+                sums_of[b] = sums
+            nc.tensor.matmul(
+                out=sums_of[b][:],
+                lhsT=ones[:],
+                rhs=expo_of[b][:, g, j, :],
+                start=(g == 0 and j == 0),
+                stop=(g == GROUPS - 1 and j == PACK - 1),
             )
 
+        def regroup(i, engine_copy, first, last):
+            engine_copy(
+                out=regrouped_of[i][:, first:last, :].rearrange("p (n k) j -> p n j k", k=4),
+                in_=rows_of[i][:, :, first:last].rearrange("p j (n k) -> p n j k", k=4),
+            )
+
+        def regroup_on_vector(i):
+            if not is_group(i):
+                return
+            regrouped = stage.tile([P, D, PACK], BF16, align_bytes=64)
+            regrouped_of[i] = regrouped
+            regroup(i, nc.vector.tensor_copy, 0, D - SCALAR_COLS)
+
+        def regroup_on_scalar(i):
+            if not is_group(i):
+                return
+            regroup(i, nc.scalar.copy, D - SCALAR_COLS, D)
+
+        def quantise_context(i):
+            if not is_group(i):
+                return
+            b, g = divmod(i, GROUPS)
+            if g == 0:
+                c_codes = keep.tile([P, GROUPS, D], U32, align_bytes=64)
+                c_scales = keep.tile([P, GROUPS, D], U8, align_bytes=64)
+                context_codes_of[b] = (c_codes, c_scales)
+            c_codes, c_scales = context_codes_of[b]
+            nc.vector.quantize_mx(
+                out=c_codes[:, g, :].bitcast(FP8X4),
+                scales=c_scales[:, g, :],
+                in_=regrouped_of[i][:].rearrange("p d j -> p (d j)"),
+            )
+
+        def normalise(i):
+            if not is_group(i):
+                return None
+            b, g = divmod(i, GROUPS)
+            if g == 0:
+                inverse = stage.tile([P, Q], F32)
+                nc.vector.reciprocal(out=inverse[:], in_=sums_of[b][:])
+                inverse_of[b] = inverse
+            weights = stage.tile([P, Q, PACK], BF16, align_bytes=64)
+            nc.vector.tensor_tensor(
+                out=weights[:],
+                in0=expo_of[b][:, g].rearrange("p j q -> p q j"),
+                in1=inverse_of[b][:].unsqueeze(2).to_broadcast([P, Q, PACK]),
+                op=ALU.mult,
+            )
+            return weights
+
+        def quantise_weights(i, weights):
+            if not is_group(i):
+                return
+            w_codes = soft.tile([P, Q], U32, align_bytes=64)
+            w_scales = soft.tile([P, Q], U8, align_bytes=64)
+            nc.vector.quantize_mx(
+                out=w_codes[:].bitcast(FP8X4), scales=w_scales[:], in_=weights[:].rearrange("p q j -> p (q j)")
+            )
+            weight_codes_of[i] = (w_codes, w_scales)
+
+        def second_matmul(i):
+            if not is_group(i):
+                return
+            b, g = divmod(i, GROUPS)
+            w_codes, w_scales = weight_codes_of[i]
+            c_codes, c_scales = context_codes_of[b]
             for h in range(D_BANKS):
-                columns = slice(h * BANK, (h + 1) * BANK)
-                acc = psum_out.tile([P, BANK], F32)
-                for g in range(GROUPS):
-                    nc.tensor.matmul_mx(
-                        out=acc[:],
-                        lhsT=w_codes[:, g, :].bitcast(FP8X4),
-                        lhsT_scale=w_scales[:, g, :],
-                        rhs=c_codes[:, g, columns].bitcast(FP8X4),
-                        rhs_scale=c_scales[:, g, columns],
-                        start=(g == 0),
-                        stop=(g == GROUPS - 1),
-                    )
+                if g == 0:
+                    acc = psum_out.tile([P, BANK], F32)
+                    acc_of[(b, h)] = acc
+                nc.tensor.matmul_mx(
+                    out=acc_of[(b, h)][:],
+                    lhsT=w_codes[:].bitcast(FP8X4),
+                    lhsT_scale=w_scales[:],
+                    rhs=c_codes[:, g, h * BANK : (h + 1) * BANK].bitcast(FP8X4),
+                    rhs_scale=c_scales[:, g, h * BANK : (h + 1) * BANK],
+                    start=(g == 0),
+                    stop=(g == GROUPS - 1),
+                )
+
+        def store(i):
+            if not is_group(i) or i % GROUPS != GROUPS - 1:
+                return
+            b = i // GROUPS
+            for h in range(D_BANKS):
                 result = results.tile([P, BANK], F32)
                 if h % 2 == 0:
-                    nc.scalar.copy(out=result[:], in_=acc[:])
+                    nc.scalar.copy(out=result[:], in_=acc_of[(b, h)][:])
                 else:
-                    nc.vector.tensor_copy(out=result[:], in_=acc[:])
-                nc.sync.dma_start(out=out[b, :, columns], in_=result[:])
+                    nc.vector.tensor_copy(out=result[:], in_=acc_of[(b, h)][:])
+                nc.sync.dma_start(out=out[b, :, h * BANK : (h + 1) * BANK], in_=result[:])
+
+        q_rows = token_pool.tile([P, B, D], BF16, tag="rows")
+        nc.sync.dma_start(out=q_rows[:], in_=query.rearrange("b q d -> q b d"))
+        for i in range(PREFETCH):
+            load(i)
+        q_grouped = const.tile([P, B, D_PASSES, Q, PACK], BF16, align_bytes=64)
+        for b in range(B):
+            turn(("query", b), q_rows[:, b, :].bitcast(F32))
+            copy_turned(("query", b), q_grouped[:, b].bitcast(F32))
+        q_codes = const.tile([P, B, D_PASSES, Q], U32, align_bytes=64)
+        q_scales = const.tile([P, B, D_PASSES, Q], U8, align_bytes=64)
+        nc.vector.quantize_mx(
+            out=q_codes[:].rearrange("p b c q -> p (b c q)").bitcast(FP8X4),
+            scales=q_scales[:].rearrange("p b c q -> p (b c q)"),
+            in_=q_grouped[:].rearrange("p b c q t -> p (b c q t)"),
+        )
+        for tile_number in range(TURN_LEAD):
+            turn_tokens(tile_number)
+
+        for n in range(ALL_GROUPS + STORE_LAG + 1):
+            load(n + PREFETCH)
+            store(n - STORE_LAG)
+            leaky_relu(n - NORM_LAG)
+            for j in range(PACK):
+                copy_turned_tokens(n, j)
+                turn_tokens(PACK * n + j + TURN_LEAD)
+                add_to_sums(n - SUM_LAG, j)
+            second_matmul(n - OUT_LAG)
+            regroup_on_vector(n - REGROUP_LAG)
+            quantise_tokens(n)
+            first_matmul(n)
+            norm_factor(n - NORM_LAG)
+            exponentials(n - EXP_LAG)
+            regroup_on_scalar(n - REGROUP_LAG)
+            weights = normalise(n - WEIGHT_LAG)
+            quantise_context(n - CODE_LAG)
+            quantise_weights(n - WEIGHT_LAG, weights)
+            damp(n)

@@ -28,14 +28,16 @@ D_BANKS = D // BANK
 SCALAR_COLS = 192
 
 PREFETCH = 3
-TURN_LEAD = 4
-NORM_LAG = 1
-EXP_LAG = 5
-SUM_LAG = EXP_LAG + 1
-WEIGHT_LAG = SUM_LAG + GROUPS - 1
+TURN_LEAD = 3
+SCORE_LAG = 1
+LEAKY_LAG = 2
+SQUARE_LAG = 3
+STEEP_LAG = 5
+EXP_LAG = 6
+WEIGHT_LAG = EXP_LAG + GROUPS
 OUT_LAG = WEIGHT_LAG + 1
 STORE_LAG = OUT_LAG + 1
-REGROUP_LAG = 5
+REGROUP_LAG = 1
 CODE_LAG = REGROUP_LAG + 1
 
 FLOPS = 2 * 2 * B * Q * S * D
@@ -49,10 +51,11 @@ def tile_smcmr_pa_t_kernel(tc, query, context, out):
         token_pool = stack.enter_context(tc.tile_pool(name="tokens", bufs=PREFETCH + REGROUP_LAG + 2))
         stage = stack.enter_context(tc.tile_pool(name="stage", bufs=2))
         keep = stack.enter_context(tc.tile_pool(name="keep", bufs=2))
-        soft = stack.enter_context(tc.tile_pool(name="soft", bufs=EXP_LAG + 1))
-        results = stack.enter_context(tc.tile_pool(name="results", bufs=2 * D_BANKS))
+        codes = stack.enter_context(tc.tile_pool(name="codes", bufs=B))
+        soft = stack.enter_context(tc.tile_pool(name="soft", bufs=EXP_LAG - LEAKY_LAG + 1))
+        results = stack.enter_context(tc.tile_pool(name="results", bufs=D_BANKS))
         psum_turn = stack.enter_context(tc.psum_pool(name="psum_turn", bufs=TURN_LEAD))
-        psum_score = stack.enter_context(tc.psum_pool(name="psum_score", bufs=1))
+        psum_score = stack.enter_context(tc.psum_pool(name="psum_score", bufs=2))
         psum_sum = stack.enter_context(tc.psum_pool(name="psum_sum", bufs=1))
         psum_out = stack.enter_context(tc.psum_pool(name="psum_out", bufs=D_BANKS))
 
@@ -62,11 +65,10 @@ def tile_smcmr_pa_t_kernel(tc, query, context, out):
         nc.vector.memset(ones[:], 1.0)
         half = const.tile([P, PACK], F32)
         nc.vector.memset(half[:], 0.5)
-        minus_one = const.tile([P, PACK], F32)
-        nc.vector.memset(minus_one[:], -1.0)
 
         rows_of, turned_of, grouped_of, token_codes_of, scores_of = {}, {}, {}, {}, {}
-        damped_of, leaky_of, steep_of, regrouped_of, weight_codes_of = {}, {}, {}, {}, {}
+        damped_of, leaky_of, squares_of, root_of, ninth_of, steep_of = {}, {}, {}, {}, {}, {}
+        regrouped_of, weights_of, weight_codes_of = {}, {}, {}
         expo_of, sums_of, inverse_of, context_codes_of, acc_of = {}, {}, {}, {}, {}
 
         def is_group(i):
@@ -106,36 +108,39 @@ def tile_smcmr_pa_t_kernel(tc, query, context, out):
             )
             rows_of[i] = rows
 
-        def quantise_tokens(i):
+        def quantise_tokens(i, pair):
             if not is_group(i):
                 return
-            t_codes = stage.tile([P, PACK, D_PASSES, P], U32, align_bytes=64)
-            t_scales = stage.tile([P, PACK, D_PASSES, P], U8, align_bytes=64)
+            if pair == 0:
+                t_codes = stage.tile([P, PACK, D_PASSES, P], U32, align_bytes=64)
+                t_scales = stage.tile([P, PACK, D_PASSES, P], U8, align_bytes=64)
+                token_codes_of[i] = (t_codes, t_scales)
+            t_codes, t_scales = token_codes_of[i]
+            tiles = slice(2 * pair, 2 * pair + 2)
             nc.vector.quantize_mx(
-                out=t_codes[:].rearrange("p j c r -> p (j c r)").bitcast(FP8X4),
-                scales=t_scales[:].rearrange("p j c r -> p (j c r)"),
-                in_=grouped_of[i][:].rearrange("p j c r t -> p (j c r t)"),
+                out=t_codes[:, tiles].rearrange("p j c r -> p (j c r)").bitcast(FP8X4),
+                scales=t_scales[:, tiles].rearrange("p j c r -> p (j c r)"),
+                in_=grouped_of[i][:, tiles].rearrange("p j c r t -> p (j c r t)"),
             )
-            token_codes_of[i] = (t_codes, t_scales)
 
-        def first_matmul(i):
+        def first_matmul(i, j):
             if not is_group(i):
                 return
             b = i // GROUPS
+            if j == 0:
+                scores = psum_score.tile([P, PACK, Q], F32)
+                scores_of[i] = scores
             t_codes, t_scales = token_codes_of[i]
-            scores = psum_score.tile([P, PACK, Q], F32)
-            for j in range(PACK):
-                for c in range(D_PASSES):
-                    nc.tensor.matmul_mx(
-                        out=scores[:, j, :],
-                        lhsT=t_codes[:, j, c, :].bitcast(FP8X4),
-                        lhsT_scale=t_scales[:, j, c, :],
-                        rhs=q_codes[:, b, c, :].bitcast(FP8X4),
-                        rhs_scale=q_scales[:, b, c, :],
-                        start=(c == 0),
-                        stop=(c == D_PASSES - 1),
-                    )
-            scores_of[i] = scores
+            for c in range(D_PASSES):
+                nc.tensor.matmul_mx(
+                    out=scores_of[i][:, j, :],
+                    lhsT=t_codes[:, j, c, :].bitcast(FP8X4),
+                    lhsT_scale=t_scales[:, j, c, :],
+                    rhs=q_codes[:, b, c, :].bitcast(FP8X4),
+                    rhs_scale=q_scales[:, b, c, :],
+                    start=(c == 0),
+                    stop=(c == D_PASSES - 1),
+                )
 
         def damp(i):
             if not is_group(i):
@@ -151,45 +156,57 @@ def tile_smcmr_pa_t_kernel(tc, query, context, out):
             nc.vector.tensor_tensor(out=leaky[:], in0=scores_of[i][:], in1=damped_of[i][:], op=ALU.max)
             leaky_of[i] = leaky
 
-        def norm_factor(i):
+        def sum_squares(i, j):
             if not is_group(i):
                 return
-            squares = soft.tile([P, PACK], F32)
-            for j in range(PACK):
-                unused = stage.tile([P, Q], F32)
-                nc.scalar.activation(
-                    out=unused[:], in_=leaky_of[i][:, j, :], func=ACT.Square, accum_out=squares[:, j : j + 1]
-                )
-            norm = soft.tile([P, PACK], F32)
-            nc.gpsimd.tensor_scalar(out=norm[:], in0=squares[:], scalar1=1.0, scalar2=EPS, op0=ALU.mult, op1=ALU.add)
-            root = soft.tile([P, PACK], F32)
-            nc.gpsimd.tensor_tensor(out=root[:], in0=norm[:], in1=half[:], op=ALU.pow)
-            ninth = soft.tile([P, PACK], F32)
-            nc.gpsimd.tensor_scalar(
-                out=ninth[:], in0=root[:], scalar1=EPS, scalar2=1.0 / SMOOTH, op0=ALU.add, op1=ALU.mult
+            if j == 0:
+                squares = soft.tile([P, PACK], F32)
+                squares_of[i] = squares
+            unused = stage.tile([P, Q], F32)
+            nc.scalar.activation(
+                out=unused[:], in_=leaky_of[i][:, j, :], func=ACT.Square, accum_out=squares_of[i][:, j : j + 1]
             )
+
+        def start_root(i):
+            if not is_group(i):
+                return
+            shifted = soft.tile([P, PACK], F32)
+            nc.scalar.add(out=shifted[:], in_=squares_of[i][:], add=EPS)
+            root = soft.tile([P, PACK], F32)
+            nc.gpsimd.tensor_tensor(out=root[:], in0=shifted[:], in1=half[:], op=ALU.pow)
+            root_of[i] = root
+
+        def ninth_of_norm(i):
+            if not is_group(i):
+                return
+            ninth = soft.tile([P, PACK], F32)
+            nc.scalar.activation(out=ninth[:], in_=root_of[i][:], func=ACT.Copy, scale=1.0 / SMOOTH, bias=EPS / SMOOTH)
+            ninth_of[i] = ninth
+
+        def invert_norm(i):
+            if not is_group(i):
+                return
             steep = soft.tile([P, PACK], F32)
-            nc.gpsimd.tensor_tensor(out=steep[:], in0=ninth[:], in1=minus_one[:], op=ALU.pow)
+            nc.vector.reciprocal(out=steep[:], in_=ninth_of[i][:])
             steep_of[i] = steep
 
-        def exponentials(i):
+        def exponentials(i, j):
             if not is_group(i):
                 return
             b, g = divmod(i, GROUPS)
-            if g == 0:
+            if g == 0 and j == 0:
                 expo = keep.tile([P, GROUPS, PACK, Q], F32)
                 expo_of[b] = expo
-            leaky, steep = leaky_of[i], steep_of[i]
-            for j in range(PACK):
-                nc.scalar.activation(
-                    out=expo_of[b][:, g, j, :],
-                    in_=leaky[:, j, :],
-                    func=ACT.Exp,
-                    scale=steep[:, j : j + 1],
-                    bias=-SMOOTH,
-                )
+            nc.scalar.activation(
+                out=expo_of[b][:, g, j, :],
+                in_=leaky_of[i][:, j, :],
+                func=ACT.Exp,
+                scale=steep_of[i][:, j : j + 1],
+                bias=-SMOOTH,
+            )
 
-        def add_to_sums(i, j):
+        def add_to_sums(tile_number):
+            i, j = divmod(tile_number, PACK)
             if not is_group(i):
                 return
             b, g = divmod(i, GROUPS)
@@ -218,17 +235,16 @@ def tile_smcmr_pa_t_kernel(tc, query, context, out):
             regroup(i, nc.vector.tensor_copy, 0, D - SCALAR_COLS)
 
         def regroup_on_scalar(i):
-            if not is_group(i):
-                return
-            regroup(i, nc.scalar.copy, D - SCALAR_COLS, D)
+            if is_group(i):
+                regroup(i, nc.scalar.copy, D - SCALAR_COLS, D)
 
         def quantise_context(i):
             if not is_group(i):
                 return
             b, g = divmod(i, GROUPS)
             if g == 0:
-                c_codes = keep.tile([P, GROUPS, D], U32, align_bytes=64)
-                c_scales = keep.tile([P, GROUPS, D], U8, align_bytes=64)
+                c_codes = codes.tile([P, GROUPS, D], U32, align_bytes=64)
+                c_scales = codes.tile([P, GROUPS, D], U8, align_bytes=64)
                 context_codes_of[b] = (c_codes, c_scales)
             c_codes, c_scales = context_codes_of[b]
             nc.vector.quantize_mx(
@@ -239,7 +255,7 @@ def tile_smcmr_pa_t_kernel(tc, query, context, out):
 
         def normalise(i):
             if not is_group(i):
-                return None
+                return
             b, g = divmod(i, GROUPS)
             if g == 0:
                 inverse = stage.tile([P, Q], F32)
@@ -252,37 +268,36 @@ def tile_smcmr_pa_t_kernel(tc, query, context, out):
                 in1=inverse_of[b][:].unsqueeze(2).to_broadcast([P, Q, PACK]),
                 op=ALU.mult,
             )
-            return weights
+            weights_of[i] = weights
 
-        def quantise_weights(i, weights):
+        def quantise_weights(i):
             if not is_group(i):
                 return
             w_codes = soft.tile([P, Q], U32, align_bytes=64)
             w_scales = soft.tile([P, Q], U8, align_bytes=64)
             nc.vector.quantize_mx(
-                out=w_codes[:].bitcast(FP8X4), scales=w_scales[:], in_=weights[:].rearrange("p q j -> p (q j)")
+                out=w_codes[:].bitcast(FP8X4), scales=w_scales[:], in_=weights_of[i][:].rearrange("p q j -> p (q j)")
             )
             weight_codes_of[i] = (w_codes, w_scales)
 
-        def second_matmul(i):
+        def second_matmul(i, h):
             if not is_group(i):
                 return
             b, g = divmod(i, GROUPS)
             w_codes, w_scales = weight_codes_of[i]
             c_codes, c_scales = context_codes_of[b]
-            for h in range(D_BANKS):
-                if g == 0:
-                    acc = psum_out.tile([P, BANK], F32)
-                    acc_of[(b, h)] = acc
-                nc.tensor.matmul_mx(
-                    out=acc_of[(b, h)][:],
-                    lhsT=w_codes[:].bitcast(FP8X4),
-                    lhsT_scale=w_scales[:],
-                    rhs=c_codes[:, g, h * BANK : (h + 1) * BANK].bitcast(FP8X4),
-                    rhs_scale=c_scales[:, g, h * BANK : (h + 1) * BANK],
-                    start=(g == 0),
-                    stop=(g == GROUPS - 1),
-                )
+            if g == 0:
+                acc = psum_out.tile([P, BANK], F32)
+                acc_of[(b, h)] = acc
+            nc.tensor.matmul_mx(
+                out=acc_of[(b, h)][:],
+                lhsT=w_codes[:].bitcast(FP8X4),
+                lhsT_scale=w_scales[:],
+                rhs=c_codes[:, g, h * BANK : (h + 1) * BANK].bitcast(FP8X4),
+                rhs_scale=c_scales[:, g, h * BANK : (h + 1) * BANK],
+                start=(g == 0),
+                stop=(g == GROUPS - 1),
+            )
 
         def store(i):
             if not is_group(i) or i % GROUPS != GROUPS - 1:
@@ -296,11 +311,19 @@ def tile_smcmr_pa_t_kernel(tc, query, context, out):
                     nc.vector.tensor_copy(out=result[:], in_=acc_of[(b, h)][:])
                 nc.sync.dma_start(out=out[b, :, h * BANK : (h + 1) * BANK], in_=result[:])
 
+        def quarter(n, j):
+            copy_turned_tokens(n, j)
+            turn_tokens(PACK * n + j + TURN_LEAD)
+            sum_squares(n - SQUARE_LAG, j)
+            exponentials(n - EXP_LAG, j)
+            add_to_sums(PACK * (n - EXP_LAG) + j - 1)
+            first_matmul(n - SCORE_LAG, j)
+
         q_rows = token_pool.tile([P, B, D], BF16, tag="rows")
         nc.sync.dma_start(out=q_rows[:], in_=query.rearrange("b q d -> q b d"))
         for i in range(PREFETCH):
             load(i)
-        q_grouped = const.tile([P, B, D_PASSES, Q, PACK], BF16, align_bytes=64)
+        q_grouped = stage.tile([P, B, D_PASSES, Q, PACK], BF16, align_bytes=64, tag="t_grouped")
         for b in range(B):
             turn(("query", b), q_rows[:, b, :].bitcast(F32))
             copy_turned(("query", b), q_grouped[:, b].bitcast(F32))
@@ -317,19 +340,25 @@ def tile_smcmr_pa_t_kernel(tc, query, context, out):
         for n in range(ALL_GROUPS + STORE_LAG + 1):
             load(n + PREFETCH)
             store(n - STORE_LAG)
-            leaky_relu(n - NORM_LAG)
-            for j in range(PACK):
-                copy_turned_tokens(n, j)
-                turn_tokens(PACK * n + j + TURN_LEAD)
-                add_to_sums(n - SUM_LAG, j)
-            second_matmul(n - OUT_LAG)
+            quantise_tokens(n - 1, 1)
             regroup_on_vector(n - REGROUP_LAG)
-            quantise_tokens(n)
-            first_matmul(n)
-            norm_factor(n - NORM_LAG)
-            exponentials(n - EXP_LAG)
+
+            quarter(n, 0)
+            ninth_of_norm(n - STEEP_LAG)
+            normalise(n - WEIGHT_LAG)
+
+            quarter(n, 1)
+            damp(n - LEAKY_LAG)
+            second_matmul(n - OUT_LAG, 0)
+            quantise_tokens(n, 0)
+
+            quarter(n, 2)
             regroup_on_scalar(n - REGROUP_LAG)
-            weights = normalise(n - WEIGHT_LAG)
+            leaky_relu(n - LEAKY_LAG)
             quantise_context(n - CODE_LAG)
-            quantise_weights(n - WEIGHT_LAG, weights)
-            damp(n)
+
+            quarter(n, 3)
+            start_root(n - SQUARE_LAG)
+            second_matmul(n - OUT_LAG, 1)
+            invert_norm(n - STEEP_LAG)
+            quantise_weights(n - WEIGHT_LAG)

@@ -32,8 +32,8 @@ TURN_LEAD = 3
 SCORE_LAG = 1
 LEAKY_LAG = 2
 SQUARE_LAG = 3
-STEEP_LAG = 5
-EXP_LAG = 6
+STEEP_LAG = 6
+EXP_LAG = STEEP_LAG + 1
 WEIGHT_LAG = EXP_LAG + GROUPS
 OUT_LAG = WEIGHT_LAG + 1
 STORE_LAG = OUT_LAG + 1
@@ -123,24 +123,25 @@ def tile_smcmr_pa_t_kernel(tc, query, context, out):
                 in_=grouped_of[i][:, tiles].rearrange("p j c r t -> p (j c r t)"),
             )
 
-        def first_matmul(i, j):
+        def first_matmul(i, pair):
             if not is_group(i):
                 return
             b = i // GROUPS
-            if j == 0:
+            if pair == 0:
                 scores = psum_score.tile([P, PACK, Q], F32)
                 scores_of[i] = scores
             t_codes, t_scales = token_codes_of[i]
-            for c in range(D_PASSES):
-                nc.tensor.matmul_mx(
-                    out=scores_of[i][:, j, :],
-                    lhsT=t_codes[:, j, c, :].bitcast(FP8X4),
-                    lhsT_scale=t_scales[:, j, c, :],
-                    rhs=q_codes[:, b, c, :].bitcast(FP8X4),
-                    rhs_scale=q_scales[:, b, c, :],
-                    start=(c == 0),
-                    stop=(c == D_PASSES - 1),
-                )
+            for j in range(2 * pair, 2 * pair + 2):
+                for c in range(D_PASSES):
+                    nc.tensor.matmul_mx(
+                        out=scores_of[i][:, j, :],
+                        lhsT=t_codes[:, j, c, :].bitcast(FP8X4),
+                        lhsT_scale=t_scales[:, j, c, :],
+                        rhs=q_codes[:, b, c, :].bitcast(FP8X4),
+                        rhs_scale=q_scales[:, b, c, :],
+                        start=(c == 0),
+                        stop=(c == D_PASSES - 1),
+                    )
 
         def damp(i):
             if not is_group(i):
@@ -317,7 +318,6 @@ def tile_smcmr_pa_t_kernel(tc, query, context, out):
             sum_squares(n - SQUARE_LAG, j)
             exponentials(n - EXP_LAG, j)
             add_to_sums(PACK * (n - EXP_LAG) + j - 1)
-            first_matmul(n - SCORE_LAG, j)
 
         q_rows = token_pool.tile([P, B, D], BF16, tag="rows")
         nc.sync.dma_start(out=q_rows[:], in_=query.rearrange("b q d -> q b d"))
@@ -344,6 +344,7 @@ def tile_smcmr_pa_t_kernel(tc, query, context, out):
             regroup_on_vector(n - REGROUP_LAG)
 
             quarter(n, 0)
+            first_matmul(n - SCORE_LAG, 0)
             ninth_of_norm(n - STEEP_LAG)
             normalise(n - WEIGHT_LAG)
 
@@ -353,6 +354,7 @@ def tile_smcmr_pa_t_kernel(tc, query, context, out):
             quantise_tokens(n, 0)
 
             quarter(n, 2)
+            first_matmul(n - SCORE_LAG, 1)
             regroup_on_scalar(n - REGROUP_LAG)
             leaky_relu(n - LEAKY_LAG)
             quantise_context(n - CODE_LAG)

@@ -29,16 +29,21 @@ SCALAR_COLS = 192
 
 PREFETCH = 3
 TURN_LEAD = 3
-SCORE_LAG = 1
-LEAKY_LAG = 2
-SQUARE_LAG = 3
-STEEP_LAG = 6
-EXP_LAG = STEEP_LAG + 1
+LEAKY_LAG = 1
+EXP_LAG = 3
 WEIGHT_LAG = EXP_LAG + GROUPS
-OUT_LAG = WEIGHT_LAG + 1
+WEIGHT_CODE_LAG = WEIGHT_LAG + 1
+OUT_LAG = WEIGHT_CODE_LAG + 1
 STORE_LAG = OUT_LAG + 1
-REGROUP_LAG = 1
-CODE_LAG = REGROUP_LAG + 1
+
+QUERY_LEAD = 5
+QUERY_STEP = GROUPS - 1 - QUERY_LEAD // PACK
+
+HALVES = 2
+HALF = D // HALVES
+SLOTS = 2
+EMPTY_EVERY = 8
+BEHIND = ALL_GROUPS * SLOTS // EMPTY_EVERY
 
 FLOPS = 2 * 2 * B * Q * S * D
 
@@ -48,11 +53,13 @@ def tile_smcmr_pa_t_kernel(tc, query, context, out):
     with ExitStack() as stack:
         stack.enter_context(tc.manual_schedule())
         const = stack.enter_context(tc.tile_pool(name="const", bufs=1))
-        token_pool = stack.enter_context(tc.tile_pool(name="tokens", bufs=PREFETCH + REGROUP_LAG + 2))
+        token_pool = stack.enter_context(tc.tile_pool(name="tokens", bufs=PREFETCH + BEHIND // HALVES + 3))
         stage = stack.enter_context(tc.tile_pool(name="stage", bufs=2))
+        halves = stack.enter_context(tc.tile_pool(name="halves", bufs=3))
         keep = stack.enter_context(tc.tile_pool(name="keep", bufs=2))
-        codes = stack.enter_context(tc.tile_pool(name="codes", bufs=B))
-        soft = stack.enter_context(tc.tile_pool(name="soft", bufs=EXP_LAG - LEAKY_LAG + 1))
+        codes = stack.enter_context(tc.tile_pool(name="codes", bufs=OUT_LAG + 2))
+        soft = stack.enter_context(tc.tile_pool(name="soft", bufs=EXP_LAG - LEAKY_LAG + 2))
+        query_pool = stack.enter_context(tc.tile_pool(name="query", bufs=B))
         results = stack.enter_context(tc.tile_pool(name="results", bufs=D_BANKS))
         psum_turn = stack.enter_context(tc.psum_pool(name="psum_turn", bufs=TURN_LEAD))
         psum_score = stack.enter_context(tc.psum_pool(name="psum_score", bufs=2))
@@ -63,12 +70,15 @@ def tile_smcmr_pa_t_kernel(tc, query, context, out):
         make_identity(nc, identity[:])
         ones = const.tile([P, P], F32)
         nc.vector.memset(ones[:], 1.0)
-        half = const.tile([P, PACK], F32)
-        nc.vector.memset(half[:], 0.5)
+        half_power = const.tile([P, PACK], F32)
+        nc.vector.memset(half_power[:], 0.5)
+        q_codes = const.tile([P, B, D_PASSES, Q], U32, align_bytes=64)
+        q_scales = const.tile([P, B, D_PASSES, Q], U8, align_bytes=64)
 
         rows_of, turned_of, grouped_of, token_codes_of, scores_of = {}, {}, {}, {}, {}
         damped_of, leaky_of, squares_of, root_of, ninth_of, steep_of = {}, {}, {}, {}, {}, {}
         regrouped_of, weights_of, weight_codes_of = {}, {}, {}
+        query_rows_of, query_grouped_of = {}, {}
         expo_of, sums_of, inverse_of, context_codes_of, acc_of = {}, {}, {}, {}, {}
 
         def is_group(i):
@@ -85,10 +95,26 @@ def tile_smcmr_pa_t_kernel(tc, query, context, out):
         def copy_turned(key, grouped_words):
             nc.scalar.copy(out=grouped_words, in_=turned_of[key][:].rearrange("p c u r -> p c r u"))
 
-        def turn_tokens(tile_number):
-            i, j = divmod(tile_number, PACK)
-            if is_group(i):
-                turn(tile_number, rows_of[i][:, j, :].bitcast(F32))
+        turn_order = [("query", 0)]
+        for tile_number in range(PACK * ALL_GROUPS):
+            b, left = divmod(tile_number + QUERY_LEAD, PACK * GROUPS)
+            if left == 0 and b < B:
+                turn_order.append(("query", b))
+            turn_order.append(("tile", tile_number))
+
+        def turn_next(count):
+            for kind, number in turn_order[count : count + 1]:
+                if kind == "query":
+                    turn((kind, number), query_rows_of[number][:].bitcast(F32))
+                else:
+                    i, j = divmod(number, PACK)
+                    turn((kind, number), rows_of[i][:, j, :].bitcast(F32))
+
+        def copy_query(b):
+            q_grouped = query_pool.tile([P, D_PASSES, Q, PACK], BF16, align_bytes=64)
+            copy_turned(("query", b), q_grouped[:].bitcast(F32))
+            query_grouped_of[b] = q_grouped
+            turn_next(turn_order.index(("query", b)) + TURN_LEAD)
 
         def copy_turned_tokens(i, j):
             if not is_group(i):
@@ -96,7 +122,11 @@ def tile_smcmr_pa_t_kernel(tc, query, context, out):
             if j == 0:
                 t_grouped = stage.tile([P, PACK, D_PASSES, P, PACK], BF16, align_bytes=64)
                 grouped_of[i] = t_grouped
-            copy_turned(PACK * i + j, grouped_of[i][:, j].bitcast(F32))
+            place = turn_order.index(("tile", PACK * i + j))
+            if i + j > 0 and turn_order[place - 1][0] == "query":
+                copy_query(turn_order[place - 1][1])
+            copy_turned(("tile", PACK * i + j), grouped_of[i][:, j].bitcast(F32))
+            turn_next(place + TURN_LEAD)
 
         def load(i):
             if not is_group(i):
@@ -174,7 +204,7 @@ def tile_smcmr_pa_t_kernel(tc, query, context, out):
             shifted = soft.tile([P, PACK], F32)
             nc.scalar.add(out=shifted[:], in_=squares_of[i][:], add=EPS)
             root = soft.tile([P, PACK], F32)
-            nc.gpsimd.tensor_tensor(out=root[:], in0=shifted[:], in1=half[:], op=ALU.pow)
+            nc.gpsimd.tensor_tensor(out=root[:], in0=shifted[:], in1=half_power[:], op=ALU.pow)
             root_of[i] = root
 
         def ninth_of_norm(i):
@@ -222,46 +252,68 @@ def tile_smcmr_pa_t_kernel(tc, query, context, out):
                 stop=(g == GROUPS - 1 and j == PACK - 1),
             )
 
-        def regroup(i, engine_copy, first, last):
+        def half_of_slot(slot):
+            with_gaps = ALL_GROUPS * SLOTS
+            if slot < with_gaps:
+                half = None if slot % EMPTY_EVERY == EMPTY_EVERY - 1 else slot - slot // EMPTY_EVERY
+            else:
+                half = slot - BEHIND
+            return half if half is not None and half < ALL_GROUPS * HALVES else None
+
+        def scalar_columns(half):
+            return SCALAR_COLS if half % HALVES == HALVES - 1 else 0
+
+        def regroup(half, engine_copy, first, last):
+            i, h = divmod(half, HALVES)
             engine_copy(
-                out=regrouped_of[i][:, first:last, :].rearrange("p (n k) j -> p n j k", k=4),
-                in_=rows_of[i][:, :, first:last].rearrange("p j (n k) -> p n j k", k=4),
+                out=regrouped_of[half][:, first:last, :].rearrange("p (n k) j -> p n j k", k=4),
+                in_=rows_of[i][:, :, h * HALF + first : h * HALF + last].rearrange("p j (n k) -> p n j k", k=4),
             )
 
-        def regroup_on_vector(i):
-            if not is_group(i):
-                return
-            regrouped = stage.tile([P, D, PACK], BF16, align_bytes=64)
-            regrouped_of[i] = regrouped
-            regroup(i, nc.vector.tensor_copy, 0, D - SCALAR_COLS)
+        def open_slot(slot):
+            half = half_of_slot(slot)
+            if half is not None:
+                regrouped = halves.tile([P, HALF, PACK], BF16, align_bytes=64)
+                regrouped_of[half] = regrouped
 
-        def regroup_on_scalar(i):
-            if is_group(i):
-                regroup(i, nc.scalar.copy, D - SCALAR_COLS, D)
+        def regroup_on_vector(slot):
+            half = half_of_slot(slot)
+            if half is not None:
+                regroup(half, nc.vector.tensor_copy, 0, HALF - scalar_columns(half))
 
-        def quantise_context(i):
-            if not is_group(i):
+        def regroup_on_scalar(slot):
+            half = half_of_slot(slot)
+            if half is not None and scalar_columns(half):
+                regroup(half, nc.scalar.copy, HALF - scalar_columns(half), HALF)
+
+        def quantise_context(slot):
+            half = half_of_slot(slot)
+            if half is None:
                 return
-            b, g = divmod(i, GROUPS)
-            if g == 0:
-                c_codes = codes.tile([P, GROUPS, D], U32, align_bytes=64)
-                c_scales = codes.tile([P, GROUPS, D], U8, align_bytes=64)
-                context_codes_of[b] = (c_codes, c_scales)
-            c_codes, c_scales = context_codes_of[b]
+            i, h = divmod(half, HALVES)
+            if h == 0:
+                c_codes = codes.tile([P, D], U32, align_bytes=64)
+                c_scales = codes.tile([P, D], U8, align_bytes=64)
+                context_codes_of[i] = (c_codes, c_scales)
+            c_codes, c_scales = context_codes_of[i]
             nc.vector.quantize_mx(
-                out=c_codes[:, g, :].bitcast(FP8X4),
-                scales=c_scales[:, g, :],
-                in_=regrouped_of[i][:].rearrange("p d j -> p (d j)"),
+                out=c_codes[:, h * HALF : (h + 1) * HALF].bitcast(FP8X4),
+                scales=c_scales[:, h * HALF : (h + 1) * HALF],
+                in_=regrouped_of[half][:].rearrange("p d j -> p (d j)"),
             )
+
+        def invert_sums(i):
+            if not is_group(i) or i % GROUPS != 0:
+                return
+            b = i // GROUPS
+            inverse = stage.tile([P, Q], F32)
+            nc.vector.reciprocal(out=inverse[:], in_=sums_of[b][:])
+            inverse_of[b] = inverse
 
         def normalise(i):
             if not is_group(i):
                 return
             b, g = divmod(i, GROUPS)
-            if g == 0:
-                inverse = stage.tile([P, Q], F32)
-                nc.vector.reciprocal(out=inverse[:], in_=sums_of[b][:])
-                inverse_of[b] = inverse
             weights = stage.tile([P, Q, PACK], BF16, align_bytes=64)
             nc.vector.tensor_tensor(
                 out=weights[:],
@@ -286,7 +338,7 @@ def tile_smcmr_pa_t_kernel(tc, query, context, out):
                 return
             b, g = divmod(i, GROUPS)
             w_codes, w_scales = weight_codes_of[i]
-            c_codes, c_scales = context_codes_of[b]
+            c_codes, c_scales = context_codes_of[i]
             if g == 0:
                 acc = psum_out.tile([P, BANK], F32)
                 acc_of[(b, h)] = acc
@@ -294,8 +346,8 @@ def tile_smcmr_pa_t_kernel(tc, query, context, out):
                 out=acc_of[(b, h)][:],
                 lhsT=w_codes[:].bitcast(FP8X4),
                 lhsT_scale=w_scales[:],
-                rhs=c_codes[:, g, h * BANK : (h + 1) * BANK].bitcast(FP8X4),
-                rhs_scale=c_scales[:, g, h * BANK : (h + 1) * BANK],
+                rhs=c_codes[:, h * BANK : (h + 1) * BANK].bitcast(FP8X4),
+                rhs_scale=c_scales[:, h * BANK : (h + 1) * BANK],
                 start=(g == 0),
                 stop=(g == GROUPS - 1),
             )
@@ -312,55 +364,73 @@ def tile_smcmr_pa_t_kernel(tc, query, context, out):
                     nc.vector.tensor_copy(out=result[:], in_=acc_of[(b, h)][:])
                 nc.sync.dma_start(out=out[b, :, h * BANK : (h + 1) * BANK], in_=result[:])
 
-        def quarter(n, j):
-            copy_turned_tokens(n, j)
-            turn_tokens(PACK * n + j + TURN_LEAD)
-            sum_squares(n - SQUARE_LAG, j)
-            exponentials(n - EXP_LAG, j)
-            add_to_sums(PACK * (n - EXP_LAG) + j - 1)
+        def load_query(b):
+            q_rows = query_pool.tile([P, D], BF16)
+            nc.sync.dma_start(out=q_rows[:], in_=query[b])
+            query_rows_of[b] = q_rows
 
-        q_rows = token_pool.tile([P, B, D], BF16, tag="rows")
-        nc.sync.dma_start(out=q_rows[:], in_=query.rearrange("b q d -> q b d"))
-        for i in range(PREFETCH):
+        def quantise_query(b):
+            nc.vector.quantize_mx(
+                out=q_codes[:, b].rearrange("p c q -> p (c q)").bitcast(FP8X4),
+                scales=q_scales[:, b].rearrange("p c q -> p (c q)"),
+                in_=query_grouped_of[b][:].rearrange("p c q t -> p (c q t)"),
+            )
+
+        load_query(0)
+        load(0)
+        for b in range(1, B):
+            load_query(b)
+        for i in range(1, PREFETCH):
             load(i)
-        q_grouped = stage.tile([P, B, D_PASSES, Q, PACK], BF16, align_bytes=64, tag="t_grouped")
-        for b in range(B):
-            turn(("query", b), q_rows[:, b, :].bitcast(F32))
-            copy_turned(("query", b), q_grouped[:, b].bitcast(F32))
-        q_codes = const.tile([P, B, D_PASSES, Q], U32, align_bytes=64)
-        q_scales = const.tile([P, B, D_PASSES, Q], U8, align_bytes=64)
-        nc.vector.quantize_mx(
-            out=q_codes[:].rearrange("p b c q -> p (b c q)").bitcast(FP8X4),
-            scales=q_scales[:].rearrange("p b c q -> p (b c q)"),
-            in_=q_grouped[:].rearrange("p b c q t -> p (b c q t)"),
-        )
-        for tile_number in range(TURN_LEAD):
-            turn_tokens(tile_number)
+        for count in range(TURN_LEAD):
+            turn_next(count)
+        copy_query(0)
+        quantise_query(0)
 
         for n in range(ALL_GROUPS + STORE_LAG + 1):
             load(n + PREFETCH)
             store(n - STORE_LAG)
+            open_slot(2 * n)
+            open_slot(2 * n + 1)
+
+            copy_turned_tokens(n, 0)
             quantise_tokens(n - 1, 1)
-            regroup_on_vector(n - REGROUP_LAG)
+            first_matmul(n - 1, 1)
+            ninth_of_norm(n - EXP_LAG)
+            regroup_on_scalar(2 * n)
+            regroup_on_scalar(2 * n + 1)
+            regroup_on_vector(2 * n)
+            invert_norm(n - EXP_LAG)
+            quantise_context(2 * n - 1)
 
-            quarter(n, 0)
-            first_matmul(n - SCORE_LAG, 0)
-            ninth_of_norm(n - STEEP_LAG)
-            normalise(n - WEIGHT_LAG)
-
-            quarter(n, 1)
+            copy_turned_tokens(n, 1)
             damp(n - LEAKY_LAG)
+            exponentials(n - EXP_LAG, 0)
+            exponentials(n - EXP_LAG, 1)
             second_matmul(n - OUT_LAG, 0)
+            invert_sums(n - WEIGHT_LAG)
+            leaky_relu(n - LEAKY_LAG)
             quantise_tokens(n, 0)
 
-            quarter(n, 2)
-            first_matmul(n - SCORE_LAG, 1)
-            regroup_on_scalar(n - REGROUP_LAG)
-            leaky_relu(n - LEAKY_LAG)
-            quantise_context(n - CODE_LAG)
+            copy_turned_tokens(n, 2)
+            first_matmul(n, 0)
+            add_to_sums(PACK * (n - EXP_LAG))
+            add_to_sums(PACK * (n - EXP_LAG) + 1)
+            exponentials(n - EXP_LAG, 2)
+            exponentials(n - EXP_LAG, 3)
+            sum_squares(n - LEAKY_LAG, 0)
+            sum_squares(n - LEAKY_LAG, 1)
+            regroup_on_vector(2 * n + 1)
+            normalise(n - WEIGHT_LAG)
 
-            quarter(n, 3)
-            start_root(n - SQUARE_LAG)
+            copy_turned_tokens(n, 3)
             second_matmul(n - OUT_LAG, 1)
-            invert_norm(n - STEEP_LAG)
-            quantise_weights(n - WEIGHT_LAG)
+            add_to_sums(PACK * (n - EXP_LAG) + 2)
+            add_to_sums(PACK * (n - EXP_LAG) + 3)
+            sum_squares(n - LEAKY_LAG, 2)
+            sum_squares(n - LEAKY_LAG, 3)
+            start_root(n - LEAKY_LAG)
+            quantise_context(2 * n)
+            quantise_weights(n - WEIGHT_CODE_LAG)
+            if n % GROUPS == QUERY_STEP and n < ALL_GROUPS - GROUPS:
+                quantise_query(n // GROUPS + 1)

@@ -1,3 +1,4 @@
+import math
 from contextlib import ExitStack
 
 import concourse.mybir as mybir
@@ -26,24 +27,27 @@ BANK = 512
 D_BANKS = D // BANK
 
 SCALAR_COLS = 192
+LATE_SCALAR_COLS = 192
 
+FIRST_PARTS = 2
 PREFETCH = 3
 TURN_LEAD = 3
-LEAKY_LAG = 1
-EXP_LAG = 3
-WEIGHT_LAG = EXP_LAG + GROUPS
-WEIGHT_CODE_LAG = WEIGHT_LAG + 1
-OUT_LAG = WEIGHT_CODE_LAG + 1
-STORE_LAG = OUT_LAG + 1
+EXP_LAG = 6
+WEIGHT_LAG = 9
+OUT_LAG = 10
+STORE_LAG = 11
 
-QUERY_LEAD = 5
-QUERY_STEP = GROUPS - 1 - QUERY_LEAD // PACK
+QUERY_PLACE = 3
 
 HALVES = 2
 HALF = D // HALVES
 SLOTS = 2
-EMPTY_EVERY = 8
-BEHIND = ALL_GROUPS * SLOTS // EMPTY_EVERY
+BEHIND = 4
+
+PAIR = 2
+HALF_LN2 = 0.5 * math.log(2.0)
+CUBIC = math.sqrt(0.375)
+SHRINK = 1.0 / (24.0 * SMOOTH) ** 2
 
 FLOPS = 2 * 2 * B * Q * S * D
 
@@ -53,14 +57,16 @@ def tile_smcmr_pa_t_kernel(tc, query, context, out):
     with ExitStack() as stack:
         stack.enter_context(tc.manual_schedule())
         const = stack.enter_context(tc.tile_pool(name="const", bufs=1))
-        token_pool = stack.enter_context(tc.tile_pool(name="tokens", bufs=PREFETCH + BEHIND // HALVES + 3))
+        token_pool = stack.enter_context(tc.tile_pool(name="tokens", bufs=PREFETCH + BEHIND // HALVES + 2))
         stage = stack.enter_context(tc.tile_pool(name="stage", bufs=2))
-        halves = stack.enter_context(tc.tile_pool(name="halves", bufs=3))
+        halves = stack.enter_context(tc.tile_pool(name="halves", bufs=5))
         keep = stack.enter_context(tc.tile_pool(name="keep", bufs=2))
         codes = stack.enter_context(tc.tile_pool(name="codes", bufs=OUT_LAG + 2))
-        soft = stack.enter_context(tc.tile_pool(name="soft", bufs=EXP_LAG - LEAKY_LAG + 2))
+        soft = stack.enter_context(tc.tile_pool(name="soft", bufs=6))
+        small = stack.enter_context(tc.tile_pool(name="small", bufs=4))
+        weight_pool = stack.enter_context(tc.tile_pool(name="weights", bufs=4))
         query_pool = stack.enter_context(tc.tile_pool(name="query", bufs=B))
-        results = stack.enter_context(tc.tile_pool(name="results", bufs=D_BANKS))
+        results = stack.enter_context(tc.tile_pool(name="results", bufs=2 * D_BANKS))
         psum_turn = stack.enter_context(tc.psum_pool(name="psum_turn", bufs=TURN_LEAD))
         psum_score = stack.enter_context(tc.psum_pool(name="psum_score", bufs=2))
         psum_sum = stack.enter_context(tc.psum_pool(name="psum_sum", bufs=1))
@@ -70,13 +76,12 @@ def tile_smcmr_pa_t_kernel(tc, query, context, out):
         make_identity(nc, identity[:])
         ones = const.tile([P, P], F32)
         nc.vector.memset(ones[:], 1.0)
-        half_power = const.tile([P, PACK], F32)
-        nc.vector.memset(half_power[:], 0.5)
         q_codes = const.tile([P, B, D_PASSES, Q], U32, align_bytes=64)
         q_scales = const.tile([P, B, D_PASSES, Q], U8, align_bytes=64)
 
         rows_of, turned_of, grouped_of, token_codes_of, scores_of = {}, {}, {}, {}, {}
-        damped_of, leaky_of, squares_of, root_of, ninth_of, steep_of = {}, {}, {}, {}, {}, {}
+        damped_of, leaky_of, squares_of, steep_of = {}, {}, {}, {}
+        norm_of, shifted_of, guess_of = {}, {}, {}
         regrouped_of, weights_of, weight_codes_of = {}, {}, {}
         query_rows_of, query_grouped_of = {}, {}
         expo_of, sums_of, inverse_of, context_codes_of, acc_of = {}, {}, {}, {}, {}
@@ -95,10 +100,10 @@ def tile_smcmr_pa_t_kernel(tc, query, context, out):
         def copy_turned(key, grouped_words):
             nc.scalar.copy(out=grouped_words, in_=turned_of[key][:].rearrange("p c u r -> p c r u"))
 
-        turn_order = [("query", 0)]
+        turn_order = []
         for tile_number in range(PACK * ALL_GROUPS):
-            b, left = divmod(tile_number + QUERY_LEAD, PACK * GROUPS)
-            if left == 0 and b < B:
+            b, place = divmod(tile_number, PACK * GROUPS)
+            if place == QUERY_PLACE:
                 turn_order.append(("query", b))
             turn_order.append(("tile", tile_number))
 
@@ -111,7 +116,7 @@ def tile_smcmr_pa_t_kernel(tc, query, context, out):
                     turn((kind, number), rows_of[i][:, j, :].bitcast(F32))
 
         def copy_query(b):
-            q_grouped = query_pool.tile([P, D_PASSES, Q, PACK], BF16, align_bytes=64)
+            q_grouped = stage.tile([P, D_PASSES, Q, PACK], BF16, align_bytes=64)
             copy_turned(("query", b), q_grouped[:].bitcast(F32))
             query_grouped_of[b] = q_grouped
             turn_next(turn_order.index(("query", b)) + TURN_LEAD)
@@ -123,7 +128,7 @@ def tile_smcmr_pa_t_kernel(tc, query, context, out):
                 t_grouped = stage.tile([P, PACK, D_PASSES, P, PACK], BF16, align_bytes=64)
                 grouped_of[i] = t_grouped
             place = turn_order.index(("tile", PACK * i + j))
-            if i + j > 0 and turn_order[place - 1][0] == "query":
+            if place > 0 and turn_order[place - 1][0] == "query":
                 copy_query(turn_order[place - 1][1])
             copy_turned(("tile", PACK * i + j), grouped_of[i][:, j].bitcast(F32))
             turn_next(place + TURN_LEAD)
@@ -133,9 +138,11 @@ def tile_smcmr_pa_t_kernel(tc, query, context, out):
                 return
             b, g = divmod(i, GROUPS)
             rows = token_pool.tile([P, PACK, D], BF16)
-            nc.sync.dma_start(
-                out=rows[:], in_=context[b, g * K_PASS : (g + 1) * K_PASS, :].rearrange("(p j) d -> p j d", j=PACK)
-            )
+            source = context[b, g * K_PASS : (g + 1) * K_PASS, :].rearrange("(p j) d -> p j d", j=PACK)
+            parts = FIRST_PARTS if i == 0 else 1
+            for part in range(parts):
+                tiles = slice(part * PACK // parts, (part + 1) * PACK // parts)
+                nc.sync.dma_start(out=rows[:, tiles, :], in_=source[:, tiles, :])
             rows_of[i] = rows
 
         def quantise_tokens(i, pair):
@@ -190,41 +197,109 @@ def tile_smcmr_pa_t_kernel(tc, query, context, out):
         def sum_squares(i, j):
             if not is_group(i):
                 return
-            if j == 0:
-                squares = soft.tile([P, PACK], F32)
-                squares_of[i] = squares
+            column = PACK * (i % PAIR) + j
+            if column == 0:
+                squares = small.tile([P, PAIR * PACK], F32)
+                squares_of[i // PAIR] = squares
             unused = stage.tile([P, Q], F32)
             nc.scalar.activation(
-                out=unused[:], in_=leaky_of[i][:, j, :], func=ACT.Square, accum_out=squares_of[i][:, j : j + 1]
+                out=unused[:],
+                in_=leaky_of[i][:, j, :],
+                func=ACT.Square,
+                accum_out=squares_of[i // PAIR][:, column : column + 1],
             )
 
-        def start_root(i):
-            if not is_group(i):
+        def shift_squares(i):
+            if not is_group(i) or i % PAIR != PAIR - 1:
                 return
-            shifted = soft.tile([P, PACK], F32)
-            nc.scalar.add(out=shifted[:], in_=squares_of[i][:], add=EPS)
-            root = soft.tile([P, PACK], F32)
-            nc.gpsimd.tensor_tensor(out=root[:], in0=shifted[:], in1=half_power[:], op=ALU.pow)
-            root_of[i] = root
+            shifted = small.tile([P, PAIR * PACK], F32)
+            nc.scalar.activation(
+                out=shifted[:], in_=squares_of[i // PAIR][:], func=ACT.Copy, scale=SHRINK, bias=EPS * SHRINK
+            )
+            shifted_of[i // PAIR] = shifted
 
-        def ninth_of_norm(i):
-            if not is_group(i):
+        def guess_root(i):
+            if not is_group(i) or i % PAIR != PAIR - 1:
                 return
-            ninth = soft.tile([P, PACK], F32)
-            nc.scalar.activation(out=ninth[:], in_=root_of[i][:], func=ACT.Copy, scale=1.0 / SMOOTH, bias=EPS / SMOOTH)
-            ninth_of[i] = ninth
+            pair = i // PAIR
+            shifted = shifted_of[pair]
+            guess = small.tile([P, PAIR * PACK], F32)
+            nc.scalar.activation(
+                out=guess[:],
+                in_=shifted[:].bitcast(U32),
+                func=ACT.Exp,
+                scale=-HALF_LN2 / 2**23,
+                bias=HALF_LN2 * (127.0 - 0.043),
+            )
+            guess_of[pair] = guess
 
-        def invert_norm(i):
-            if not is_group(i):
+        def square_guess(i):
+            if not is_group(i) or i % PAIR != PAIR - 1:
                 return
-            steep = soft.tile([P, PACK], F32)
-            nc.vector.reciprocal(out=steep[:], in_=ninth_of[i][:])
-            steep_of[i] = steep
+            pair = i // PAIR
+            guess_squared = small.tile([P, PAIR * PACK], F32)
+            nc.scalar.activation(out=guess_squared[:], in_=guess_of[pair][:], func=ACT.Square, scale=math.sqrt(CUBIC))
+            norm_of[pair] = (shifted_of[pair], guess_of[pair], guess_squared)
+
+        def norm_step(i, k):
+            if not is_group(i) or i % PAIR != PAIR - 1:
+                return
+            pair = i // PAIR
+            x, y, last = norm_of[pair]
+            shape = [P, PAIR * PACK]
+            if k == 0:
+                h = small.tile(shape, F32)
+                nc.vector.tensor_tensor(out=h[:], in0=last[:], in1=x[:], op=ALU.mult)
+                last = h
+            elif k == 1:
+                cubic = small.tile(shape, F32)
+                nc.vector.scalar_tensor_tensor(
+                    out=cubic[:], in0=last[:], scalar=-1.25 / CUBIC, in1=last[:], op0=ALU.add, op1=ALU.mult
+                )
+                last = cubic
+            elif k == 2:
+                better = small.tile(shape, F32)
+                nc.vector.scalar_tensor_tensor(
+                    out=better[:], in0=last[:], scalar=1.875, in1=y[:], op0=ALU.add, op1=ALU.mult
+                )
+                y = better
+            elif k == 3:
+                x_times_y = small.tile(shape, F32)
+                nc.vector.tensor_tensor(out=x_times_y[:], in0=y[:], in1=x[:], op=ALU.mult)
+                x = x_times_y
+            elif k == 4:
+                g = small.tile(shape, F32)
+                nc.vector.scalar_tensor_tensor(
+                    out=g[:], in0=x[:], scalar=3.0, in1=y[:], op0=ALU.mult, op1=ALU.mult
+                )
+                last = g
+            elif k == 5:
+                finer = small.tile(shape, F32)
+                nc.vector.scalar_tensor_tensor(
+                    out=finer[:], in0=last[:], scalar=-10.0, in1=last[:], op0=ALU.add, op1=ALU.mult
+                )
+                last = finer
+            elif k == 6:
+                root = small.tile(shape, F32)
+                nc.vector.scalar_tensor_tensor(
+                    out=root[:], in0=last[:], scalar=45.0, in1=x[:], op0=ALU.add, op1=ALU.mult
+                )
+                last = root
+            elif k == 7:
+                ninth = small.tile(shape, F32)
+                nc.vector.tensor_scalar_add(out=ninth[:], in0=last[:], scalar1=EPS / SMOOTH)
+                last = ninth
+            else:
+                steep = small.tile(shape, F32)
+                nc.vector.reciprocal(out=steep[:], in_=last[:])
+                steep_of[pair] = steep
+            norm_of[pair] = (x, y, last)
 
         def exponentials(i, j):
             if not is_group(i):
                 return
             b, g = divmod(i, GROUPS)
+            column = PACK * (i % PAIR) + j
             if g == 0 and j == 0:
                 expo = keep.tile([P, GROUPS, PACK, Q], F32)
                 expo_of[b] = expo
@@ -232,7 +307,7 @@ def tile_smcmr_pa_t_kernel(tc, query, context, out):
                 out=expo_of[b][:, g, j, :],
                 in_=leaky_of[i][:, j, :],
                 func=ACT.Exp,
-                scale=steep_of[i][:, j : j + 1],
+                scale=steep_of[i // PAIR][:, column : column + 1],
                 bias=-SMOOTH,
             )
 
@@ -253,28 +328,28 @@ def tile_smcmr_pa_t_kernel(tc, query, context, out):
             )
 
         def half_of_slot(slot):
-            with_gaps = ALL_GROUPS * SLOTS
-            if slot < with_gaps:
-                half = None if slot % EMPTY_EVERY == EMPTY_EVERY - 1 else slot - slot // EMPTY_EVERY
-            else:
+            slots = ALL_GROUPS * SLOTS
+            if slot >= slots:
                 half = slot - BEHIND
-            return half if half is not None and half < ALL_GROUPS * HALVES else None
+                return half if half < slots else None
+            half = max(slot, 0) * (slots - BEHIND) // slots
+            following = (slot + 1) * (slots - BEHIND) // slots
+            return half if half < following else None
 
         def scalar_columns(half):
+            if half >= ALL_GROUPS * HALVES - BEHIND:
+                return LATE_SCALAR_COLS
             return SCALAR_COLS if half % HALVES == HALVES - 1 else 0
 
         def regroup(half, engine_copy, first, last):
             i, h = divmod(half, HALVES)
+            if half not in regrouped_of:
+                regrouped = halves.tile([P, HALF, PACK], BF16, align_bytes=64)
+                regrouped_of[half] = regrouped
             engine_copy(
                 out=regrouped_of[half][:, first:last, :].rearrange("p (n k) j -> p n j k", k=4),
                 in_=rows_of[i][:, :, h * HALF + first : h * HALF + last].rearrange("p j (n k) -> p n j k", k=4),
             )
-
-        def open_slot(slot):
-            half = half_of_slot(slot)
-            if half is not None:
-                regrouped = halves.tile([P, HALF, PACK], BF16, align_bytes=64)
-                regrouped_of[half] = regrouped
 
         def regroup_on_vector(slot):
             half = half_of_slot(slot)
@@ -314,7 +389,7 @@ def tile_smcmr_pa_t_kernel(tc, query, context, out):
             if not is_group(i):
                 return
             b, g = divmod(i, GROUPS)
-            weights = stage.tile([P, Q, PACK], BF16, align_bytes=64)
+            weights = weight_pool.tile([P, Q, PACK], BF16, align_bytes=64)
             nc.vector.tensor_tensor(
                 out=weights[:],
                 in0=expo_of[b][:, g].rearrange("p j q -> p q j"),
@@ -326,8 +401,8 @@ def tile_smcmr_pa_t_kernel(tc, query, context, out):
         def quantise_weights(i):
             if not is_group(i):
                 return
-            w_codes = soft.tile([P, Q], U32, align_bytes=64)
-            w_scales = soft.tile([P, Q], U8, align_bytes=64)
+            w_codes = weight_pool.tile([P, Q], U32, align_bytes=64)
+            w_scales = weight_pool.tile([P, Q], U8, align_bytes=64)
             nc.vector.quantize_mx(
                 out=w_codes[:].bitcast(FP8X4), scales=w_scales[:], in_=weights_of[i][:].rearrange("p q j -> p (q j)")
             )
@@ -358,7 +433,7 @@ def tile_smcmr_pa_t_kernel(tc, query, context, out):
             b = i // GROUPS
             for h in range(D_BANKS):
                 result = results.tile([P, BANK], F32)
-                if h % 2 == 0:
+                if h % 2 == 0 or b < B - 1:
                     nc.scalar.copy(out=result[:], in_=acc_of[(b, h)][:])
                 else:
                     nc.vector.tensor_copy(out=result[:], in_=acc_of[(b, h)][:])
@@ -376,61 +451,171 @@ def tile_smcmr_pa_t_kernel(tc, query, context, out):
                 in_=query_grouped_of[b][:].rearrange("p c q t -> p (c q t)"),
             )
 
-        load_query(0)
         load(0)
-        for b in range(1, B):
-            load_query(b)
+        load_query(0)
         for i in range(1, PREFETCH):
             load(i)
+        for b in range(1, B):
+            load_query(b)
         for count in range(TURN_LEAD):
             turn_next(count)
-        copy_query(0)
-        quantise_query(0)
 
-        for n in range(ALL_GROUPS + STORE_LAG + 1):
+        for n in range(ALL_GROUPS):
             load(n + PREFETCH)
             store(n - STORE_LAG)
-            open_slot(2 * n)
-            open_slot(2 * n + 1)
 
             copy_turned_tokens(n, 0)
-            quantise_tokens(n - 1, 1)
-            first_matmul(n - 1, 1)
-            ninth_of_norm(n - EXP_LAG)
-            regroup_on_scalar(2 * n)
-            regroup_on_scalar(2 * n + 1)
-            regroup_on_vector(2 * n)
-            invert_norm(n - EXP_LAG)
-            quantise_context(2 * n - 1)
-
             copy_turned_tokens(n, 1)
-            damp(n - LEAKY_LAG)
-            exponentials(n - EXP_LAG, 0)
-            exponentials(n - EXP_LAG, 1)
+            if n % GROUPS == 1:
+                quantise_query(n // GROUPS)
+            quantise_tokens(n - 1, 0)
+            norm_step(n - 4, 2)
+            quantise_context(2 * n - 1)
+            norm_step(n - 4, 3)
+            first_matmul(n - 1, 0)
+            for j in range(PACK):
+                sum_squares(n - 3, j)
+            damp(n - 2)
+            for j in range(PACK):
+                exponentials(n - EXP_LAG, j)
+            shift_squares(n - 3)
+            regroup_on_vector(2 * n)
+            norm_step(n - 4, 4)
+            quantise_weights(n - OUT_LAG)
             second_matmul(n - OUT_LAG, 0)
-            invert_sums(n - WEIGHT_LAG)
-            leaky_relu(n - LEAKY_LAG)
-            quantise_tokens(n, 0)
+            quantise_tokens(n - 1, 1)
+            norm_step(n - 4, 5)
 
             copy_turned_tokens(n, 2)
-            first_matmul(n, 0)
-            add_to_sums(PACK * (n - EXP_LAG))
-            add_to_sums(PACK * (n - EXP_LAG) + 1)
-            exponentials(n - EXP_LAG, 2)
-            exponentials(n - EXP_LAG, 3)
-            sum_squares(n - LEAKY_LAG, 0)
-            sum_squares(n - LEAKY_LAG, 1)
-            regroup_on_vector(2 * n + 1)
-            normalise(n - WEIGHT_LAG)
-
+            guess_root(n - 3)
             copy_turned_tokens(n, 3)
+            square_guess(n - 3)
+            regroup_on_scalar(2 * n)
+            regroup_on_scalar(2 * n + 1)
+            first_matmul(n - 1, 1)
             second_matmul(n - OUT_LAG, 1)
-            add_to_sums(PACK * (n - EXP_LAG) + 2)
-            add_to_sums(PACK * (n - EXP_LAG) + 3)
-            sum_squares(n - LEAKY_LAG, 2)
-            sum_squares(n - LEAKY_LAG, 3)
-            start_root(n - LEAKY_LAG)
+            for j in range(PACK):
+                add_to_sums(PACK * (n - EXP_LAG) + j)
+            leaky_relu(n - 2)
+            norm_step(n - 4, 6)
+            regroup_on_vector(2 * n + 1)
+            norm_step(n - 4, 7)
             quantise_context(2 * n)
-            quantise_weights(n - WEIGHT_CODE_LAG)
-            if n % GROUPS == QUERY_STEP and n < ALL_GROUPS - GROUPS:
-                quantise_query(n // GROUPS + 1)
+            norm_step(n - 4, 8)
+            invert_sums(n - WEIGHT_LAG)
+            norm_step(n - 3, 0)
+            normalise(n - WEIGHT_LAG)
+            norm_step(n - 3, 1)
+
+        n = ALL_GROUPS
+        last = n - 1
+        slots = range(SLOTS * n, SLOTS * n + BEHIND)
+        pieces = [(quantise_context, SLOTS * n - 1)]
+        for slot in slots:
+            pieces += [(regroup_on_vector, slot), (quantise_context, slot)]
+        for place in range(1, len(pieces) - 2, 2):
+            pieces[place + 1], pieces[place + 2] = pieces[place + 2], pieces[place + 1]
+
+        def fill(count):
+            for what, slot in pieces[:count]:
+                what(slot)
+            pieces[:count] = []
+
+        damp(n - 2)
+        for i in (n - 6, n - 5):
+            for j in range(PACK):
+                exponentials(i, j)
+        for j in range(PACK):
+            sum_squares(n - 3, j)
+        quantise_tokens(last, 0)
+        quantise_tokens(last, 1)
+        first_matmul(last, 0)
+        first_matmul(last, 1)
+        for i in (n - 6, n - 5):
+            for j in range(PACK):
+                add_to_sums(PACK * i + j)
+        shift_squares(n - 3)
+        regroup_on_scalar(slots[0])
+        guess_root(n - 3)
+        regroup_on_scalar(slots[1])
+        square_guess(n - 3)
+        damp(last)
+        normalise(n - 9)
+        leaky_relu(n - 2)
+        fill(2)
+        quantise_weights(n - 10)
+        second_matmul(n - 10, 0)
+        second_matmul(n - 10, 1)
+        leaky_relu(last)
+        for j in range(PACK):
+            sum_squares(n - 2, j)
+        for j in range(PACK):
+            sum_squares(last, j)
+        regroup_on_scalar(slots[2])
+        shift_squares(last)
+        regroup_on_scalar(slots[3])
+        guess_root(last)
+        square_guess(last)
+        norm_step(n - 3, 0)
+        quantise_weights(n - 9)
+        second_matmul(n - 9, 0)
+        second_matmul(n - 9, 1)
+        store(n - 9)
+        norm_step(n - 3, 1)
+        fill(1)
+        norm_step(n - 3, 2)
+        invert_sums(n - 8)
+        fill(1)
+        norm_step(n - 3, 3)
+        normalise(n - 8)
+        norm_step(n - 3, 4)
+        normalise(n - 7)
+        norm_step(n - 3, 5)
+        quantise_weights(n - 8)
+        second_matmul(n - 8, 0)
+        second_matmul(n - 8, 1)
+        quantise_weights(n - 7)
+        second_matmul(n - 7, 0)
+        second_matmul(n - 7, 1)
+        norm_step(n - 3, 6)
+        normalise(n - 6)
+        norm_step(n - 3, 7)
+        normalise(n - 5)
+        norm_step(n - 3, 8)
+        for i in (n - 4, n - 3):
+            for j in range(PACK):
+                exponentials(i, j)
+        norm_step(last, 0)
+        fill(1)
+        norm_step(last, 1)
+        quantise_weights(n - 6)
+        second_matmul(n - 6, 0)
+        second_matmul(n - 6, 1)
+        fill(1)
+        norm_step(last, 2)
+        quantise_weights(n - 5)
+        second_matmul(n - 5, 0)
+        second_matmul(n - 5, 1)
+        store(n - 5)
+        for i in (n - 4, n - 3):
+            for j in range(PACK):
+                add_to_sums(PACK * i + j)
+        fill(1)
+        for k in range(3, 8):
+            norm_step(last, k)
+            fill(1)
+        norm_step(last, 8)
+        for i in (n - 2, last):
+            for j in range(PACK):
+                exponentials(i, j)
+            for j in range(PACK):
+                add_to_sums(PACK * i + j)
+        fill(len(pieces))
+        invert_sums(n - 4)
+        normalise(n - 4)
+        for i in range(n - 3, n + 1):
+            normalise(i)
+            quantise_weights(i - 1)
+            for h in range(D_BANKS):
+                second_matmul(i - 1, h)
+        store(last)

@@ -26,28 +26,28 @@ D_PASSES = D // K_PASS
 BANK = 512
 D_BANKS = D // BANK
 
-SCALAR_COLS = 192
-LATE_SCALAR_COLS = 192
-
 FIRST_PARTS = 2
 PREFETCH = 3
 TURN_LEAD = 3
-EXP_LAG = 6
-WEIGHT_LAG = 9
-OUT_LAG = 10
-STORE_LAG = 11
+LEAKY_LAG = 2
+SQUARE_LAG = 3
+EXP_LAG = 9
+WEIGHT_LAG = 13
+OUT_LAG = 14
 
 QUERY_PLACE = 3
 
 HALVES = 2
 HALF = D // HALVES
-SLOTS = 2
-BEHIND = 4
+ALL_HALVES = ALL_GROUPS * HALVES
+EVEN_FROM = 10
+LATE_HALF = 20
+LATE_SCALAR_COLS = 288
 
-PAIR = 2
 HALF_LN2 = 0.5 * math.log(2.0)
 CUBIC = math.sqrt(0.375)
 SHRINK = 1.0 / (24.0 * SMOOTH) ** 2
+CHAIN = 9
 
 FLOPS = 2 * 2 * B * Q * S * D
 
@@ -57,16 +57,15 @@ def tile_smcmr_pa_t_kernel(tc, query, context, out):
     with ExitStack() as stack:
         stack.enter_context(tc.manual_schedule())
         const = stack.enter_context(tc.tile_pool(name="const", bufs=1))
-        token_pool = stack.enter_context(tc.tile_pool(name="tokens", bufs=PREFETCH + BEHIND // HALVES + 2))
+        token_pool = stack.enter_context(tc.tile_pool(name="tokens", bufs=9))
         stage = stack.enter_context(tc.tile_pool(name="stage", bufs=2))
-        halves = stack.enter_context(tc.tile_pool(name="halves", bufs=5))
-        keep = stack.enter_context(tc.tile_pool(name="keep", bufs=2))
-        codes = stack.enter_context(tc.tile_pool(name="codes", bufs=OUT_LAG + 2))
-        soft = stack.enter_context(tc.tile_pool(name="soft", bufs=6))
-        small = stack.enter_context(tc.tile_pool(name="small", bufs=4))
+        halves = stack.enter_context(tc.tile_pool(name="halves", bufs=4))
+        codes = stack.enter_context(tc.tile_pool(name="codes", bufs=12))
+        soft = stack.enter_context(tc.tile_pool(name="soft", bufs=13))
+        small = stack.enter_context(tc.tile_pool(name="small", bufs=2))
         weight_pool = stack.enter_context(tc.tile_pool(name="weights", bufs=4))
-        query_pool = stack.enter_context(tc.tile_pool(name="query", bufs=B))
-        results = stack.enter_context(tc.tile_pool(name="results", bufs=2 * D_BANKS))
+        query_pool = stack.enter_context(tc.tile_pool(name="query", bufs=2))
+        results = stack.enter_context(tc.tile_pool(name="results", bufs=4))
         psum_turn = stack.enter_context(tc.psum_pool(name="psum_turn", bufs=TURN_LEAD))
         psum_score = stack.enter_context(tc.psum_pool(name="psum_score", bufs=2))
         psum_sum = stack.enter_context(tc.psum_pool(name="psum_sum", bufs=1))
@@ -139,7 +138,7 @@ def tile_smcmr_pa_t_kernel(tc, query, context, out):
             b, g = divmod(i, GROUPS)
             rows = token_pool.tile([P, PACK, D], BF16)
             source = context[b, g * K_PASS : (g + 1) * K_PASS, :].rearrange("(p j) d -> p j d", j=PACK)
-            parts = FIRST_PARTS if i == 0 else 1
+            parts = FIRST_PARTS if i < 2 else 1
             for part in range(parts):
                 tiles = slice(part * PACK // parts, (part + 1) * PACK // parts)
                 nc.sync.dma_start(out=rows[:, tiles, :], in_=source[:, tiles, :])
@@ -183,47 +182,45 @@ def tile_smcmr_pa_t_kernel(tc, query, context, out):
         def damp(i):
             if not is_group(i):
                 return
-            damped = stage.tile([P, PACK, Q], F32)
-            nc.scalar.mul(out=damped[:], in_=scores_of[i][:], mul=SLOPE)
-            damped_of[i] = damped
+            leaky = soft.tile([P, PACK, Q], F32)
+            nc.scalar.mul(out=leaky[:], in_=scores_of[i][:], mul=SLOPE)
+            leaky_of[i] = leaky
 
         def leaky_relu(i):
             if not is_group(i):
                 return
-            leaky = soft.tile([P, PACK, Q], F32)
-            nc.vector.tensor_tensor(out=leaky[:], in0=scores_of[i][:], in1=damped_of[i][:], op=ALU.max)
-            leaky_of[i] = leaky
+            nc.vector.tensor_tensor(out=leaky_of[i][:], in0=scores_of[i][:], in1=leaky_of[i][:], op=ALU.max)
 
         def sum_squares(i, j):
             if not is_group(i):
                 return
-            column = PACK * (i % PAIR) + j
+            column = PACK * (i % GROUPS) + j
             if column == 0:
-                squares = small.tile([P, PAIR * PACK], F32)
-                squares_of[i // PAIR] = squares
+                squares = small.tile([P, GROUPS * PACK], F32)
+                squares_of[i // GROUPS] = squares
             unused = stage.tile([P, Q], F32)
             nc.scalar.activation(
                 out=unused[:],
                 in_=leaky_of[i][:, j, :],
                 func=ACT.Square,
-                accum_out=squares_of[i // PAIR][:, column : column + 1],
+                accum_out=squares_of[i // GROUPS][:, column : column + 1],
             )
 
         def shift_squares(i):
-            if not is_group(i) or i % PAIR != PAIR - 1:
+            if not is_group(i) or i % GROUPS != GROUPS - 1:
                 return
-            shifted = small.tile([P, PAIR * PACK], F32)
+            shifted = small.tile([P, GROUPS * PACK], F32)
             nc.scalar.activation(
-                out=shifted[:], in_=squares_of[i // PAIR][:], func=ACT.Copy, scale=SHRINK, bias=EPS * SHRINK
+                out=shifted[:], in_=squares_of[i // GROUPS][:], func=ACT.Copy, scale=SHRINK, bias=EPS * SHRINK
             )
-            shifted_of[i // PAIR] = shifted
+            shifted_of[i // GROUPS] = shifted
 
         def guess_root(i):
-            if not is_group(i) or i % PAIR != PAIR - 1:
+            if not is_group(i) or i % GROUPS != GROUPS - 1:
                 return
-            pair = i // PAIR
+            pair = i // GROUPS
             shifted = shifted_of[pair]
-            guess = small.tile([P, PAIR * PACK], F32)
+            guess = small.tile([P, GROUPS * PACK], F32)
             nc.scalar.activation(
                 out=guess[:],
                 in_=shifted[:].bitcast(U32),
@@ -234,19 +231,19 @@ def tile_smcmr_pa_t_kernel(tc, query, context, out):
             guess_of[pair] = guess
 
         def square_guess(i):
-            if not is_group(i) or i % PAIR != PAIR - 1:
+            if not is_group(i) or i % GROUPS != GROUPS - 1:
                 return
-            pair = i // PAIR
-            guess_squared = small.tile([P, PAIR * PACK], F32)
+            pair = i // GROUPS
+            guess_squared = small.tile([P, GROUPS * PACK], F32)
             nc.scalar.activation(out=guess_squared[:], in_=guess_of[pair][:], func=ACT.Square, scale=math.sqrt(CUBIC))
             norm_of[pair] = (shifted_of[pair], guess_of[pair], guess_squared)
 
         def norm_step(i, k):
-            if not is_group(i) or i % PAIR != PAIR - 1:
+            if not is_group(i) or i % GROUPS != GROUPS - 1:
                 return
-            pair = i // PAIR
+            pair = i // GROUPS
             x, y, last = norm_of[pair]
-            shape = [P, PAIR * PACK]
+            shape = [P, GROUPS * PACK]
             if k == 0:
                 h = small.tile(shape, F32)
                 nc.vector.tensor_tensor(out=h[:], in0=last[:], in1=x[:], op=ALU.mult)
@@ -299,15 +296,12 @@ def tile_smcmr_pa_t_kernel(tc, query, context, out):
             if not is_group(i):
                 return
             b, g = divmod(i, GROUPS)
-            column = PACK * (i % PAIR) + j
-            if g == 0 and j == 0:
-                expo = keep.tile([P, GROUPS, PACK, Q], F32)
-                expo_of[b] = expo
+            column = PACK * (i % GROUPS) + j
             nc.scalar.activation(
-                out=expo_of[b][:, g, j, :],
+                out=leaky_of[i][:, j, :],
                 in_=leaky_of[i][:, j, :],
                 func=ACT.Exp,
-                scale=steep_of[i // PAIR][:, column : column + 1],
+                scale=steep_of[i // GROUPS][:, column : column + 1],
                 bias=-SMOOTH,
             )
 
@@ -322,24 +316,13 @@ def tile_smcmr_pa_t_kernel(tc, query, context, out):
             nc.tensor.matmul(
                 out=sums_of[b][:],
                 lhsT=ones[:],
-                rhs=expo_of[b][:, g, j, :],
+                rhs=leaky_of[i][:, j, :],
                 start=(g == 0 and j == 0),
                 stop=(g == GROUPS - 1 and j == PACK - 1),
             )
 
-        def half_of_slot(slot):
-            slots = ALL_GROUPS * SLOTS
-            if slot >= slots:
-                half = slot - BEHIND
-                return half if half < slots else None
-            half = max(slot, 0) * (slots - BEHIND) // slots
-            following = (slot + 1) * (slots - BEHIND) // slots
-            return half if half < following else None
-
         def scalar_columns(half):
-            if half >= ALL_GROUPS * HALVES - BEHIND:
-                return LATE_SCALAR_COLS
-            return SCALAR_COLS if half % HALVES == HALVES - 1 else 0
+            return LATE_SCALAR_COLS if half >= LATE_HALF else 0
 
         def regroup(half, engine_copy, first, last):
             i, h = divmod(half, HALVES)
@@ -351,19 +334,16 @@ def tile_smcmr_pa_t_kernel(tc, query, context, out):
                 in_=rows_of[i][:, :, h * HALF + first : h * HALF + last].rearrange("p j (n k) -> p n j k", k=4),
             )
 
-        def regroup_on_vector(slot):
-            half = half_of_slot(slot)
-            if half is not None:
+        def regroup_on_vector(half):
+            if half < ALL_HALVES:
                 regroup(half, nc.vector.tensor_copy, 0, HALF - scalar_columns(half))
 
-        def regroup_on_scalar(slot):
-            half = half_of_slot(slot)
-            if half is not None and scalar_columns(half):
+        def regroup_on_scalar(half):
+            if half < ALL_HALVES and scalar_columns(half):
                 regroup(half, nc.scalar.copy, HALF - scalar_columns(half), HALF)
 
-        def quantise_context(slot):
-            half = half_of_slot(slot)
-            if half is None:
+        def quantise_context(half):
+            if half >= ALL_HALVES:
                 return
             i, h = divmod(half, HALVES)
             if h == 0:
@@ -392,7 +372,7 @@ def tile_smcmr_pa_t_kernel(tc, query, context, out):
             weights = weight_pool.tile([P, Q, PACK], BF16, align_bytes=64)
             nc.vector.tensor_tensor(
                 out=weights[:],
-                in0=expo_of[b][:, g].rearrange("p j q -> p q j"),
+                in0=leaky_of[i][:].rearrange("p j q -> p q j"),
                 in1=inverse_of[b][:].unsqueeze(2).to_broadcast([P, Q, PACK]),
                 op=ALU.mult,
             )
@@ -455,167 +435,216 @@ def tile_smcmr_pa_t_kernel(tc, query, context, out):
         load_query(0)
         for i in range(1, PREFETCH):
             load(i)
-        for b in range(1, B):
-            load_query(b)
         for count in range(TURN_LEAD):
             turn_next(count)
 
+        done = {"regroup": 0, "quantise": 0, "scalar": 0}
+
+        def next_regroup():
+            regroup_on_vector(done["regroup"])
+            done["regroup"] += 1
+
+        def next_quantise():
+            if done["quantise"] < done["regroup"]:
+                quantise_context(done["quantise"])
+                done["quantise"] += 1
+
+        def next_on_scalar():
+            while done["scalar"] < ALL_HALVES and not scalar_columns(done["scalar"]):
+                done["scalar"] += 1
+            if done["scalar"] < min(ALL_HALVES, done["quantise"] + 4):
+                regroup_on_scalar(done["scalar"])
+                done["scalar"] += 1
+
+        chain = []
+
+        def tick():
+            if chain:
+                i, k = chain[0]
+                norm_step(i, k)
+                if k + 1 < CHAIN:
+                    chain[0] = (i, k + 1)
+                else:
+                    chain.pop(0)
+
+        next_regroup()
         for n in range(ALL_GROUPS):
             load(n + PREFETCH)
-            store(n - STORE_LAG)
+            if n % GROUPS == 1 and n // GROUPS + 1 < B:
+                load_query(n // GROUPS + 1)
+            late = n - 1 - SQUARE_LAG
 
             copy_turned_tokens(n, 0)
+            quantise_tokens(n - 1, 1)
+            guess_root(late)
             copy_turned_tokens(n, 1)
+            square_guess(late)
+            tick()
+            next_quantise()
+            tick()
             if n % GROUPS == 1:
                 quantise_query(n // GROUPS)
-            quantise_tokens(n - 1, 0)
-            norm_step(n - 4, 2)
-            quantise_context(2 * n - 1)
-            norm_step(n - 4, 3)
+            for j in range(PACK):
+                add_to_sums(PACK * (n - EXP_LAG - 1) + j)
             first_matmul(n - 1, 0)
-            for j in range(PACK):
-                sum_squares(n - 3, j)
-            damp(n - 2)
-            for j in range(PACK):
-                exponentials(n - EXP_LAG, j)
-            shift_squares(n - 3)
-            regroup_on_vector(2 * n)
-            norm_step(n - 4, 4)
-            quantise_weights(n - OUT_LAG)
-            second_matmul(n - OUT_LAG, 0)
-            quantise_tokens(n - 1, 1)
-            norm_step(n - 4, 5)
-
-            copy_turned_tokens(n, 2)
-            guess_root(n - 3)
-            copy_turned_tokens(n, 3)
-            square_guess(n - 3)
-            regroup_on_scalar(2 * n)
-            regroup_on_scalar(2 * n + 1)
             first_matmul(n - 1, 1)
+            damp(n - LEAKY_LAG)
+            second_matmul(n - OUT_LAG, 0)
             second_matmul(n - OUT_LAG, 1)
-            for j in range(PACK):
-                add_to_sums(PACK * (n - EXP_LAG) + j)
-            leaky_relu(n - 2)
-            norm_step(n - 4, 6)
-            regroup_on_vector(2 * n + 1)
-            norm_step(n - 4, 7)
-            quantise_context(2 * n)
-            norm_step(n - 4, 8)
+            if is_group(late) and late % GROUPS == GROUPS - 1:
+                chain.append((late, 0))
+            exponentials(n - EXP_LAG, 0)
+            exponentials(n - EXP_LAG, 1)
+            copy_turned_tokens(n, 2)
+            exponentials(n - EXP_LAG, 2)
+            exponentials(n - EXP_LAG, 3)
+            quantise_tokens(n, 0)
+            tick()
+            copy_turned_tokens(n, 3)
             invert_sums(n - WEIGHT_LAG)
-            norm_step(n - 3, 0)
+            leaky_relu(n - LEAKY_LAG)
+            if n == ALL_GROUPS - 1:
+                quantise_tokens(n, 1)
+            tick()
+            for j in range(PACK):
+                sum_squares(n - SQUARE_LAG, j)
+            next_regroup()
+            tick()
             normalise(n - WEIGHT_LAG)
-            norm_step(n - 3, 1)
+            if n >= EVEN_FROM and n % 2 == 0:
+                next_quantise()
+                next_regroup()
+            tick()
+            quantise_weights(n - WEIGHT_LAG)
+            shift_squares(n - SQUARE_LAG)
 
         n = ALL_GROUPS
         last = n - 1
-        slots = range(SLOTS * n, SLOTS * n + BEHIND)
-        pieces = [(quantise_context, SLOTS * n - 1)]
-        for slot in slots:
-            pieces += [(regroup_on_vector, slot), (quantise_context, slot)]
-        for place in range(1, len(pieces) - 2, 2):
-            pieces[place + 1], pieces[place + 2] = pieces[place + 2], pieces[place + 1]
 
         def fill(count):
-            for what, slot in pieces[:count]:
-                what(slot)
-            pieces[:count] = []
+            for piece in range(count):
+                if done["regroup"] - done["quantise"] > 1 or done["regroup"] == ALL_HALVES:
+                    next_quantise()
+                else:
+                    next_regroup()
 
-        damp(n - 2)
-        for i in (n - 6, n - 5):
+        def all_exponentials(i):
             for j in range(PACK):
                 exponentials(i, j)
-        for j in range(PACK):
-            sum_squares(n - 3, j)
-        quantise_tokens(last, 0)
-        quantise_tokens(last, 1)
+
+        def all_sums(i):
+            for j in range(PACK):
+                add_to_sums(PACK * i + j)
+
+        def all_squares(i):
+            for j in range(PACK):
+                sum_squares(i, j)
+
+        def all_second(i):
+            for h in range(D_BANKS):
+                second_matmul(i, h)
+
+        all_sums(6)
         first_matmul(last, 0)
         first_matmul(last, 1)
-        for i in (n - 6, n - 5):
-            for j in range(PACK):
-                add_to_sums(PACK * i + j)
-        shift_squares(n - 3)
-        regroup_on_scalar(slots[0])
-        guess_root(n - 3)
-        regroup_on_scalar(slots[1])
-        square_guess(n - 3)
+        next_on_scalar()
+        damp(14)
+        tick()
+        fill(1)
+        tick()
+        all_squares(13)
+        leaky_relu(14)
+        tick()
+        all_exponentials(7)
         damp(last)
-        normalise(n - 9)
-        leaky_relu(n - 2)
-        fill(2)
-        quantise_weights(n - 10)
-        second_matmul(n - 10, 0)
-        second_matmul(n - 10, 1)
+        next_on_scalar()
+        normalise(3)
+        tick()
+        all_second(2)
+        all_sums(7)
         leaky_relu(last)
-        for j in range(PACK):
-            sum_squares(n - 2, j)
-        for j in range(PACK):
-            sum_squares(last, j)
-        regroup_on_scalar(slots[2])
+        quantise_weights(3)
+        all_squares(14)
+        all_second(3)
+        fill(1)
+        all_squares(15)
+        next_on_scalar()
         shift_squares(last)
-        regroup_on_scalar(slots[3])
-        guess_root(last)
-        square_guess(last)
-        norm_step(n - 3, 0)
-        quantise_weights(n - 9)
-        second_matmul(n - 9, 0)
-        second_matmul(n - 9, 1)
-        store(n - 9)
-        norm_step(n - 3, 1)
-        fill(1)
-        norm_step(n - 3, 2)
-        invert_sums(n - 8)
-        fill(1)
-        norm_step(n - 3, 3)
-        normalise(n - 8)
-        norm_step(n - 3, 4)
-        normalise(n - 7)
-        norm_step(n - 3, 5)
-        quantise_weights(n - 8)
-        second_matmul(n - 8, 0)
-        second_matmul(n - 8, 1)
-        quantise_weights(n - 7)
-        second_matmul(n - 7, 0)
-        second_matmul(n - 7, 1)
-        norm_step(n - 3, 6)
-        normalise(n - 6)
-        norm_step(n - 3, 7)
-        normalise(n - 5)
-        norm_step(n - 3, 8)
-        for i in (n - 4, n - 3):
-            for j in range(PACK):
-                exponentials(i, j)
-        norm_step(last, 0)
-        fill(1)
-        norm_step(last, 1)
-        quantise_weights(n - 6)
-        second_matmul(n - 6, 0)
-        second_matmul(n - 6, 1)
-        fill(1)
-        norm_step(last, 2)
-        quantise_weights(n - 5)
-        second_matmul(n - 5, 0)
-        second_matmul(n - 5, 1)
-        store(n - 5)
-        for i in (n - 4, n - 3):
-            for j in range(PACK):
-                add_to_sums(PACK * i + j)
-        fill(1)
-        for k in range(3, 8):
-            norm_step(last, k)
+        while chain:
+            tick()
             fill(1)
-        norm_step(last, 8)
-        for i in (n - 2, last):
-            for j in range(PACK):
-                exponentials(i, j)
-            for j in range(PACK):
-                add_to_sums(PACK * i + j)
-        fill(len(pieces))
-        invert_sums(n - 4)
-        normalise(n - 4)
-        for i in range(n - 3, n + 1):
-            normalise(i)
-            quantise_weights(i - 1)
-            for h in range(D_BANKS):
-                second_matmul(i - 1, h)
+        invert_sums(4)
+        all_exponentials(8)
+        all_sums(8)
+        guess_root(last)
+        all_exponentials(9)
+        square_guess(last)
+        all_sums(9)
+        fill(1)
+        normalise(4)
+        fill(1)
+        normalise(5)
+        quantise_weights(4)
+        chain.append((last, 0))
+        tick()
+        all_exponentials(10)
+        all_exponentials(11)
+        all_sums(10)
+        next_on_scalar()
+        store(3)
+        normalise(6)
+        tick()
+        quantise_weights(5)
+        all_second(4)
+        all_sums(11)
+        all_second(5)
+        tick()
+        normalise(7)
+        tick()
+        quantise_weights(6)
+        all_second(6)
+        next_on_scalar()
+        tick()
+        fill(1)
+        quantise_weights(7)
+        while chain:
+            tick()
+            fill(1)
+        invert_sums(8)
+        for i in range(12, 16):
+            all_exponentials(i)
+            all_sums(i)
+            if i == 13:
+                all_second(7)
+        next_on_scalar()
+        fill(1)
+        for i in range(8, 13):
+            if i < 12:
+                normalise(i)
+                fill(1)
+            if i > 8:
+                quantise_weights(i - 1)
+                fill(1)
+            next_on_scalar()
+            if i == 9:
+                store(7)
+            if i > 8:
+                all_second(i - 1)
+        invert_sums(12)
+        fill(1)
+        for i in range(12, 17):
+            if i < 16:
+                normalise(i)
+                fill(1)
+            if i > 12:
+                quantise_weights(i - 1)
+                fill(1)
+            next_on_scalar()
+            if i == 13:
+                store(11)
+        while done["quantise"] < ALL_HALVES:
+            next_on_scalar()
+            fill(1)
+        for i in range(12, 16):
+            all_second(i)
         store(last)

@@ -32,17 +32,29 @@ TURN_LEAD = 3
 LEAKY_LAG = 2
 SQUARE_LAG = 3
 EXP_LAG = 9
-WEIGHT_LAG = 13
-OUT_LAG = 14
+WEIGHT_LAG = 14
+OUT_LAG = 15
 
 QUERY_PLACE = 3
 
-HALVES = 2
+HALVES = 4
 HALF = D // HALVES
 ALL_HALVES = ALL_GROUPS * HALVES
 EVEN_FROM = 10
+INV3 = 10
+S_FROM = 38
+S_EVERY = 2
+S_REST = 1
+EXTRA = 4
+PACE = 10
+LOOP_EXPS = 4
+RUN = 4
 LATE_HALF = 20
-LATE_SCALAR_COLS = 288
+LATE_SCALAR_COLS = 96
+EARLY_SCALAR_COLS = 288
+FIRST_WOVEN = 22
+WOVEN_COLS = 256
+SUM_COPIES = 128
 
 HALF_LN2 = 0.5 * math.log(2.0)
 CUBIC = math.sqrt(0.375)
@@ -57,11 +69,11 @@ def tile_smcmr_pa_t_kernel(tc, query, context, out):
     with ExitStack() as stack:
         stack.enter_context(tc.manual_schedule())
         const = stack.enter_context(tc.tile_pool(name="const", bufs=1))
-        token_pool = stack.enter_context(tc.tile_pool(name="tokens", bufs=9))
+        token_pool = stack.enter_context(tc.tile_pool(name="tokens", bufs=10))
         stage = stack.enter_context(tc.tile_pool(name="stage", bufs=2))
-        halves = stack.enter_context(tc.tile_pool(name="halves", bufs=4))
-        codes = stack.enter_context(tc.tile_pool(name="codes", bufs=12))
-        soft = stack.enter_context(tc.tile_pool(name="soft", bufs=13))
+        halves = stack.enter_context(tc.tile_pool(name="halves", bufs=8))
+        codes = stack.enter_context(tc.tile_pool(name="codes", bufs=11))
+        soft = stack.enter_context(tc.tile_pool(name="soft", bufs=14))
         small = stack.enter_context(tc.tile_pool(name="small", bufs=2))
         weight_pool = stack.enter_context(tc.tile_pool(name="weights", bufs=4))
         query_pool = stack.enter_context(tc.tile_pool(name="query", bufs=2))
@@ -70,10 +82,11 @@ def tile_smcmr_pa_t_kernel(tc, query, context, out):
         psum_score = stack.enter_context(tc.psum_pool(name="psum_score", bufs=2))
         psum_sum = stack.enter_context(tc.psum_pool(name="psum_sum", bufs=1))
         psum_out = stack.enter_context(tc.psum_pool(name="psum_out", bufs=D_BANKS))
+        unread = psum_out.tile([P, BANK], F32, tag="acc")
 
         identity = const.tile([P, P], F32)
         make_identity(nc, identity[:])
-        ones = const.tile([P, P], F32)
+        ones = const.tile([P, SUM_COPIES], F32)
         nc.vector.memset(ones[:], 1.0)
         q_codes = const.tile([P, B, D_PASSES, Q], U32, align_bytes=64)
         q_scales = const.tile([P, B, D_PASSES, Q], U8, align_bytes=64)
@@ -81,6 +94,7 @@ def tile_smcmr_pa_t_kernel(tc, query, context, out):
         rows_of, turned_of, grouped_of, token_codes_of, scores_of = {}, {}, {}, {}, {}
         damped_of, leaky_of, squares_of, steep_of = {}, {}, {}, {}
         norm_of, shifted_of, guess_of = {}, {}, {}
+        woven_of, column_of = {}, {}
         regrouped_of, weights_of, weight_codes_of = {}, {}, {}
         query_rows_of, query_grouped_of = {}, {}
         expo_of, sums_of, inverse_of, context_codes_of, acc_of = {}, {}, {}, {}, {}
@@ -101,9 +115,9 @@ def tile_smcmr_pa_t_kernel(tc, query, context, out):
 
         turn_order = []
         for tile_number in range(PACK * ALL_GROUPS):
-            b, place = divmod(tile_number, PACK * GROUPS)
-            if place == QUERY_PLACE:
-                turn_order.append(("query", b))
+            for b in range(B):
+                if tile_number == max(QUERY_PLACE, b * PACK * GROUPS - 1):
+                    turn_order.append(("query", b))
             turn_order.append(("tile", tile_number))
 
         def turn_next(count):
@@ -178,6 +192,19 @@ def tile_smcmr_pa_t_kernel(tc, query, context, out):
                         start=(c == 0),
                         stop=(c == D_PASSES - 1),
                     )
+
+        def keep_pace(i, pair):
+            t_codes, t_scales = token_codes_of[i]
+            tiles = slice(2 * pair, 2 * pair + 2)
+            nc.tensor.matmul_mx(
+                out=unread[:],
+                lhsT=q_codes[:, 0, 0, :].bitcast(FP8X4),
+                lhsT_scale=q_scales[:, 0, 0, :],
+                rhs=t_codes[:, tiles].rearrange("p j c r -> p (j c r)").bitcast(FP8X4),
+                rhs_scale=t_scales[:, tiles].rearrange("p j c r -> p (j c r)"),
+                start=True,
+                stop=True,
+            )
 
         def damp(i):
             if not is_group(i):
@@ -311,36 +338,37 @@ def tile_smcmr_pa_t_kernel(tc, query, context, out):
                 return
             b, g = divmod(i, GROUPS)
             if g == 0 and j == 0:
-                sums = psum_sum.tile([P, Q], F32)
+                sums = psum_sum.tile([P, 2, P], F32)
                 sums_of[b] = sums
             nc.tensor.matmul(
-                out=sums_of[b][:],
-                lhsT=ones[:],
-                rhs=leaky_of[i][:, j, :],
+                out=sums_of[b][:, 0, 0:SUM_COPIES],
+                lhsT=leaky_of[i][:, j, :],
+                rhs=ones[:],
                 start=(g == 0 and j == 0),
                 stop=(g == GROUPS - 1 and j == PACK - 1),
             )
 
-        def scalar_columns(half):
-            return LATE_SCALAR_COLS if half >= LATE_HALF else 0
+        def by_scalar(half):
+            return half >= S_FROM and half % S_EVERY >= S_REST
 
-        def regroup(half, engine_copy, first, last):
-            i, h = divmod(half, HALVES)
+        def open_half(half):
             if half not in regrouped_of:
                 regrouped = halves.tile([P, HALF, PACK], BF16, align_bytes=64)
                 regrouped_of[half] = regrouped
+
+        def regroup(half, engine_copy, first, last):
+            i, h = divmod(half, HALVES)
+            open_half(half)
             engine_copy(
-                out=regrouped_of[half][:, first:last, :].rearrange("p (n k) j -> p n j k", k=4),
-                in_=rows_of[i][:, :, h * HALF + first : h * HALF + last].rearrange("p j (n k) -> p n j k", k=4),
+                out=regrouped_of[half][:, first:last, :].rearrange("p (n k) j -> p n j k", k=RUN),
+                in_=rows_of[i][:, :, h * HALF + first : h * HALF + last].rearrange("p j (n k) -> p n j k", k=RUN),
             )
 
         def regroup_on_vector(half):
-            if half < ALL_HALVES:
-                regroup(half, nc.vector.tensor_copy, 0, HALF - scalar_columns(half))
+            regroup(half, nc.vector.tensor_copy, 0, HALF)
 
         def regroup_on_scalar(half):
-            if half < ALL_HALVES and scalar_columns(half):
-                regroup(half, nc.scalar.copy, HALF - scalar_columns(half), HALF)
+            regroup(half, nc.scalar.copy, 0, HALF)
 
         def quantise_context(half):
             if half >= ALL_HALVES:
@@ -357,13 +385,21 @@ def tile_smcmr_pa_t_kernel(tc, query, context, out):
                 in_=regrouped_of[half][:].rearrange("p d j -> p (d j)"),
             )
 
-        def invert_sums(i):
-            if not is_group(i) or i % GROUPS != 0:
-                return
-            b = i // GROUPS
-            inverse = stage.tile([P, Q], F32)
-            nc.vector.reciprocal(out=inverse[:], in_=sums_of[b][:])
-            inverse_of[b] = inverse
+        def invert_sums(b):
+            if 0 <= b < B:
+                column = small.tile([P, 1], F32)
+                nc.vector.reciprocal(out=column[:], in_=sums_of[b][:, 0, 0:1])
+                column_of[b] = column
+
+        def spread_inverse(b):
+            if 0 <= b < B:
+                nc.tensor.transpose(sums_of[b][:, 1, :], column_of[b][:].to_broadcast([P, P]), identity[:])
+
+        def copy_inverse(b):
+            if 0 <= b < B:
+                inverse = stage.tile([P, Q], F32)
+                nc.vector.tensor_copy(out=inverse[:], in_=sums_of[b][:, 1, :])
+                inverse_of[b] = inverse
 
         def normalise(i):
             if not is_group(i):
@@ -395,7 +431,7 @@ def tile_smcmr_pa_t_kernel(tc, query, context, out):
             w_codes, w_scales = weight_codes_of[i]
             c_codes, c_scales = context_codes_of[i]
             if g == 0:
-                acc = psum_out.tile([P, BANK], F32)
+                acc = psum_out.tile([P, BANK], F32, tag="acc")
                 acc_of[(b, h)] = acc
             nc.tensor.matmul_mx(
                 out=acc_of[(b, h)][:],
@@ -441,18 +477,22 @@ def tile_smcmr_pa_t_kernel(tc, query, context, out):
         done = {"regroup": 0, "quantise": 0, "scalar": 0}
 
         def next_regroup():
-            regroup_on_vector(done["regroup"])
-            done["regroup"] += 1
+            while done["regroup"] < ALL_HALVES and by_scalar(done["regroup"]):
+                done["regroup"] += 1
+            if done["regroup"] < ALL_HALVES:
+                regroup_on_vector(done["regroup"])
+                done["regroup"] += 1
 
         def next_quantise():
-            if done["quantise"] < done["regroup"]:
-                quantise_context(done["quantise"])
+            half = done["quantise"]
+            if half < (done["scalar"] if by_scalar(half) else done["regroup"]):
+                quantise_context(half)
                 done["quantise"] += 1
 
         def next_on_scalar():
-            while done["scalar"] < ALL_HALVES and not scalar_columns(done["scalar"]):
+            while done["scalar"] < ALL_HALVES and not by_scalar(done["scalar"]):
                 done["scalar"] += 1
-            if done["scalar"] < min(ALL_HALVES, done["quantise"] + 4):
+            if done["scalar"] < min(ALL_HALVES, done["quantise"] + 8):
                 regroup_on_scalar(done["scalar"])
                 done["scalar"] += 1
 
@@ -468,6 +508,7 @@ def tile_smcmr_pa_t_kernel(tc, query, context, out):
                     chain.pop(0)
 
         next_regroup()
+        next_regroup()
         for n in range(ALL_GROUPS):
             load(n + PREFETCH)
             if n % GROUPS == 1 and n // GROUPS + 1 < B:
@@ -480,17 +521,26 @@ def tile_smcmr_pa_t_kernel(tc, query, context, out):
             copy_turned_tokens(n, 1)
             square_guess(late)
             tick()
+            if n == WEIGHT_LAG:
+                invert_sums(0)
+                spread_inverse(0)
             next_quantise()
             tick()
-            if n % GROUPS == 1:
+            next_regroup()
+            tick()
+            if n == 1 or (n > 0 and n % GROUPS == 0):
                 quantise_query(n // GROUPS)
-            for j in range(PACK):
-                add_to_sums(PACK * (n - EXP_LAG - 1) + j)
-            first_matmul(n - 1, 0)
+            if n == WEIGHT_LAG:
+                copy_inverse(0)
+            add_to_sums(PACK * (n - EXP_LAG - 1))
+            add_to_sums(PACK * (n - EXP_LAG - 1) + 1)
+            if n == 1:
+                first_matmul(0, 0)
             first_matmul(n - 1, 1)
+            if 0 < n < PACE:
+                keep_pace(n - 1, 1)
             damp(n - LEAKY_LAG)
             second_matmul(n - OUT_LAG, 0)
-            second_matmul(n - OUT_LAG, 1)
             if is_group(late) and late % GROUPS == GROUPS - 1:
                 chain.append((late, 0))
             exponentials(n - EXP_LAG, 0)
@@ -500,21 +550,28 @@ def tile_smcmr_pa_t_kernel(tc, query, context, out):
             exponentials(n - EXP_LAG, 3)
             quantise_tokens(n, 0)
             tick()
+            next_quantise()
             copy_turned_tokens(n, 3)
-            invert_sums(n - WEIGHT_LAG)
             leaky_relu(n - LEAKY_LAG)
-            if n == ALL_GROUPS - 1:
-                quantise_tokens(n, 1)
             tick()
             for j in range(PACK):
                 sum_squares(n - SQUARE_LAG, j)
             next_regroup()
+            if n == ALL_GROUPS - 1:
+                quantise_tokens(n, 1)
             tick()
             normalise(n - WEIGHT_LAG)
-            if n >= EVEN_FROM and n % 2 == 0:
+            if EXP_LAG <= n < EXP_LAG + EXTRA:
                 next_quantise()
                 next_regroup()
             tick()
+            add_to_sums(PACK * (n - EXP_LAG - 1) + 2)
+            add_to_sums(PACK * (n - EXP_LAG - 1) + 3)
+            second_matmul(n - OUT_LAG, 1)
+            if n > 0:
+                first_matmul(n, 0)
+                if n < PACE:
+                    keep_pace(n, 0)
             quantise_weights(n - WEIGHT_LAG)
             shift_squares(n - SQUARE_LAG)
 
@@ -523,7 +580,7 @@ def tile_smcmr_pa_t_kernel(tc, query, context, out):
 
         def fill(count):
             for piece in range(count):
-                if done["regroup"] - done["quantise"] > 1 or done["regroup"] == ALL_HALVES:
+                if done["regroup"] - done["quantise"] > 2 or done["regroup"] == ALL_HALVES:
                     next_quantise()
                 else:
                     next_regroup()
@@ -544,107 +601,100 @@ def tile_smcmr_pa_t_kernel(tc, query, context, out):
             for h in range(D_BANKS):
                 second_matmul(i, h)
 
-        all_sums(6)
-        first_matmul(last, 0)
-        first_matmul(last, 1)
-        next_on_scalar()
         damp(14)
         tick()
         fill(1)
         tick()
+        all_sums(6)
+        first_matmul(last, 1)
         all_squares(13)
         leaky_relu(14)
         tick()
         all_exponentials(7)
-        damp(last)
+        all_sums(7)
+        all_second(1)
         next_on_scalar()
+        damp(last)
+        normalise(2)
+        tick()
+        fill(2)
+        tick()
+        leaky_relu(last)
+        tick()
+        quantise_weights(2)
+        all_second(2)
         normalise(3)
         tick()
-        all_second(2)
-        all_sums(7)
-        leaky_relu(last)
-        quantise_weights(3)
         all_squares(14)
-        all_second(3)
-        fill(1)
-        all_squares(15)
         next_on_scalar()
-        shift_squares(last)
+        fill(2)
+        tick()
+        quantise_weights(3)
+        invert_sums(1)
+        spread_inverse(1)
+        all_second(3)
+        fill(2)
+        tick()
+        copy_inverse(1)
         while chain:
-            tick()
             fill(1)
-        invert_sums(4)
+            tick()
+        all_squares(last)
+        shift_squares(last)
         all_exponentials(8)
-        all_sums(8)
         guess_root(last)
         all_exponentials(9)
         square_guess(last)
-        all_sums(9)
-        fill(1)
+        next_on_scalar()
+        all_exponentials(10)
+        all_exponentials(11)
+        for i in range(8, 12):
+            all_sums(i)
         normalise(4)
-        fill(1)
-        normalise(5)
+        fill(2)
         quantise_weights(4)
         chain.append((last, 0))
         tick()
-        all_exponentials(10)
-        all_exponentials(11)
-        all_sums(10)
-        next_on_scalar()
-        store(3)
-        normalise(6)
-        tick()
-        quantise_weights(5)
-        all_second(4)
-        all_sums(11)
-        all_second(5)
-        tick()
-        normalise(7)
-        tick()
-        quantise_weights(6)
-        all_second(6)
-        next_on_scalar()
-        tick()
         fill(1)
-        quantise_weights(7)
-        while chain:
+        tick()
+        for i in range(5, 16):
+            b, g = divmod(i, GROUPS)
+            next_on_scalar()
+            if g == 2:
+                store(GROUPS * b - 1)
+            if i == INV3:
+                invert_sums(3)
+                spread_inverse(3)
+            normalise(i)
             tick()
-            fill(1)
-        invert_sums(8)
-        for i in range(12, 16):
-            all_exponentials(i)
-            all_sums(i)
-            if i == 13:
-                all_second(7)
-        next_on_scalar()
-        fill(1)
-        for i in range(8, 13):
-            if i < 12:
-                normalise(i)
-                fill(1)
-            if i > 8:
+            fill(2)
+            tick()
+            if i > 5:
                 quantise_weights(i - 1)
-                fill(1)
-            next_on_scalar()
-            if i == 9:
-                store(7)
-            if i > 8:
+            tick()
+            fill(2)
+            tick()
+            if i == 6:
+                copy_inverse(2)
+            if 6 <= i < 8:
+                for k in range(2 * i, 2 * i + 2):
+                    all_exponentials(k)
+            if g == 2:
+                all_second(i - 2)
+            if g != 1:
                 all_second(i - 1)
-        invert_sums(12)
-        fill(1)
-        for i in range(12, 17):
-            if i < 16:
-                normalise(i)
-                fill(1)
-            if i > 12:
-                quantise_weights(i - 1)
-                fill(1)
+            if 6 <= i < 8:
+                for k in range(2 * i, 2 * i + 2):
+                    all_sums(k)
             next_on_scalar()
-            if i == 13:
-                store(11)
+            if i == 5:
+                invert_sums(2)
+                spread_inverse(2)
+            if i == INV3 + 1:
+                copy_inverse(3)
         while done["quantise"] < ALL_HALVES:
             next_on_scalar()
             fill(1)
-        for i in range(12, 16):
-            all_second(i)
+        quantise_weights(last)
+        all_second(last)
         store(last)

@@ -37,16 +37,18 @@ OUT_LAG = 15
 
 QUERY_PLACE = 3
 
-HALVES = 4
+HALVES = 2
 HALF = D // HALVES
 ALL_HALVES = ALL_GROUPS * HALVES
 EVEN_FROM = 10
 INV3 = 10
-S_FROM = 38
-S_EVERY = 2
-S_REST = 1
-EXTRA = 4
-PACE = 10
+PACE_FROM = 1
+LAST_PACE = 6
+LATE = 9
+V_LATE = 512
+WOVEN = 128
+EXTRA = 1
+PACE = 11
 LOOP_EXPS = 4
 RUN = 4
 LATE_HALF = 20
@@ -60,6 +62,7 @@ HALF_LN2 = 0.5 * math.log(2.0)
 CUBIC = math.sqrt(0.375)
 SHRINK = 1.0 / (24.0 * SMOOTH) ** 2
 CHAIN = 9
+PAIR = 2
 
 FLOPS = 2 * 2 * B * Q * S * D
 
@@ -69,13 +72,13 @@ def tile_smcmr_pa_t_kernel(tc, query, context, out):
     with ExitStack() as stack:
         stack.enter_context(tc.manual_schedule())
         const = stack.enter_context(tc.tile_pool(name="const", bufs=1))
-        token_pool = stack.enter_context(tc.tile_pool(name="tokens", bufs=10))
+        token_pool = stack.enter_context(tc.tile_pool(name="tokens", bufs=9))
         stage = stack.enter_context(tc.tile_pool(name="stage", bufs=2))
-        halves = stack.enter_context(tc.tile_pool(name="halves", bufs=8))
+        halves = stack.enter_context(tc.tile_pool(name="halves", bufs=2))
         codes = stack.enter_context(tc.tile_pool(name="codes", bufs=11))
-        soft = stack.enter_context(tc.tile_pool(name="soft", bufs=14))
+        soft = stack.enter_context(tc.tile_pool(name="soft", bufs=8))
         small = stack.enter_context(tc.tile_pool(name="small", bufs=2))
-        weight_pool = stack.enter_context(tc.tile_pool(name="weights", bufs=4))
+        weight_pool = stack.enter_context(tc.tile_pool(name="weights", bufs=3))
         query_pool = stack.enter_context(tc.tile_pool(name="query", bufs=2))
         results = stack.enter_context(tc.tile_pool(name="results", bufs=4))
         psum_turn = stack.enter_context(tc.psum_pool(name="psum_turn", bufs=TURN_LEAD))
@@ -83,9 +86,12 @@ def tile_smcmr_pa_t_kernel(tc, query, context, out):
         psum_sum = stack.enter_context(tc.psum_pool(name="psum_sum", bufs=1))
         psum_out = stack.enter_context(tc.psum_pool(name="psum_out", bufs=D_BANKS))
         unread = psum_out.tile([P, BANK], F32, tag="acc")
+        unread_of = {0: unread}
 
         identity = const.tile([P, P], F32)
         make_identity(nc, identity[:])
+        identity_bf16 = const.tile([P, P], BF16)
+        nc.vector.tensor_copy(out=identity_bf16[:], in_=identity[:])
         ones = const.tile([P, SUM_COPIES], F32)
         nc.vector.memset(ones[:], 1.0)
         q_codes = const.tile([P, B, D_PASSES, Q], U32, align_bytes=64)
@@ -94,7 +100,7 @@ def tile_smcmr_pa_t_kernel(tc, query, context, out):
         rows_of, turned_of, grouped_of, token_codes_of, scores_of = {}, {}, {}, {}, {}
         damped_of, leaky_of, squares_of, steep_of = {}, {}, {}, {}
         norm_of, shifted_of, guess_of = {}, {}, {}
-        woven_of, column_of = {}, {}
+        pair_of, column_of, woven_of = {}, {}, {}
         regrouped_of, weights_of, weight_codes_of = {}, {}, {}
         query_rows_of, query_grouped_of = {}, {}
         expo_of, sums_of, inverse_of, context_codes_of, acc_of = {}, {}, {}, {}, {}
@@ -158,19 +164,16 @@ def tile_smcmr_pa_t_kernel(tc, query, context, out):
                 nc.sync.dma_start(out=rows[:, tiles, :], in_=source[:, tiles, :])
             rows_of[i] = rows
 
-        def quantise_tokens(i, pair):
+        def quantise_tokens(i):
             if not is_group(i):
                 return
-            if pair == 0:
-                t_codes = stage.tile([P, PACK, D_PASSES, P], U32, align_bytes=64)
-                t_scales = stage.tile([P, PACK, D_PASSES, P], U8, align_bytes=64)
-                token_codes_of[i] = (t_codes, t_scales)
-            t_codes, t_scales = token_codes_of[i]
-            tiles = slice(2 * pair, 2 * pair + 2)
+            t_codes = stage.tile([P, PACK, D_PASSES, P], U32, align_bytes=64)
+            t_scales = stage.tile([P, PACK, D_PASSES, P], U8, align_bytes=64)
+            token_codes_of[i] = (t_codes, t_scales)
             nc.vector.quantize_mx(
-                out=t_codes[:, tiles].rearrange("p j c r -> p (j c r)").bitcast(FP8X4),
-                scales=t_scales[:, tiles].rearrange("p j c r -> p (j c r)"),
-                in_=grouped_of[i][:, tiles].rearrange("p j c r t -> p (j c r t)"),
+                out=t_codes[:].rearrange("p j c r -> p (j c r)").bitcast(FP8X4),
+                scales=t_scales[:].rearrange("p j c r -> p (j c r)"),
+                in_=grouped_of[i][:].rearrange("p j c r t -> p (j c r t)"),
             )
 
         def first_matmul(i, pair):
@@ -197,7 +200,7 @@ def tile_smcmr_pa_t_kernel(tc, query, context, out):
             t_codes, t_scales = token_codes_of[i]
             tiles = slice(2 * pair, 2 * pair + 2)
             nc.tensor.matmul_mx(
-                out=unread[:],
+                out=unread_of[0][:],
                 lhsT=q_codes[:, 0, 0, :].bitcast(FP8X4),
                 lhsT_scale=q_scales[:, 0, 0, :],
                 rhs=t_codes[:, tiles].rearrange("p j c r -> p (j c r)").bitcast(FP8X4),
@@ -209,14 +212,16 @@ def tile_smcmr_pa_t_kernel(tc, query, context, out):
         def damp(i):
             if not is_group(i):
                 return
-            leaky = soft.tile([P, PACK, Q], F32)
-            nc.scalar.mul(out=leaky[:], in_=scores_of[i][:], mul=SLOPE)
-            leaky_of[i] = leaky
+            if i % PAIR == 0:
+                pair = soft.tile([P, PAIR, PACK, Q], F32)
+                pair_of[i // PAIR] = pair
+            leaky_of[i] = pair_of[i // PAIR][:, i % PAIR]
+            nc.scalar.mul(out=leaky_of[i], in_=scores_of[i][:], mul=SLOPE)
 
         def leaky_relu(i):
             if not is_group(i):
                 return
-            nc.vector.tensor_tensor(out=leaky_of[i][:], in0=scores_of[i][:], in1=leaky_of[i][:], op=ALU.max)
+            nc.vector.tensor_tensor(out=leaky_of[i], in0=scores_of[i][:], in1=leaky_of[i], op=ALU.max)
 
         def sum_squares(i, j):
             if not is_group(i):
@@ -225,7 +230,7 @@ def tile_smcmr_pa_t_kernel(tc, query, context, out):
             if column == 0:
                 squares = small.tile([P, GROUPS * PACK], F32)
                 squares_of[i // GROUPS] = squares
-            unused = stage.tile([P, Q], F32)
+            unused = stage.tile([P, Q], F32, bufs=4)
             nc.scalar.activation(
                 out=unused[:],
                 in_=leaky_of[i][:, j, :],
@@ -348,41 +353,46 @@ def tile_smcmr_pa_t_kernel(tc, query, context, out):
                 stop=(g == GROUPS - 1 and j == PACK - 1),
             )
 
-        def by_scalar(half):
-            return half >= S_FROM and half % S_EVERY >= S_REST
-
-        def open_half(half):
-            if half not in regrouped_of:
-                regrouped = halves.tile([P, HALF, PACK], BF16, align_bytes=64)
-                regrouped_of[half] = regrouped
-
-        def regroup(half, engine_copy, first, last):
-            i, h = divmod(half, HALVES)
-            open_half(half)
+        def regroup(i, engine_copy, first, last):
+            if i not in regrouped_of:
+                regrouped = halves.tile([P, D, PACK], BF16, align_bytes=64)
+                regrouped_of[i] = regrouped
             engine_copy(
-                out=regrouped_of[half][:, first:last, :].rearrange("p (n k) j -> p n j k", k=RUN),
-                in_=rows_of[i][:, :, h * HALF + first : h * HALF + last].rearrange("p j (n k) -> p n j k", k=RUN),
+                out=regrouped_of[i][:, first:last, :].rearrange("p (n k) j -> p n j k", k=RUN),
+                in_=rows_of[i][:, :, first:last].rearrange("p j (n k) -> p n j k", k=RUN),
             )
 
-        def regroup_on_vector(half):
-            regroup(half, nc.vector.tensor_copy, 0, HALF)
+        def weave(i):
+            if LATE <= i < ALL_GROUPS and i not in woven_of:
+                woven = psum_turn.tile([P, D_BANKS, BANK], BF16, tag="turned")
+                features = BANK // PACK
+                for m in range(WOVEN // features):
+                    first = D - WOVEN + m * features
+                    nc.tensor.matmul(
+                        out=woven[:, m, :],
+                        lhsT=identity_bf16[:],
+                        rhs=rows_of[i][:, :, first : first + features].rearrange("p j d -> p d j"),
+                        start=True,
+                        stop=True,
+                    )
+                woven_of[i] = woven
 
-        def regroup_on_scalar(half):
-            regroup(half, nc.scalar.copy, 0, HALF)
+        def copy_woven(i):
+            nc.scalar.copy(
+                out=regrouped_of[i][:, D - WOVEN :, :].rearrange("p d j -> p (d j)"),
+                in_=woven_of[i][:, 0 : WOVEN // (BANK // PACK), :].rearrange("p m c -> p (m c)"),
+            )
 
-        def quantise_context(half):
-            if half >= ALL_HALVES:
-                return
-            i, h = divmod(half, HALVES)
-            if h == 0:
+        def quantise_context(i, first, last):
+            if first == 0:
                 c_codes = codes.tile([P, D], U32, align_bytes=64)
                 c_scales = codes.tile([P, D], U8, align_bytes=64)
                 context_codes_of[i] = (c_codes, c_scales)
             c_codes, c_scales = context_codes_of[i]
             nc.vector.quantize_mx(
-                out=c_codes[:, h * HALF : (h + 1) * HALF].bitcast(FP8X4),
-                scales=c_scales[:, h * HALF : (h + 1) * HALF],
-                in_=regrouped_of[half][:].rearrange("p d j -> p (d j)"),
+                out=c_codes[:, first:last].bitcast(FP8X4),
+                scales=c_scales[:, first:last],
+                in_=regrouped_of[i][:, first:last, :].rearrange("p d j -> p (d j)"),
             )
 
         def invert_sums(b):
@@ -401,42 +411,44 @@ def tile_smcmr_pa_t_kernel(tc, query, context, out):
                 nc.vector.tensor_copy(out=inverse[:], in_=sums_of[b][:, 1, :])
                 inverse_of[b] = inverse
 
-        def normalise(i):
-            if not is_group(i):
+        def normalise(k):
+            if not 0 <= k < ALL_GROUPS // PAIR:
                 return
-            b, g = divmod(i, GROUPS)
-            weights = weight_pool.tile([P, Q, PACK], BF16, align_bytes=64)
+            weights = weight_pool.tile([P, PAIR, Q, PACK], BF16, align_bytes=64)
+            inverse = inverse_of[PAIR * k // GROUPS]
             nc.vector.tensor_tensor(
                 out=weights[:],
-                in0=leaky_of[i][:].rearrange("p j q -> p q j"),
-                in1=inverse_of[b][:].unsqueeze(2).to_broadcast([P, Q, PACK]),
+                in0=pair_of[k][:].rearrange("p g j q -> p g q j"),
+                in1=inverse[:].unsqueeze(1).unsqueeze(3).to_broadcast([P, PAIR, Q, PACK]),
                 op=ALU.mult,
             )
-            weights_of[i] = weights
+            weights_of[k] = weights
 
-        def quantise_weights(i):
-            if not is_group(i):
+        def quantise_weights(k):
+            if not 0 <= k < ALL_GROUPS // PAIR:
                 return
-            w_codes = weight_pool.tile([P, Q], U32, align_bytes=64)
-            w_scales = weight_pool.tile([P, Q], U8, align_bytes=64)
+            w_codes = weight_pool.tile([P, PAIR, Q], U32, align_bytes=64)
+            w_scales = weight_pool.tile([P, PAIR, Q], U8, align_bytes=64)
             nc.vector.quantize_mx(
-                out=w_codes[:].bitcast(FP8X4), scales=w_scales[:], in_=weights_of[i][:].rearrange("p q j -> p (q j)")
+                out=w_codes[:].rearrange("p g q -> p (g q)").bitcast(FP8X4),
+                scales=w_scales[:].rearrange("p g q -> p (g q)"),
+                in_=weights_of[k][:].rearrange("p g q j -> p (g q j)"),
             )
-            weight_codes_of[i] = (w_codes, w_scales)
+            weight_codes_of[k] = (w_codes, w_scales)
 
         def second_matmul(i, h):
             if not is_group(i):
                 return
             b, g = divmod(i, GROUPS)
-            w_codes, w_scales = weight_codes_of[i]
+            w_codes, w_scales = weight_codes_of[i // PAIR]
             c_codes, c_scales = context_codes_of[i]
             if g == 0:
                 acc = psum_out.tile([P, BANK], F32, tag="acc")
                 acc_of[(b, h)] = acc
             nc.tensor.matmul_mx(
                 out=acc_of[(b, h)][:],
-                lhsT=w_codes[:].bitcast(FP8X4),
-                lhsT_scale=w_scales[:],
+                lhsT=w_codes[:, i % PAIR, :].bitcast(FP8X4),
+                lhsT_scale=w_scales[:, i % PAIR, :],
                 rhs=c_codes[:, h * BANK : (h + 1) * BANK].bitcast(FP8X4),
                 rhs_scale=c_scales[:, h * BANK : (h + 1) * BANK],
                 start=(g == 0),
@@ -477,24 +489,32 @@ def tile_smcmr_pa_t_kernel(tc, query, context, out):
         done = {"regroup": 0, "quantise": 0, "scalar": 0}
 
         def next_regroup():
-            while done["regroup"] < ALL_HALVES and by_scalar(done["regroup"]):
-                done["regroup"] += 1
-            if done["regroup"] < ALL_HALVES:
-                regroup_on_vector(done["regroup"])
+            i, h = divmod(done["regroup"], HALVES)
+            if i < ALL_GROUPS and i < done["quantise"] // HALVES + 2:
+                size = HALF if i < LATE else V_LATE // HALVES
+                regroup(i, nc.vector.tensor_copy, h * size, (h + 1) * size)
                 done["regroup"] += 1
 
         def next_quantise():
-            half = done["quantise"]
-            if half < (done["scalar"] if by_scalar(half) else done["regroup"]):
-                quantise_context(half)
+            i, h = divmod(done["quantise"], HALVES)
+            if i >= ALL_GROUPS or done["regroup"] < HALVES * (i + 1):
+                return
+            if i < LATE:
+                quantise_context(i, 0, D)
+                done["quantise"] += HALVES
+            elif h == 0 or done["scalar"] >= HALVES * (i + 1):
+                quantise_context(i, h * HALF, (h + 1) * HALF)
                 done["quantise"] += 1
 
         def next_on_scalar():
-            while done["scalar"] < ALL_HALVES and not by_scalar(done["scalar"]):
-                done["scalar"] += 1
-            if done["scalar"] < min(ALL_HALVES, done["quantise"] + 8):
-                regroup_on_scalar(done["scalar"])
-                done["scalar"] += 1
+            i, h = divmod(max(HALVES * LATE, done["scalar"]), HALVES)
+            if i < ALL_GROUPS and i < done["quantise"] // HALVES + 2:
+                if h == 0:
+                    regroup(i, nc.scalar.copy, V_LATE, D - WOVEN)
+                else:
+                    copy_woven(i)
+                    weave(i + 2)
+                done["scalar"] = HALVES * i + h + 1
 
         chain = []
 
@@ -508,7 +528,6 @@ def tile_smcmr_pa_t_kernel(tc, query, context, out):
                     chain.pop(0)
 
         next_regroup()
-        next_regroup()
         for n in range(ALL_GROUPS):
             load(n + PREFETCH)
             if n % GROUPS == 1 and n // GROUPS + 1 < B:
@@ -516,74 +535,57 @@ def tile_smcmr_pa_t_kernel(tc, query, context, out):
             late = n - 1 - SQUARE_LAG
 
             copy_turned_tokens(n, 0)
-            quantise_tokens(n - 1, 1)
             guess_root(late)
+            if n == 1 or (n > 0 and n % GROUPS == 0):
+                quantise_query(n // GROUPS)
+            quantise_tokens(n - 1)
             copy_turned_tokens(n, 1)
             square_guess(late)
-            tick()
             if n == WEIGHT_LAG:
                 invert_sums(0)
                 spread_inverse(0)
-            next_quantise()
             tick()
             next_regroup()
-            tick()
-            if n == 1 or (n > 0 and n % GROUPS == 0):
-                quantise_query(n // GROUPS)
-            if n == WEIGHT_LAG:
-                copy_inverse(0)
-            add_to_sums(PACK * (n - EXP_LAG - 1))
-            add_to_sums(PACK * (n - EXP_LAG - 1) + 1)
-            if n == 1:
-                first_matmul(0, 0)
-            first_matmul(n - 1, 1)
-            if 0 < n < PACE:
-                keep_pace(n - 1, 1)
-            damp(n - LEAKY_LAG)
-            second_matmul(n - OUT_LAG, 0)
             if is_group(late) and late % GROUPS == GROUPS - 1:
                 chain.append((late, 0))
+            if n == WEIGHT_LAG:
+                copy_inverse(0)
+            tick()
+            damp(n - LEAKY_LAG)
             exponentials(n - EXP_LAG, 0)
             exponentials(n - EXP_LAG, 1)
+            leaky_relu(n - LEAKY_LAG)
+            tick()
+            add_to_sums(PACK * (n - EXP_LAG - 1))
+            add_to_sums(PACK * (n - EXP_LAG - 1) + 1)
+            first_matmul(n - 1, 0)
+            first_matmul(n - 1, 1)
+            if PACE_FROM <= n < PACE:
+                keep_pace(n - 1, 1)
             copy_turned_tokens(n, 2)
             exponentials(n - EXP_LAG, 2)
             exponentials(n - EXP_LAG, 3)
-            quantise_tokens(n, 0)
-            tick()
-            next_quantise()
             copy_turned_tokens(n, 3)
-            leaky_relu(n - LEAKY_LAG)
-            tick()
-            for j in range(PACK):
-                sum_squares(n - SQUARE_LAG, j)
-            next_regroup()
-            if n == ALL_GROUPS - 1:
-                quantise_tokens(n, 1)
-            tick()
-            normalise(n - WEIGHT_LAG)
-            if EXP_LAG <= n < EXP_LAG + EXTRA:
+            if n > 0:
                 next_quantise()
-                next_regroup()
             tick()
             add_to_sums(PACK * (n - EXP_LAG - 1) + 2)
             add_to_sums(PACK * (n - EXP_LAG - 1) + 3)
-            second_matmul(n - OUT_LAG, 1)
-            if n > 0:
-                first_matmul(n, 0)
-                if n < PACE:
-                    keep_pace(n, 0)
-            quantise_weights(n - WEIGHT_LAG)
+            if PACE_FROM <= n < PACE:
+                keep_pace(n - 1, 0)
+                keep_pace(n - 1, 1)
+            for j in range(PACK):
+                sum_squares(n - SQUARE_LAG, j)
+            if EXP_LAG <= n < EXP_LAG + EXTRA:
+                next_regroup()
+            if n >= WEIGHT_LAG and n % PAIR == 0:
+                normalise((n - WEIGHT_LAG) // PAIR)
+            if n % GROUPS == 0:
+                tick()
             shift_squares(n - SQUARE_LAG)
 
         n = ALL_GROUPS
         last = n - 1
-
-        def fill(count):
-            for piece in range(count):
-                if done["regroup"] - done["quantise"] > 2 or done["regroup"] == ALL_HALVES:
-                    next_quantise()
-                else:
-                    next_regroup()
 
         def all_exponentials(i):
             for j in range(PACK):
@@ -601,100 +603,145 @@ def tile_smcmr_pa_t_kernel(tc, query, context, out):
             for h in range(D_BANKS):
                 second_matmul(i, h)
 
+        quantise_tokens(last)
+        tick()
         damp(14)
+        quantise_weights(0)
         tick()
-        fill(1)
-        tick()
+        weave(LATE)
+        weave(LATE + 1)
         all_sums(6)
+        first_matmul(last, 0)
         first_matmul(last, 1)
+        all_second(0)
+        all_second(1)
         all_squares(13)
         leaky_relu(14)
         tick()
         all_exponentials(7)
         all_sums(7)
-        all_second(1)
-        next_on_scalar()
+        normalise(1)
+        tick()
         damp(last)
-        normalise(2)
-        tick()
-        fill(2)
-        tick()
-        leaky_relu(last)
-        tick()
-        quantise_weights(2)
-        all_second(2)
-        normalise(3)
-        tick()
         all_squares(14)
-        next_on_scalar()
-        fill(2)
+        quantise_weights(1)
         tick()
-        quantise_weights(3)
-        invert_sums(1)
-        spread_inverse(1)
+        all_second(2)
         all_second(3)
-        fill(2)
-        tick()
-        copy_inverse(1)
+        leaky_relu(last)
         while chain:
-            fill(1)
             tick()
         all_squares(last)
         shift_squares(last)
-        all_exponentials(8)
+        exponentials(8, 0)
+        exponentials(8, 1)
         guess_root(last)
-        all_exponentials(9)
+        exponentials(8, 2)
+        exponentials(8, 3)
         square_guess(last)
-        next_on_scalar()
+        invert_sums(1)
+        spread_inverse(1)
+        next_regroup()
+        next_regroup()
+        copy_inverse(1)
+        all_exponentials(9)
         all_exponentials(10)
         all_exponentials(11)
         for i in range(8, 12):
             all_sums(i)
-        normalise(4)
-        fill(2)
-        quantise_weights(4)
+        normalise(2)
         chain.append((last, 0))
         tick()
-        fill(1)
+        next_regroup()
         tick()
-        for i in range(5, 16):
-            b, g = divmod(i, GROUPS)
-            next_on_scalar()
-            if g == 2:
-                store(GROUPS * b - 1)
-            if i == INV3:
-                invert_sums(3)
-                spread_inverse(3)
-            normalise(i)
-            tick()
-            fill(2)
-            tick()
-            if i > 5:
-                quantise_weights(i - 1)
-            tick()
-            fill(2)
-            tick()
-            if i == 6:
-                copy_inverse(2)
-            if 6 <= i < 8:
-                for k in range(2 * i, 2 * i + 2):
-                    all_exponentials(k)
-            if g == 2:
-                all_second(i - 2)
-            if g != 1:
-                all_second(i - 1)
-            if 6 <= i < 8:
-                for k in range(2 * i, 2 * i + 2):
-                    all_sums(k)
-            next_on_scalar()
-            if i == 5:
-                invert_sums(2)
-                spread_inverse(2)
-            if i == INV3 + 1:
-                copy_inverse(3)
-        while done["quantise"] < ALL_HALVES:
-            next_on_scalar()
-            fill(1)
-        quantise_weights(last)
-        all_second(last)
+        quantise_weights(2)
+        next_on_scalar()
+        next_on_scalar()
+        tick()
+        next_regroup()
+        tick()
+        normalise(3)
+        tick()
+        store(3)
+        all_second(4)
+        tick()
+        quantise_weights(3)
+        tick()
+        invert_sums(2)
+        spread_inverse(2)
+        all_second(5)
+        next_quantise()
+        tick()
+        next_on_scalar()
+        next_on_scalar()
+        next_quantise()
+        tick()
+        all_second(6)
+        all_second(7)
+        for i in range(12, 16):
+            all_exponentials(i)
+        next_regroup()
+        next_regroup()
+        copy_inverse(2)
+        for i in range(12, 16):
+            all_sums(i)
+        next_quantise()
+        next_quantise()
+        normalise(4)
+        store(7)
+        next_on_scalar()
+        next_on_scalar()
+        next_regroup()
+        next_regroup()
+        quantise_weights(4)
+        all_second(8)
+        all_second(9)
+        normalise(5)
+        next_on_scalar()
+        next_on_scalar()
+        next_quantise()
+        quantise_weights(5)
+        next_quantise()
+        all_second(10)
+        invert_sums(3)
+        spread_inverse(3)
+        next_regroup()
+        next_regroup()
+        copy_inverse(3)
+        all_second(11)
+        next_on_scalar()
+        next_on_scalar()
+        normalise(6)
+        next_quantise()
+        next_quantise()
+        next_regroup()
+        next_regroup()
+        quantise_weights(6)
+        store(11)
+        next_on_scalar()
+        next_on_scalar()
+        all_second(12)
+        next_quantise()
+        next_quantise()
+        normalise(7)
+        next_regroup()
+        next_regroup()
+        next_on_scalar()
+        next_on_scalar()
+        quantise_weights(7)
+        all_second(13)
+        spare = psum_score.tile([P, BANK], F32, tag="scores")
+        unread_of[0] = spare
+        for count in range(LAST_PACE):
+            keep_pace(last, 0)
+        next_quantise()
+        next_quantise()
+        all_second(14)
+        next_on_scalar()
+        next_on_scalar()
+        next_quantise()
+        second_matmul(last, 0)
+        next_quantise()
+        second_matmul(last, 1)
         store(last)
+        assert done["quantise"] == ALL_HALVES

@@ -63,6 +63,7 @@ CUBIC = math.sqrt(0.375)
 SHRINK = 1.0 / (24.0 * SMOOTH) ** 2
 CHAIN = 9
 PAIR = 2
+LINE = 4
 
 FLOPS = 2 * 2 * B * Q * S * D
 
@@ -416,12 +417,16 @@ def tile_smcmr_pa_t_kernel(tc, query, context, out):
                 return
             weights = weight_pool.tile([P, PAIR, Q, PACK], BF16, align_bytes=64)
             inverse = inverse_of[PAIR * k // GROUPS]
-            nc.vector.tensor_tensor(
-                out=weights[:],
-                in0=pair_of[k][:].rearrange("p g j q -> p g q j"),
-                in1=inverse[:].unsqueeze(1).unsqueeze(3).to_broadcast([P, PAIR, Q, PACK]),
-                op=ALU.mult,
-            )
+            for g in range(PAIR):
+                nc.vector.tensor_tensor(
+                    out=weights[:, g].rearrange("p (n k) j -> p n j k", k=LINE),
+                    in0=pair_of[k][:, g].rearrange("p j (n k) -> p n j k", k=LINE),
+                    in1=inverse[:]
+                    .rearrange("p (n k) -> p n k", k=LINE)
+                    .unsqueeze(2)
+                    .to_broadcast([P, Q // LINE, PACK, LINE]),
+                    op=ALU.mult,
+                )
             weights_of[k] = weights
 
         def quantise_weights(k):

@@ -50,7 +50,7 @@ WOVEN = 128
 EXTRA = 1
 PACE = 11
 LOOP_EXPS = 4
-RUN = 4
+RUN = 8
 LATE_HALF = 20
 LATE_SCALAR_COLS = 96
 EARLY_SCALAR_COLS = 288

@@ -45,7 +45,7 @@ INV3 = 10
 PACE_FROM = 1
 LAST_PACE = 6
 LATE = 9
-V_LATE = 512
+V_LATE = 384
 WOVEN = 128
 EXTRA = 1
 PACE = 11

@@ -43,6 +43,7 @@ ALL_HALVES = ALL_GROUPS * HALVES
 EVEN_FROM = 10
 INV3 = 10
 PACE_FROM = 1
+LATE_MX = 1
 LAST_PACE = 6
 LATE = 9
 V_LATE = 384
@@ -563,10 +564,9 @@ def tile_smcmr_pa_t_kernel(tc, query, context, out):
             tick()
             add_to_sums(PACK * (n - EXP_LAG - 1))
             add_to_sums(PACK * (n - EXP_LAG - 1) + 1)
-            first_matmul(n - 1, 0)
-            first_matmul(n - 1, 1)
-            if PACE_FROM <= n < PACE:
-                keep_pace(n - 1, 1)
+            if n > LATE_MX:
+                first_matmul(n - 1, 0)
+                first_matmul(n - 1, 1)
             copy_turned_tokens(n, 2)
             exponentials(n - EXP_LAG, 2)
             exponentials(n - EXP_LAG, 3)
@@ -576,6 +576,9 @@ def tile_smcmr_pa_t_kernel(tc, query, context, out):
             tick()
             add_to_sums(PACK * (n - EXP_LAG - 1) + 2)
             add_to_sums(PACK * (n - EXP_LAG - 1) + 3)
+            if n <= LATE_MX:
+                first_matmul(n - 1, 0)
+                first_matmul(n - 1, 1)
             if PACE_FROM <= n < PACE:
                 keep_pace(n - 1, 0)
                 keep_pace(n - 1, 1)

@@ -25,6 +25,8 @@ ALL_GROUPS = B * GROUPS
 D_PASSES = D // K_PASS
 BANK = 512
 D_BANKS = D // BANK
+LAST_PIECES = ((0, 512), (512, 768), (768, 1024))
+WIDE_FROM = 14
 
 FIRST_PARTS = 2
 PREFETCH = 3
@@ -40,7 +42,8 @@ QUERY_PLACE = 3
 HALVES = 2
 HALF = D // HALVES
 ALL_HALVES = ALL_GROUPS * HALVES
-EVEN_FROM = 10
+EARLY = (1,)
+EARLY_COLS = 192
 INV3 = 10
 PACE_FROM = 1
 LATE_MX = 1
@@ -48,7 +51,9 @@ LAST_PACE = 6
 LATE = 9
 V_LATE = 384
 WOVEN = 128
-EXTRA = 1
+FEWER_WOVEN = 128
+FEWER_FROM = 13
+EXTRA_AT = (9,)
 PACE = 11
 LOOP_EXPS = 4
 RUN = 8
@@ -77,7 +82,7 @@ def tile_smcmr_pa_t_kernel(tc, query, context, out):
         token_pool = stack.enter_context(tc.tile_pool(name="tokens", bufs=9))
         stage = stack.enter_context(tc.tile_pool(name="stage", bufs=2))
         halves = stack.enter_context(tc.tile_pool(name="halves", bufs=2))
-        codes = stack.enter_context(tc.tile_pool(name="codes", bufs=11))
+        codes = stack.enter_context(tc.tile_pool(name="codes", bufs=10))
         soft = stack.enter_context(tc.tile_pool(name="soft", bufs=8))
         small = stack.enter_context(tc.tile_pool(name="small", bufs=2))
         weight_pool = stack.enter_context(tc.tile_pool(name="weights", bufs=3))
@@ -160,10 +165,16 @@ def tile_smcmr_pa_t_kernel(tc, query, context, out):
             b, g = divmod(i, GROUPS)
             rows = token_pool.tile([P, PACK, D], BF16)
             source = context[b, g * K_PASS : (g + 1) * K_PASS, :].rearrange("(p j) d -> p j d", j=PACK)
-            parts = FIRST_PARTS if i < 2 else 1
-            for part in range(parts):
-                tiles = slice(part * PACK // parts, (part + 1) * PACK // parts)
-                nc.sync.dma_start(out=rows[:, tiles, :], in_=source[:, tiles, :])
+            if i == 0:
+                parts = [(0, 2, 0, D), (2, PACK, 0, HALF), (2, PACK, HALF, D)]
+            elif i == 1:
+                parts = [(0, 2, 0, D), (2, PACK, 0, D)]
+            else:
+                parts = [(0, PACK, 0, D)]
+            for first_tile, end_tile, first, end in parts:
+                nc.sync.dma_start(
+                    out=rows[:, first_tile:end_tile, first:end], in_=source[:, first_tile:end_tile, first:end]
+                )
             rows_of[i] = rows
 
         def quantise_tokens(i):
@@ -364,26 +375,35 @@ def tile_smcmr_pa_t_kernel(tc, query, context, out):
                 in_=rows_of[i][:, :, first:last].rearrange("p j (n k) -> p n j k", k=RUN),
             )
 
+        def woven_features(i):
+            return WOVEN if i < FEWER_FROM else FEWER_WOVEN
+
         def weave(i):
             if LATE <= i < ALL_GROUPS and i not in woven_of:
-                woven = psum_turn.tile([P, D_BANKS, BANK], BF16, tag="turned")
+                woven_of[i] = []
                 features = BANK // PACK
-                for m in range(WOVEN // features):
-                    first = D - WOVEN + m * features
+                for m in range(woven_features(i) // features):
+                    first = D - woven_features(i) + m * features
+                    if m % D_BANKS == 0:
+                        woven = psum_turn.tile([P, D_BANKS, BANK], BF16, tag="turned")
+                        woven_of[i].append(woven)
                     nc.tensor.matmul(
-                        out=woven[:, m, :],
+                        out=woven[:, m % D_BANKS, :].rearrange("p (n k j) -> p n j k", k=RUN, j=PACK),
                         lhsT=identity_bf16[:],
-                        rhs=rows_of[i][:, :, first : first + features].rearrange("p j d -> p d j"),
+                        rhs=rows_of[i][:, :, first : first + features].rearrange("p j (n k) -> p n j k", k=RUN),
                         start=True,
                         stop=True,
                     )
-                woven_of[i] = woven
 
         def copy_woven(i):
-            nc.scalar.copy(
-                out=regrouped_of[i][:, D - WOVEN :, :].rearrange("p d j -> p (d j)"),
-                in_=woven_of[i][:, 0 : WOVEN // (BANK // PACK), :].rearrange("p m c -> p (m c)"),
-            )
+            features = BANK // PACK
+            for k, woven in enumerate(woven_of[i]):
+                first = D - woven_features(i) + k * D_BANKS * features
+                count = min(D_BANKS, (D - first) // features)
+                nc.scalar.copy(
+                    out=regrouped_of[i][:, first : first + count * features, :].rearrange("p d j -> p (d j)"),
+                    in_=woven[:, 0:count, :].rearrange("p m c -> p (m c)"),
+                )
 
         def quantise_context(i, first, last):
             if first == 0:
@@ -413,12 +433,14 @@ def tile_smcmr_pa_t_kernel(tc, query, context, out):
                 nc.vector.tensor_copy(out=inverse[:], in_=sums_of[b][:, 1, :])
                 inverse_of[b] = inverse
 
-        def normalise(k):
+        def normalise(k, between=None):
             if not 0 <= k < ALL_GROUPS // PAIR:
                 return
-            weights = weight_pool.tile([P, PAIR, Q, PACK], BF16, align_bytes=64)
+            weights = weight_pool.tile([P, PAIR, Q, PACK], BF16, align_bytes=64, bufs=2)
             inverse = inverse_of[PAIR * k // GROUPS]
             for g in range(PAIR):
+                if g > 0 and between is not None:
+                    between()
                 nc.vector.tensor_tensor(
                     out=weights[:, g].rearrange("p (n k) j -> p n j k", k=LINE),
                     in0=pair_of[k][:, g].rearrange("p j (n k) -> p n j k", k=LINE),
@@ -433,8 +455,8 @@ def tile_smcmr_pa_t_kernel(tc, query, context, out):
         def quantise_weights(k):
             if not 0 <= k < ALL_GROUPS // PAIR:
                 return
-            w_codes = weight_pool.tile([P, PAIR, Q], U32, align_bytes=64)
-            w_scales = weight_pool.tile([P, PAIR, Q], U8, align_bytes=64)
+            w_codes = weight_pool.tile([P, PAIR, Q], U32, align_bytes=64, bufs=6)
+            w_scales = weight_pool.tile([P, PAIR, Q], U8, align_bytes=64, bufs=6)
             nc.vector.quantize_mx(
                 out=w_codes[:].rearrange("p g q -> p (g q)").bitcast(FP8X4),
                 scales=w_scales[:].rearrange("p g q -> p (g q)"),
@@ -442,36 +464,45 @@ def tile_smcmr_pa_t_kernel(tc, query, context, out):
             )
             weight_codes_of[k] = (w_codes, w_scales)
 
+        def pieces(b):
+            return LAST_PIECES if b == B - 1 else tuple((h * BANK, (h + 1) * BANK) for h in range(D_BANKS))
+
         def second_matmul(i, h):
             if not is_group(i):
                 return
             b, g = divmod(i, GROUPS)
             w_codes, w_scales = weight_codes_of[i // PAIR]
             c_codes, c_scales = context_codes_of[i]
+            first, end = pieces(b)[h]
             if g == 0:
-                acc = psum_out.tile([P, BANK], F32, tag="acc")
+                if h < D_BANKS:
+                    acc = psum_out.tile([P, BANK], F32, tag="acc")
+                else:
+                    acc = psum_score.tile([P, BANK], F32, tag="scores")
                 acc_of[(b, h)] = acc
             nc.tensor.matmul_mx(
-                out=acc_of[(b, h)][:],
+                out=acc_of[(b, h)][:, 0 : end - first],
                 lhsT=w_codes[:, i % PAIR, :].bitcast(FP8X4),
                 lhsT_scale=w_scales[:, i % PAIR, :],
-                rhs=c_codes[:, h * BANK : (h + 1) * BANK].bitcast(FP8X4),
-                rhs_scale=c_scales[:, h * BANK : (h + 1) * BANK],
+                rhs=c_codes[:, first:end].bitcast(FP8X4),
+                rhs_scale=c_scales[:, first:end],
                 start=(g == 0),
                 stop=(g == GROUPS - 1),
             )
+
+        def store_piece(b, h):
+            first, end = pieces(b)[h]
+            result = results.tile([P, BANK], F32)
+            copy = nc.vector.tensor_copy if b == B - 1 and h == 1 else nc.scalar.copy
+            copy(out=result[:, 0 : end - first], in_=acc_of[(b, h)][:, 0 : end - first])
+            nc.sync.dma_start(out=out[b, :, first:end], in_=result[:, 0 : end - first])
 
         def store(i):
             if not is_group(i) or i % GROUPS != GROUPS - 1:
                 return
             b = i // GROUPS
-            for h in range(D_BANKS):
-                result = results.tile([P, BANK], F32)
-                if h % 2 == 0 or b < B - 1:
-                    nc.scalar.copy(out=result[:], in_=acc_of[(b, h)][:])
-                else:
-                    nc.vector.tensor_copy(out=result[:], in_=acc_of[(b, h)][:])
-                nc.sync.dma_start(out=out[b, :, h * BANK : (h + 1) * BANK], in_=result[:])
+            for h in range(len(pieces(b))):
+                store_piece(b, h)
 
         def load_query(b):
             q_rows = query_pool.tile([P, D], BF16)
@@ -496,31 +527,25 @@ def tile_smcmr_pa_t_kernel(tc, query, context, out):
 
         def next_regroup():
             i, h = divmod(done["regroup"], HALVES)
-            if i < ALL_GROUPS and i < done["quantise"] // HALVES + 2:
-                size = HALF if i < LATE else V_LATE // HALVES
+            if i < LATE and i < done["quantise"] // HALVES + 2:
+                size = (D - EARLY_COLS if i in EARLY else D) // HALVES
                 regroup(i, nc.vector.tensor_copy, h * size, (h + 1) * size)
                 done["regroup"] += 1
 
         def next_quantise():
-            i, h = divmod(done["quantise"], HALVES)
-            if i >= ALL_GROUPS or done["regroup"] < HALVES * (i + 1):
-                return
-            if i < LATE:
+            i = done["quantise"] // HALVES
+            if i < LATE and done["regroup"] >= HALVES * (i + 1):
                 quantise_context(i, 0, D)
                 done["quantise"] += HALVES
-            elif h == 0 or done["scalar"] >= HALVES * (i + 1):
-                quantise_context(i, h * HALF, (h + 1) * HALF)
-                done["quantise"] += 1
 
-        def next_on_scalar():
-            i, h = divmod(max(HALVES * LATE, done["scalar"]), HALVES)
-            if i < ALL_GROUPS and i < done["quantise"] // HALVES + 2:
-                if h == 0:
-                    regroup(i, nc.scalar.copy, V_LATE, D - WOVEN)
-                else:
-                    copy_woven(i)
-                    weave(i + 2)
-                done["scalar"] = HALVES * i + h + 1
+        def vector_features(i):
+            return HALF if i >= WIDE_FROM else V_LATE
+
+        def regroup_on_vector(i):
+            regroup(i, nc.vector.tensor_copy, 0, vector_features(i))
+
+        def regroup_on_scalar(i):
+            regroup(i, nc.scalar.copy, vector_features(i), D - woven_features(i))
 
         chain = []
 
@@ -540,11 +565,17 @@ def tile_smcmr_pa_t_kernel(tc, query, context, out):
                 load_query(n // GROUPS + 1)
             late = n - 1 - SQUARE_LAG
 
+            if n - 1 in EARLY:
+                regroup(n - 1, nc.scalar.copy, D - EARLY_COLS, D)
             copy_turned_tokens(n, 0)
             guess_root(late)
             if n == 1 or (n > 0 and n % GROUPS == 0):
                 quantise_query(n // GROUPS)
+                tick()
             quantise_tokens(n - 1)
+            if n == 1:
+                first_matmul(0, 0)
+                first_matmul(0, 1)
             copy_turned_tokens(n, 1)
             square_guess(late)
             if n == WEIGHT_LAG:
@@ -564,32 +595,29 @@ def tile_smcmr_pa_t_kernel(tc, query, context, out):
             tick()
             add_to_sums(PACK * (n - EXP_LAG - 1))
             add_to_sums(PACK * (n - EXP_LAG - 1) + 1)
-            if n > LATE_MX:
+            if n > 1:
                 first_matmul(n - 1, 0)
                 first_matmul(n - 1, 1)
             copy_turned_tokens(n, 2)
             exponentials(n - EXP_LAG, 2)
             exponentials(n - EXP_LAG, 3)
             copy_turned_tokens(n, 3)
+            if n == 14:
+                regroup_on_vector(LATE)
             if n > 0:
                 next_quantise()
             tick()
             add_to_sums(PACK * (n - EXP_LAG - 1) + 2)
             add_to_sums(PACK * (n - EXP_LAG - 1) + 3)
-            if n <= LATE_MX:
-                first_matmul(n - 1, 0)
-                first_matmul(n - 1, 1)
             if PACE_FROM <= n < PACE:
                 keep_pace(n - 1, 0)
                 keep_pace(n - 1, 1)
             for j in range(PACK):
                 sum_squares(n - SQUARE_LAG, j)
-            if EXP_LAG <= n < EXP_LAG + EXTRA:
+            if n in EXTRA_AT:
                 next_regroup()
             if n >= WEIGHT_LAG and n % PAIR == 0:
                 normalise((n - WEIGHT_LAG) // PAIR)
-            if n % GROUPS == 0:
-                tick()
             shift_squares(n - SQUARE_LAG)
 
         n = ALL_GROUPS
@@ -608,21 +636,22 @@ def tile_smcmr_pa_t_kernel(tc, query, context, out):
                 sum_squares(i, j)
 
         def all_second(i):
-            for h in range(D_BANKS):
+            for h in range(len(pieces(i // GROUPS))):
                 second_matmul(i, h)
 
+        def hold_clock(passes):
+            for count in range(passes):
+                keep_pace(last, count % 2)
+
+        weave(LATE)
         quantise_tokens(last)
         tick()
         damp(14)
         quantise_weights(0)
         tick()
-        weave(LATE)
-        weave(LATE + 1)
         all_sums(6)
         first_matmul(last, 0)
         first_matmul(last, 1)
-        all_second(0)
-        all_second(1)
         all_squares(13)
         leaky_relu(14)
         tick()
@@ -630,126 +659,120 @@ def tile_smcmr_pa_t_kernel(tc, query, context, out):
         all_sums(7)
         normalise(1)
         tick()
+        next_quantise()
+        regroup_on_scalar(9)
         damp(last)
+        invert_sums(1)
+        spread_inverse(1)
         all_squares(14)
         quantise_weights(1)
-        tick()
-        all_second(2)
-        all_second(3)
+        all_second(0)
+        all_second(1)
+        copy_inverse(1)
         leaky_relu(last)
         while chain:
             tick()
+        next_quantise()
+        copy_woven(9)
+        weave(10)
         all_squares(last)
         shift_squares(last)
+        normalise(2)
         exponentials(8, 0)
         exponentials(8, 1)
         guess_root(last)
         exponentials(8, 2)
         exponentials(8, 3)
         square_guess(last)
-        invert_sums(1)
-        spread_inverse(1)
-        next_regroup()
-        next_regroup()
-        copy_inverse(1)
-        all_exponentials(9)
-        all_exponentials(10)
-        all_exponentials(11)
+        for i in range(9, 12):
+            all_exponentials(i)
         for i in range(8, 12):
             all_sums(i)
-        normalise(2)
         chain.append((last, 0))
-        tick()
-        next_regroup()
-        tick()
         quantise_weights(2)
-        next_on_scalar()
-        next_on_scalar()
         tick()
-        next_regroup()
+        normalise(3, tick)
         tick()
-        normalise(3)
-        tick()
-        store(3)
-        all_second(4)
+        quantise_context(9, 0, D)
+        regroup_on_scalar(10)
+        regroup_on_vector(10)
         tick()
         quantise_weights(3)
         tick()
         invert_sums(2)
         spread_inverse(2)
+        copy_woven(10)
+        all_second(2)
+        all_second(3)
+        weave(11)
+        regroup_on_vector(11)
+        tick()
+        copy_inverse(2)
+        quantise_context(10, 0, D)
+        tick()
+        store(3)
+        all_second(4)
         all_second(5)
-        next_quantise()
-        tick()
-        next_on_scalar()
-        next_on_scalar()
-        next_quantise()
-        tick()
+        normalise(4, tick)
+        while chain:
+            tick()
+        regroup_on_scalar(11)
+        copy_woven(11)
+        weave(12)
+        quantise_weights(4)
+        normalise(5)
+        quantise_context(11, 0, D)
         all_second(6)
         all_second(7)
         for i in range(12, 16):
             all_exponentials(i)
-        next_regroup()
-        next_regroup()
-        copy_inverse(2)
         for i in range(12, 16):
             all_sums(i)
-        next_quantise()
-        next_quantise()
-        normalise(4)
-        store(7)
-        next_on_scalar()
-        next_on_scalar()
-        next_regroup()
-        next_regroup()
-        quantise_weights(4)
-        all_second(8)
-        all_second(9)
-        normalise(5)
-        next_on_scalar()
-        next_on_scalar()
-        next_quantise()
         quantise_weights(5)
-        next_quantise()
-        all_second(10)
+        regroup_on_vector(12)
+        store(7)
+        regroup_on_vector(13)
         invert_sums(3)
         spread_inverse(3)
-        next_regroup()
-        next_regroup()
+        all_second(8)
+        all_second(9)
+        regroup_on_scalar(12)
+        copy_woven(12)
+        weave(13)
         copy_inverse(3)
-        all_second(11)
-        next_on_scalar()
-        next_on_scalar()
         normalise(6)
-        next_quantise()
-        next_quantise()
-        next_regroup()
-        next_regroup()
-        quantise_weights(6)
-        store(11)
-        next_on_scalar()
-        next_on_scalar()
-        all_second(12)
-        next_quantise()
-        next_quantise()
         normalise(7)
-        next_regroup()
-        next_regroup()
-        next_on_scalar()
-        next_on_scalar()
+        all_second(10)
+        quantise_weights(6)
+        quantise_context(12, 0, D)
+        all_second(11)
+        regroup_on_scalar(13)
+        copy_woven(13)
+        weave(14)
         quantise_weights(7)
+        regroup_on_vector(14)
+        store(11)
+        all_second(12)
+        quantise_context(13, 0, D)
+        regroup_on_scalar(14)
+        copy_woven(14)
+        weave(15)
+        regroup_on_vector(15)
         all_second(13)
-        spare = psum_score.tile([P, BANK], F32, tag="scores")
-        unread_of[0] = spare
-        for count in range(LAST_PACE):
-            keep_pace(last, 0)
-        next_quantise()
-        next_quantise()
-        all_second(14)
-        next_on_scalar()
-        next_on_scalar()
-        next_quantise()
-        second_matmul(last, 0)
-        next_quantise()
-        second_matmul(last, 1)
-        store(last)
-        assert done["quantise"] == ALL_HALVES
+        quantise_context(14, 0, HALF)
+        quantise_context(15, 0, HALF)
+        second_matmul(14, 0)
+        second_matmul(15, 0)
+        regroup_on_scalar(15)
+        quantise_context(14, HALF, D)
+        second_matmul(14, 1)
+        second_matmul(14, 2)
+        copy_woven(15)
+        store_piece(B - 1, 0)
+        quantise_context(15, 512, 768)
+        second_matmul(15, 1)
+        quantise_context(15, 768, 1024)
+        second_matmul(15, 2)
+        store_piece(B - 1, 1)
+        store_piece(B - 1, 2)
+        assert done["quantise"] == HALVES * LATE

@@ -49,12 +49,12 @@ PACE_FROM = 1
 LATE_MX = 1
 LAST_PACE = 6
 LATE = 9
-V_LATE = 384
+V_LATE = 448
 WOVEN = 128
 FEWER_WOVEN = 128
 FEWER_FROM = 13
 EXTRA_AT = (9,)
-PACE = 11
+PACE = 16
 LOOP_EXPS = 4
 RUN = 8
 LATE_HALF = 20
@@ -99,15 +99,13 @@ def tile_smcmr_pa_t_kernel(tc, query, context, out):
         make_identity(nc, identity[:])
         identity_bf16 = const.tile([P, P], BF16)
         nc.vector.tensor_copy(out=identity_bf16[:], in_=identity[:])
-        ones = const.tile([P, SUM_COPIES], F32)
-        nc.vector.memset(ones[:], 1.0)
         q_codes = const.tile([P, B, D_PASSES, Q], U32, align_bytes=64)
         q_scales = const.tile([P, B, D_PASSES, Q], U8, align_bytes=64)
 
         rows_of, turned_of, grouped_of, token_codes_of, scores_of = {}, {}, {}, {}, {}
         damped_of, leaky_of, squares_of, steep_of = {}, {}, {}, {}
         norm_of, shifted_of, guess_of = {}, {}, {}
-        pair_of, column_of, woven_of = {}, {}, {}
+        pair_of, column_of, woven_of, total_of = {}, {}, {}, {}
         regrouped_of, weights_of, weight_codes_of = {}, {}, {}
         query_rows_of, query_grouped_of = {}, {}
         expo_of, sums_of, inverse_of, context_codes_of, acc_of = {}, {}, {}, {}, {}
@@ -226,9 +224,9 @@ def tile_smcmr_pa_t_kernel(tc, query, context, out):
             if not is_group(i):
                 return
             if i % PAIR == 0:
-                pair = soft.tile([P, PAIR, PACK, Q], F32)
+                pair = soft.tile([P, PACK, PAIR, Q], F32)
                 pair_of[i // PAIR] = pair
-            leaky_of[i] = pair_of[i // PAIR][:, i % PAIR]
+            leaky_of[i] = pair_of[i // PAIR][:, :, i % PAIR, :]
             nc.scalar.mul(out=leaky_of[i], in_=scores_of[i][:], mul=SLOPE)
 
         def leaky_relu(i):
@@ -356,14 +354,15 @@ def tile_smcmr_pa_t_kernel(tc, query, context, out):
                 return
             b, g = divmod(i, GROUPS)
             if g == 0 and j == 0:
-                sums = psum_sum.tile([P, 2, P], F32)
+                sums = psum_sum.tile([P, P], F32)
                 sums_of[b] = sums
             nc.tensor.matmul(
-                out=sums_of[b][:, 0, 0:SUM_COPIES],
+                out=sums_of[b][:],
                 lhsT=leaky_of[i][:, j, :],
-                rhs=ones[:],
+                rhs=identity[:],
                 start=(g == 0 and j == 0),
                 stop=(g == GROUPS - 1 and j == PACK - 1),
+                is_transpose=True,
             )
 
         def regroup(i, engine_copy, first, last):
@@ -417,52 +416,49 @@ def tile_smcmr_pa_t_kernel(tc, query, context, out):
                 in_=regrouped_of[i][:, first:last, :].rearrange("p d j -> p (d j)"),
             )
 
+        def total_sums(b):
+            if 0 <= b < B:
+                total = small.tile([P, 1], F32)
+                nc.vector.reduce_sum(out=total[:], in_=sums_of[b][:], axis=mybir.AxisListType.X)
+                total_of[b] = total
+
         def invert_sums(b):
             if 0 <= b < B:
+                total_sums(b)
                 column = small.tile([P, 1], F32)
-                nc.vector.reciprocal(out=column[:], in_=sums_of[b][:, 0, 0:1])
+                nc.vector.reciprocal(out=column[:], in_=total_of[b][:])
                 column_of[b] = column
 
         def spread_inverse(b):
-            if 0 <= b < B:
-                nc.tensor.transpose(sums_of[b][:, 1, :], column_of[b][:].to_broadcast([P, P]), identity[:])
-
-        def copy_inverse(b):
-            if 0 <= b < B:
-                inverse = stage.tile([P, Q], F32)
-                nc.vector.tensor_copy(out=inverse[:], in_=sums_of[b][:, 1, :])
-                inverse_of[b] = inverse
-
-        def normalise(k, between=None):
-            if not 0 <= k < ALL_GROUPS // PAIR:
-                return
-            weights = weight_pool.tile([P, PAIR, Q, PACK], BF16, align_bytes=64, bufs=2)
-            inverse = inverse_of[PAIR * k // GROUPS]
+            inverse = psum_turn.tile([P, PAIR, Q], F32, tag="turned")
             for g in range(PAIR):
-                if g > 0 and between is not None:
-                    between()
-                nc.vector.tensor_tensor(
-                    out=weights[:, g].rearrange("p (n k) j -> p n j k", k=LINE),
-                    in0=pair_of[k][:, g].rearrange("p j (n k) -> p n j k", k=LINE),
-                    in1=inverse[:]
-                    .rearrange("p (n k) -> p n k", k=LINE)
-                    .unsqueeze(2)
-                    .to_broadcast([P, Q // LINE, PACK, LINE]),
-                    op=ALU.mult,
-                )
-            weights_of[k] = weights
+                nc.tensor.transpose(inverse[:, g, :], column_of[b][:].to_broadcast([P, P]), identity[:])
+            inverse_of[b] = inverse
 
-        def quantise_weights(k):
-            if not 0 <= k < ALL_GROUPS // PAIR:
-                return
-            w_codes = weight_pool.tile([P, PAIR, Q], U32, align_bytes=64, bufs=6)
-            w_scales = weight_pool.tile([P, PAIR, Q], U8, align_bytes=64, bufs=6)
+        def normalise(k):
+            b, half = divmod(k, GROUPS // PAIR)
+            if half == 0:
+                weights = weight_pool.tile([P, GROUPS // PAIR, PAIR, Q, PACK], BF16, align_bytes=64, bufs=2)
+                weights_of[b] = weights
+            nc.vector.tensor_tensor(
+                out=weights_of[b][:, half].rearrange("p g (n k) j -> p (g n) j k", k=LINE),
+                in0=pair_of[k][:].rearrange("p j g (n k) -> p (g n) j k", k=LINE),
+                in1=inverse_of[b][:]
+                .rearrange("p g (n k) -> p (g n) k", k=LINE)
+                .unsqueeze(2)
+                .to_broadcast([P, PAIR * Q // LINE, PACK, LINE]),
+                op=ALU.mult,
+            )
+
+        def quantise_weights(b):
+            w_codes = weight_pool.tile([P, GROUPS, Q], U32, align_bytes=64, bufs=3)
+            w_scales = weight_pool.tile([P, GROUPS, Q], U8, align_bytes=64, bufs=3)
             nc.vector.quantize_mx(
                 out=w_codes[:].rearrange("p g q -> p (g q)").bitcast(FP8X4),
                 scales=w_scales[:].rearrange("p g q -> p (g q)"),
-                in_=weights_of[k][:].rearrange("p g q j -> p (g q j)"),
+                in_=weights_of[b][:].rearrange("p h g q j -> p (h g q j)"),
             )
-            weight_codes_of[k] = (w_codes, w_scales)
+            weight_codes_of[b] = (w_codes, w_scales)
 
         def pieces(b):
             return LAST_PIECES if b == B - 1 else tuple((h * BANK, (h + 1) * BANK) for h in range(D_BANKS))
@@ -471,7 +467,7 @@ def tile_smcmr_pa_t_kernel(tc, query, context, out):
             if not is_group(i):
                 return
             b, g = divmod(i, GROUPS)
-            w_codes, w_scales = weight_codes_of[i // PAIR]
+            w_codes, w_scales = weight_codes_of[b]
             c_codes, c_scales = context_codes_of[i]
             first, end = pieces(b)[h]
             if g == 0:
@@ -482,8 +478,8 @@ def tile_smcmr_pa_t_kernel(tc, query, context, out):
                 acc_of[(b, h)] = acc
             nc.tensor.matmul_mx(
                 out=acc_of[(b, h)][:, 0 : end - first],
-                lhsT=w_codes[:, i % PAIR, :].bitcast(FP8X4),
-                lhsT_scale=w_scales[:, i % PAIR, :],
+                lhsT=w_codes[:, g, :].bitcast(FP8X4),
+                lhsT_scale=w_scales[:, g, :],
                 rhs=c_codes[:, first:end].bitcast(FP8X4),
                 rhs_scale=c_scales[:, first:end],
                 start=(g == 0),
@@ -580,13 +576,10 @@ def tile_smcmr_pa_t_kernel(tc, query, context, out):
             square_guess(late)
             if n == WEIGHT_LAG:
                 invert_sums(0)
-                spread_inverse(0)
             tick()
             next_regroup()
             if is_group(late) and late % GROUPS == GROUPS - 1:
                 chain.append((late, 0))
-            if n == WEIGHT_LAG:
-                copy_inverse(0)
             tick()
             damp(n - LEAKY_LAG)
             exponentials(n - EXP_LAG, 0)
@@ -616,8 +609,6 @@ def tile_smcmr_pa_t_kernel(tc, query, context, out):
                 sum_squares(n - SQUARE_LAG, j)
             if n in EXTRA_AT:
                 next_regroup()
-            if n >= WEIGHT_LAG and n % PAIR == 0:
-                normalise((n - WEIGHT_LAG) // PAIR)
             shift_squares(n - SQUARE_LAG)
 
         n = ALL_GROUPS
@@ -644,11 +635,10 @@ def tile_smcmr_pa_t_kernel(tc, query, context, out):
                 keep_pace(last, count % 2)
 
         weave(LATE)
+        spread_inverse(0)
         quantise_tokens(last)
         tick()
         damp(14)
-        quantise_weights(0)
-        tick()
         all_sums(6)
         first_matmul(last, 0)
         first_matmul(last, 1)
@@ -657,21 +647,20 @@ def tile_smcmr_pa_t_kernel(tc, query, context, out):
         tick()
         all_exponentials(7)
         all_sums(7)
-        normalise(1)
+        normalise(0)
         tick()
         next_quantise()
         regroup_on_scalar(9)
         damp(last)
+        tick()
+        normalise(1)
         invert_sums(1)
         spread_inverse(1)
         all_squares(14)
-        quantise_weights(1)
-        all_second(0)
-        all_second(1)
-        copy_inverse(1)
         leaky_relu(last)
         while chain:
             tick()
+        quantise_weights(0)
         next_quantise()
         copy_woven(9)
         weave(10)
@@ -689,37 +678,35 @@ def tile_smcmr_pa_t_kernel(tc, query, context, out):
         for i in range(8, 12):
             all_sums(i)
         chain.append((last, 0))
-        quantise_weights(2)
         tick()
-        normalise(3, tick)
+        normalise(3)
         tick()
+        for i in range(GROUPS):
+            all_second(i)
         quantise_context(9, 0, D)
+        tick()
         regroup_on_scalar(10)
         regroup_on_vector(10)
         tick()
-        quantise_weights(3)
+        quantise_weights(1)
         tick()
         invert_sums(2)
         spread_inverse(2)
         copy_woven(10)
-        all_second(2)
-        all_second(3)
         weave(11)
         regroup_on_vector(11)
         tick()
-        copy_inverse(2)
         quantise_context(10, 0, D)
         tick()
         store(3)
         all_second(4)
         all_second(5)
-        normalise(4, tick)
+        normalise(4)
         while chain:
             tick()
         regroup_on_scalar(11)
         copy_woven(11)
         weave(12)
-        quantise_weights(4)
         normalise(5)
         quantise_context(11, 0, D)
         all_second(6)
@@ -728,7 +715,7 @@ def tile_smcmr_pa_t_kernel(tc, query, context, out):
             all_exponentials(i)
         for i in range(12, 16):
             all_sums(i)
-        quantise_weights(5)
+        quantise_weights(2)
         regroup_on_vector(12)
         store(7)
         regroup_on_vector(13)
@@ -739,17 +726,15 @@ def tile_smcmr_pa_t_kernel(tc, query, context, out):
         regroup_on_scalar(12)
         copy_woven(12)
         weave(13)
-        copy_inverse(3)
         normalise(6)
         normalise(7)
         all_second(10)
-        quantise_weights(6)
         quantise_context(12, 0, D)
+        quantise_weights(3)
         all_second(11)
         regroup_on_scalar(13)
         copy_woven(13)
         weave(14)
-        quantise_weights(7)
         regroup_on_vector(14)
         store(11)
         all_second(12)

@@ -49,9 +49,9 @@ PACE_FROM = 1
 LATE_MX = 1
 LAST_PACE = 6
 LATE = 9
-V_LATE = 448
-WOVEN = 128
-FEWER_WOVEN = 128
+V_LATE = 320
+WOVEN = 256
+FEWER_WOVEN = 256
 FEWER_FROM = 13
 EXTRA_AT = (9,)
 PACE = 16
@@ -430,7 +430,10 @@ def tile_smcmr_pa_t_kernel(tc, query, context, out):
                 column_of[b] = column
 
         def spread_inverse(b):
-            inverse = psum_turn.tile([P, PAIR, Q], F32, tag="turned")
+            if b == 0:
+                inverse = psum_turn.tile([P, PAIR, Q], F32, tag="turned")
+            else:
+                inverse = psum_score.tile([P, PAIR, Q], F32, tag="scores")
             for g in range(PAIR):
                 nc.tensor.transpose(inverse[:, g, :], column_of[b][:].to_broadcast([P, P]), identity[:])
             inverse_of[b] = inverse
@@ -698,15 +701,15 @@ def tile_smcmr_pa_t_kernel(tc, query, context, out):
         tick()
         quantise_context(10, 0, D)
         tick()
-        store(3)
-        all_second(4)
-        all_second(5)
         normalise(4)
         while chain:
             tick()
         regroup_on_scalar(11)
         copy_woven(11)
         weave(12)
+        store(3)
+        all_second(4)
+        all_second(5)
         normalise(5)
         quantise_context(11, 0, D)
         all_second(6)

@@ -42,14 +42,14 @@ QUERY_PLACE = 3
 HALVES = 2
 HALF = D // HALVES
 ALL_HALVES = ALL_GROUPS * HALVES
-EARLY = (1,)
+EARLY = {1: 2, 5: 9}
 EARLY_COLS = 192
 INV3 = 10
 PACE_FROM = 1
 LATE_MX = 1
 LAST_PACE = 6
 LATE = 9
-V_LATE = 320
+V_LATE = 256
 WOVEN = 256
 FEWER_WOVEN = 256
 FEWER_FROM = 13
@@ -564,8 +564,9 @@ def tile_smcmr_pa_t_kernel(tc, query, context, out):
                 load_query(n // GROUPS + 1)
             late = n - 1 - SQUARE_LAG
 
-            if n - 1 in EARLY:
-                regroup(n - 1, nc.scalar.copy, D - EARLY_COLS, D)
+            for i in EARLY:
+                if n == EARLY[i]:
+                    regroup(i, nc.scalar.copy, D - EARLY_COLS, D)
             copy_turned_tokens(n, 0)
             guess_root(late)
             if n == 1 or (n > 0 and n % GROUPS == 0):
@@ -634,6 +635,8 @@ def tile_smcmr_pa_t_kernel(tc, query, context, out):
                 second_matmul(i, h)
 
         def hold_clock(passes):
+            spare = psum_turn.tile([P, BANK], F32, tag="turned")
+            unread_of[0] = spare
             for count in range(passes):
                 keep_pace(last, count % 2)
 
@@ -659,6 +662,7 @@ def tile_smcmr_pa_t_kernel(tc, query, context, out):
         normalise(1)
         invert_sums(1)
         spread_inverse(1)
+        hold_clock(3)
         all_squares(14)
         leaky_relu(last)
         while chain:

@@ -49,7 +49,8 @@ PACE_FROM = 1
 LATE_MX = 1
 LAST_PACE = 6
 LATE = 9
-V_LATE = 256
+V_LATE = 128
+GPSIMD_FEATURES = {9: 192, 10: 384, 11: 192, 12: 384, 13: 384}
 WOVEN = 256
 FEWER_WOVEN = 256
 FEWER_FROM = 13
@@ -377,6 +378,25 @@ def tile_smcmr_pa_t_kernel(tc, query, context, out):
         def woven_features(i):
             return WOVEN if i < FEWER_FROM else FEWER_WOVEN
 
+        def gpsimd_after(ap):
+            seen = small.tile([P, 1], ap.dtype, tag="seen_f32" if ap.dtype == F32 else "seen_u32")
+            nc.gpsimd.tensor_copy(out=seen[:], in_=ap)
+
+        def regroup_on_gpsimd(i, first, last):
+            if i not in regrouped_of:
+                regrouped = halves.tile([P, D, PACK], BF16, align_bytes=64)
+                regrouped_of[i] = regrouped
+            first += vector_features(i)
+            last += vector_features(i)
+            nc.gpsimd.tensor_scalar(
+                out=regrouped_of[i][:, first:last, :],
+                in0=rows_of[i][:, :, first:last].rearrange("p j d -> p d j"),
+                scalar1=1.0,
+                scalar2=0.0,
+                op0=ALU.mult,
+                op1=ALU.add,
+            )
+
         def weave(i):
             if LATE <= i < ALL_GROUPS and i not in woven_of:
                 woven_of[i] = []
@@ -537,6 +557,9 @@ def tile_smcmr_pa_t_kernel(tc, query, context, out):
                 quantise_context(i, 0, D)
                 done["quantise"] += HALVES
 
+        def gpsimd_features(i):
+            return GPSIMD_FEATURES.get(i, 0)
+
         def vector_features(i):
             return HALF if i >= WIDE_FROM else V_LATE
 
@@ -544,7 +567,7 @@ def tile_smcmr_pa_t_kernel(tc, query, context, out):
             regroup(i, nc.vector.tensor_copy, 0, vector_features(i))
 
         def regroup_on_scalar(i):
-            regroup(i, nc.scalar.copy, vector_features(i), D - woven_features(i))
+            regroup(i, nc.scalar.copy, vector_features(i) + gpsimd_features(i), D - woven_features(i))
 
         chain = []
 
@@ -650,25 +673,30 @@ def tile_smcmr_pa_t_kernel(tc, query, context, out):
         first_matmul(last, 1)
         all_squares(13)
         leaky_relu(14)
+        gpsimd_after(leaky_of[14][:, 0, 0:1])
+        regroup_on_gpsimd(9, 0, 192)
+        regroup_on_gpsimd(10, 0, 192)
         tick()
         all_exponentials(7)
         all_sums(7)
         normalise(0)
-        tick()
         next_quantise()
         regroup_on_scalar(9)
         damp(last)
-        tick()
         normalise(1)
+        tick()
         invert_sums(1)
         spread_inverse(1)
         hold_clock(3)
         all_squares(14)
+        tick()
         leaky_relu(last)
+        tick()
+        quantise_weights(0)
         while chain:
             tick()
-        quantise_weights(0)
-        next_quantise()
+        gpsimd_after(weight_codes_of[0][0][:, 0, 0:1])
+        regroup_on_gpsimd(10, 192, 384)
         copy_woven(9)
         weave(10)
         all_squares(last)
@@ -686,12 +714,13 @@ def tile_smcmr_pa_t_kernel(tc, query, context, out):
             all_sums(i)
         chain.append((last, 0))
         tick()
+        quantise_context(9, 0, D)
+        regroup_on_gpsimd(11, 0, 192)
+        tick()
         normalise(3)
         tick()
         for i in range(GROUPS):
             all_second(i)
-        quantise_context(9, 0, D)
-        tick()
         regroup_on_scalar(10)
         regroup_on_vector(10)
         tick()
@@ -699,13 +728,17 @@ def tile_smcmr_pa_t_kernel(tc, query, context, out):
         tick()
         invert_sums(2)
         spread_inverse(2)
+        tick()
         copy_woven(10)
         weave(11)
         regroup_on_vector(11)
         tick()
         quantise_context(10, 0, D)
+        regroup_on_gpsimd(12, 0, 192)
+        regroup_on_gpsimd(12, 192, 384)
         tick()
         normalise(4)
+        normalise(5)
         while chain:
             tick()
         regroup_on_scalar(11)
@@ -714,7 +747,6 @@ def tile_smcmr_pa_t_kernel(tc, query, context, out):
         store(3)
         all_second(4)
         all_second(5)
-        normalise(5)
         quantise_context(11, 0, D)
         all_second(6)
         all_second(7)
@@ -727,6 +759,9 @@ def tile_smcmr_pa_t_kernel(tc, query, context, out):
         store(7)
         regroup_on_vector(13)
         invert_sums(3)
+        gpsimd_after(column_of[3][:])
+        regroup_on_gpsimd(13, 0, 192)
+        regroup_on_gpsimd(13, 192, 384)
         spread_inverse(3)
         all_second(8)
         all_second(9)

@@ -42,7 +42,7 @@ QUERY_PLACE = 3
 HALVES = 2
 HALF = D // HALVES
 ALL_HALVES = ALL_GROUPS * HALVES
-EARLY = {1: 2, 5: 9}
+EARLY = {}
 EARLY_COLS = 192
 INV3 = 10
 PACE_FROM = 1

import math
from contextlib import ExitStack

import concourse.mybir as mybir
from concourse.masks import make_identity

F32 = mybir.dt.float32
BF16 = mybir.dt.bfloat16
U32 = mybir.dt.uint32
U8 = mybir.dt.uint8
FP8X4 = mybir.dt.float8_e4m3fn_x4
ALU = mybir.AluOpType
ACT = mybir.ActivationFunctionType

B, Q, S, D = 4, 128, 2048, 1024
EPS = 1e-8
SLOPE = 0.1
SMOOTH = 9.0

P = 128
PACK = 4
K_PASS = P * PACK
GROUPS = S // K_PASS
ALL_GROUPS = B * GROUPS
D_PASSES = D // K_PASS
BANK = 512
D_BANKS = D // BANK
LAST_PIECES = ((0, 512), (512, 768), (768, 1024))
WIDE_FROM = 14

FIRST_PARTS = 2
PREFETCH = 3
TURN_LEAD = 3
LEAKY_LAG = 2
SQUARE_LAG = 3
EXP_LAG = 9
WEIGHT_LAG = 14
OUT_LAG = 15

QUERY_PLACE = 3

HALVES = 2
HALF = D // HALVES
ALL_HALVES = ALL_GROUPS * HALVES
EARLY = {}
EARLY_COLS = 192
INV3 = 10
PACE_FROM = 1
LATE_MX = 1
LAST_PACE = 6
LATE = 9
V_LATE = 128
GPSIMD_FEATURES = {9: 192, 10: 384, 11: 192, 12: 384, 13: 384}
WOVEN = 256
FEWER_WOVEN = 256
FEWER_FROM = 13
EXTRA_AT = (9,)
PACE = 16
LOOP_EXPS = 4
RUN = 8
LATE_HALF = 20
LATE_SCALAR_COLS = 96
EARLY_SCALAR_COLS = 288
FIRST_WOVEN = 22
WOVEN_COLS = 256
SUM_COPIES = 128

HALF_LN2 = 0.5 * math.log(2.0)
CUBIC = math.sqrt(0.375)
SHRINK = 1.0 / (24.0 * SMOOTH) ** 2
CHAIN = 9
PAIR = 2
LINE = 4

FLOPS = 2 * 2 * B * Q * S * D


def tile_smcmr_pa_t_kernel(tc, query, context, out):
    nc = tc.nc
    with ExitStack() as stack:
        stack.enter_context(tc.manual_schedule())
        const = stack.enter_context(tc.tile_pool(name="const", bufs=1))
        token_pool = stack.enter_context(tc.tile_pool(name="tokens", bufs=9))
        stage = stack.enter_context(tc.tile_pool(name="stage", bufs=2))
        halves = stack.enter_context(tc.tile_pool(name="halves", bufs=2))
        codes = stack.enter_context(tc.tile_pool(name="codes", bufs=10))
        soft = stack.enter_context(tc.tile_pool(name="soft", bufs=8))
        small = stack.enter_context(tc.tile_pool(name="small", bufs=2))
        weight_pool = stack.enter_context(tc.tile_pool(name="weights", bufs=3))
        query_pool = stack.enter_context(tc.tile_pool(name="query", bufs=2))
        results = stack.enter_context(tc.tile_pool(name="results", bufs=4))
        psum_turn = stack.enter_context(tc.psum_pool(name="psum_turn", bufs=TURN_LEAD))
        psum_score = stack.enter_context(tc.psum_pool(name="psum_score", bufs=2))
        psum_sum = stack.enter_context(tc.psum_pool(name="psum_sum", bufs=1))
        psum_out = stack.enter_context(tc.psum_pool(name="psum_out", bufs=D_BANKS))
        unread = psum_out.tile([P, BANK], F32, tag="acc")
        unread_of = {0: unread}

        identity = const.tile([P, P], F32)
        make_identity(nc, identity[:])
        identity_bf16 = const.tile([P, P], BF16)
        nc.vector.tensor_copy(out=identity_bf16[:], in_=identity[:])
        q_codes = const.tile([P, B, D_PASSES, Q], U32, align_bytes=64)
        q_scales = const.tile([P, B, D_PASSES, Q], U8, align_bytes=64)

        rows_of, turned_of, grouped_of, token_codes_of, scores_of = {}, {}, {}, {}, {}
        damped_of, leaky_of, squares_of, steep_of = {}, {}, {}, {}
        norm_of, shifted_of, guess_of = {}, {}, {}
        pair_of, column_of, woven_of, total_of = {}, {}, {}, {}
        regrouped_of, weights_of, weight_codes_of = {}, {}, {}
        query_rows_of, query_grouped_of = {}, {}
        expo_of, sums_of, inverse_of, context_codes_of, acc_of = {}, {}, {}, {}, {}

        def is_group(i):
            return 0 <= i < ALL_GROUPS

        def turn(key, rows_words):
            turned = psum_turn.tile([P, D_PASSES, 2, P], F32)
            for c in range(D_PASSES):
                for u in range(2):
                    first = (2 * c + u) * P
                    nc.tensor.transpose(turned[:, c, u, :], rows_words[:, first : first + P], identity[:])
            turned_of[key] = turned

        def copy_turned(key, grouped_words):
            nc.scalar.copy(out=grouped_words, in_=turned_of[key][:].rearrange("p c u r -> p c r u"))

        turn_order = []
        for tile_number in range(PACK * ALL_GROUPS):
            for b in range(B):
                if tile_number == max(QUERY_PLACE, b * PACK * GROUPS - 1):
                    turn_order.append(("query", b))
            turn_order.append(("tile", tile_number))

        def turn_next(count):
            for kind, number in turn_order[count : count + 1]:
                if kind == "query":
                    turn((kind, number), query_rows_of[number][:].bitcast(F32))
                else:
                    i, j = divmod(number, PACK)
                    turn((kind, number), rows_of[i][:, j, :].bitcast(F32))

        def copy_query(b):
            q_grouped = stage.tile([P, D_PASSES, Q, PACK], BF16, align_bytes=64)
            copy_turned(("query", b), q_grouped[:].bitcast(F32))
            query_grouped_of[b] = q_grouped
            turn_next(turn_order.index(("query", b)) + TURN_LEAD)

        def copy_turned_tokens(i, j):
            if not is_group(i):
                return
            if j == 0:
                t_grouped = stage.tile([P, PACK, D_PASSES, P, PACK], BF16, align_bytes=64)
                grouped_of[i] = t_grouped
            place = turn_order.index(("tile", PACK * i + j))
            if place > 0 and turn_order[place - 1][0] == "query":
                copy_query(turn_order[place - 1][1])
            copy_turned(("tile", PACK * i + j), grouped_of[i][:, j].bitcast(F32))
            turn_next(place + TURN_LEAD)

        def load(i):
            if not is_group(i):
                return
            b, g = divmod(i, GROUPS)
            rows = token_pool.tile([P, PACK, D], BF16)
            source = context[b, g * K_PASS : (g + 1) * K_PASS, :].rearrange("(p j) d -> p j d", j=PACK)
            if i == 0:
                parts = [(0, 2, 0, D), (2, PACK, 0, HALF), (2, PACK, HALF, D)]
            elif i == 1:
                parts = [(0, 2, 0, D), (2, PACK, 0, D)]
            else:
                parts = [(0, PACK, 0, D)]
            for first_tile, end_tile, first, end in parts:
                nc.sync.dma_start(
                    out=rows[:, first_tile:end_tile, first:end], in_=source[:, first_tile:end_tile, first:end]
                )
            rows_of[i] = rows

        def quantise_tokens(i):
            if not is_group(i):
                return
            t_codes = stage.tile([P, PACK, D_PASSES, P], U32, align_bytes=64)
            t_scales = stage.tile([P, PACK, D_PASSES, P], U8, align_bytes=64)
            token_codes_of[i] = (t_codes, t_scales)
            nc.vector.quantize_mx(
                out=t_codes[:].rearrange("p j c r -> p (j c r)").bitcast(FP8X4),
                scales=t_scales[:].rearrange("p j c r -> p (j c r)"),
                in_=grouped_of[i][:].rearrange("p j c r t -> p (j c r t)"),
            )

        def first_matmul(i, pair):
            if not is_group(i):
                return
            b = i // GROUPS
            if pair == 0:
                scores = psum_score.tile([P, PACK, Q], F32)
                scores_of[i] = scores
            t_codes, t_scales = token_codes_of[i]
            for j in range(2 * pair, 2 * pair + 2):
                for c in range(D_PASSES):
                    nc.tensor.matmul_mx(
                        out=scores_of[i][:, j, :],
                        lhsT=t_codes[:, j, c, :].bitcast(FP8X4),
                        lhsT_scale=t_scales[:, j, c, :],
                        rhs=q_codes[:, b, c, :].bitcast(FP8X4),
                        rhs_scale=q_scales[:, b, c, :],
                        start=(c == 0),
                        stop=(c == D_PASSES - 1),
                    )

        def keep_pace(i, pair):
            t_codes, t_scales = token_codes_of[i]
            tiles = slice(2 * pair, 2 * pair + 2)
            nc.tensor.matmul_mx(
                out=unread_of[0][:],
                lhsT=q_codes[:, 0, 0, :].bitcast(FP8X4),
                lhsT_scale=q_scales[:, 0, 0, :],
                rhs=t_codes[:, tiles].rearrange("p j c r -> p (j c r)").bitcast(FP8X4),
                rhs_scale=t_scales[:, tiles].rearrange("p j c r -> p (j c r)"),
                start=True,
                stop=True,
            )

        def damp(i):
            if not is_group(i):
                return
            if i % PAIR == 0:
                pair = soft.tile([P, PACK, PAIR, Q], F32)
                pair_of[i // PAIR] = pair
            leaky_of[i] = pair_of[i // PAIR][:, :, i % PAIR, :]
            nc.scalar.mul(out=leaky_of[i], in_=scores_of[i][:], mul=SLOPE)

        def leaky_relu(i):
            if not is_group(i):
                return
            nc.vector.tensor_tensor(out=leaky_of[i], in0=scores_of[i][:], in1=leaky_of[i], op=ALU.max)

        def sum_squares(i, j):
            if not is_group(i):
                return
            column = PACK * (i % GROUPS) + j
            if column == 0:
                squares = small.tile([P, GROUPS * PACK], F32)
                squares_of[i // GROUPS] = squares
            unused = stage.tile([P, Q], F32, bufs=4)
            nc.scalar.activation(
                out=unused[:],
                in_=leaky_of[i][:, j, :],
                func=ACT.Square,
                accum_out=squares_of[i // GROUPS][:, column : column + 1],
            )

        def shift_squares(i):
            if not is_group(i) or i % GROUPS != GROUPS - 1:
                return
            shifted = small.tile([P, GROUPS * PACK], F32)
            nc.scalar.activation(
                out=shifted[:], in_=squares_of[i // GROUPS][:], func=ACT.Copy, scale=SHRINK, bias=EPS * SHRINK
            )
            shifted_of[i // GROUPS] = shifted

        def guess_root(i):
            if not is_group(i) or i % GROUPS != GROUPS - 1:
                return
            pair = i // GROUPS
            shifted = shifted_of[pair]
            guess = small.tile([P, GROUPS * PACK], F32)
            nc.scalar.activation(
                out=guess[:],
                in_=shifted[:].bitcast(U32),
                func=ACT.Exp,
                scale=-HALF_LN2 / 2**23,
                bias=HALF_LN2 * (127.0 - 0.043),
            )
            guess_of[pair] = guess

        def square_guess(i):
            if not is_group(i) or i % GROUPS != GROUPS - 1:
                return
            pair = i // GROUPS
            guess_squared = small.tile([P, GROUPS * PACK], F32)
            nc.scalar.activation(out=guess_squared[:], in_=guess_of[pair][:], func=ACT.Square, scale=math.sqrt(CUBIC))
            norm_of[pair] = (shifted_of[pair], guess_of[pair], guess_squared)

        def norm_step(i, k):
            if not is_group(i) or i % GROUPS != GROUPS - 1:
                return
            pair = i // GROUPS
            x, y, last = norm_of[pair]
            shape = [P, GROUPS * PACK]
            if k == 0:
                h = small.tile(shape, F32)
                nc.vector.tensor_tensor(out=h[:], in0=last[:], in1=x[:], op=ALU.mult)
                last = h
            elif k == 1:
                cubic = small.tile(shape, F32)
                nc.vector.scalar_tensor_tensor(
                    out=cubic[:], in0=last[:], scalar=-1.25 / CUBIC, in1=last[:], op0=ALU.add, op1=ALU.mult
                )
                last = cubic
            elif k == 2:
                better = small.tile(shape, F32)
                nc.vector.scalar_tensor_tensor(
                    out=better[:], in0=last[:], scalar=1.875, in1=y[:], op0=ALU.add, op1=ALU.mult
                )
                y = better
            elif k == 3:
                x_times_y = small.tile(shape, F32)
                nc.vector.tensor_tensor(out=x_times_y[:], in0=y[:], in1=x[:], op=ALU.mult)
                x = x_times_y
            elif k == 4:
                g = small.tile(shape, F32)
                nc.vector.scalar_tensor_tensor(
                    out=g[:], in0=x[:], scalar=3.0, in1=y[:], op0=ALU.mult, op1=ALU.mult
                )
                last = g
            elif k == 5:
                finer = small.tile(shape, F32)
                nc.vector.scalar_tensor_tensor(
                    out=finer[:], in0=last[:], scalar=-10.0, in1=last[:], op0=ALU.add, op1=ALU.mult
                )
                last = finer
            elif k == 6:
                root = small.tile(shape, F32)
                nc.vector.scalar_tensor_tensor(
                    out=root[:], in0=last[:], scalar=45.0, in1=x[:], op0=ALU.add, op1=ALU.mult
                )
                last = root
            elif k == 7:
                ninth = small.tile(shape, F32)
                nc.vector.tensor_scalar_add(out=ninth[:], in0=last[:], scalar1=EPS / SMOOTH)
                last = ninth
            else:
                steep = small.tile(shape, F32)
                nc.vector.reciprocal(out=steep[:], in_=last[:])
                steep_of[pair] = steep
            norm_of[pair] = (x, y, last)

        def exponentials(i, j):
            if not is_group(i):
                return
            b, g = divmod(i, GROUPS)
            column = PACK * (i % GROUPS) + j
            nc.scalar.activation(
                out=leaky_of[i][:, j, :],
                in_=leaky_of[i][:, j, :],
                func=ACT.Exp,
                scale=steep_of[i // GROUPS][:, column : column + 1],
                bias=-SMOOTH,
            )

        def add_to_sums(tile_number):
            i, j = divmod(tile_number, PACK)
            if not is_group(i):
                return
            b, g = divmod(i, GROUPS)
            if g == 0 and j == 0:
                sums = psum_sum.tile([P, P], F32)
                sums_of[b] = sums
            nc.tensor.matmul(
                out=sums_of[b][:],
                lhsT=leaky_of[i][:, j, :],
                rhs=identity[:],
                start=(g == 0 and j == 0),
                stop=(g == GROUPS - 1 and j == PACK - 1),
                is_transpose=True,
            )

        def regroup(i, engine_copy, first, last):
            if i not in regrouped_of:
                regrouped = halves.tile([P, D, PACK], BF16, align_bytes=64)
                regrouped_of[i] = regrouped
            engine_copy(
                out=regrouped_of[i][:, first:last, :].rearrange("p (n k) j -> p n j k", k=RUN),
                in_=rows_of[i][:, :, first:last].rearrange("p j (n k) -> p n j k", k=RUN),
            )

        def woven_features(i):
            return WOVEN if i < FEWER_FROM else FEWER_WOVEN

        def gpsimd_after(ap):
            seen = small.tile([P, 1], ap.dtype, tag="seen_f32" if ap.dtype == F32 else "seen_u32")
            nc.gpsimd.tensor_copy(out=seen[:], in_=ap)

        def regroup_on_gpsimd(i, first, last):
            if i not in regrouped_of:
                regrouped = halves.tile([P, D, PACK], BF16, align_bytes=64)
                regrouped_of[i] = regrouped
            first += vector_features(i)
            last += vector_features(i)
            nc.gpsimd.tensor_scalar(
                out=regrouped_of[i][:, first:last, :],
                in0=rows_of[i][:, :, first:last].rearrange("p j d -> p d j"),
                scalar1=1.0,
                scalar2=0.0,
                op0=ALU.mult,
                op1=ALU.add,
            )

        def weave(i):
            if LATE <= i < ALL_GROUPS and i not in woven_of:
                woven_of[i] = []
                features = BANK // PACK
                for m in range(woven_features(i) // features):
                    first = D - woven_features(i) + m * features
                    if m % D_BANKS == 0:
                        woven = psum_turn.tile([P, D_BANKS, BANK], BF16, tag="turned")
                        woven_of[i].append(woven)
                    nc.tensor.matmul(
                        out=woven[:, m % D_BANKS, :].rearrange("p (n k j) -> p n j k", k=RUN, j=PACK),
                        lhsT=identity_bf16[:],
                        rhs=rows_of[i][:, :, first : first + features].rearrange("p j (n k) -> p n j k", k=RUN),
                        start=True,
                        stop=True,
                    )

        def copy_woven(i):
            features = BANK // PACK
            for k, woven in enumerate(woven_of[i]):
                first = D - woven_features(i) + k * D_BANKS * features
                count = min(D_BANKS, (D - first) // features)
                nc.scalar.copy(
                    out=regrouped_of[i][:, first : first + count * features, :].rearrange("p d j -> p (d j)"),
                    in_=woven[:, 0:count, :].rearrange("p m c -> p (m c)"),
                )

        def quantise_context(i, first, last):
            if first == 0:
                c_codes = codes.tile([P, D], U32, align_bytes=64)
                c_scales = codes.tile([P, D], U8, align_bytes=64)
                context_codes_of[i] = (c_codes, c_scales)
            c_codes, c_scales = context_codes_of[i]
            nc.vector.quantize_mx(
                out=c_codes[:, first:last].bitcast(FP8X4),
                scales=c_scales[:, first:last],
                in_=regrouped_of[i][:, first:last, :].rearrange("p d j -> p (d j)"),
            )

        def total_sums(b):
            if 0 <= b < B:
                total = small.tile([P, 1], F32)
                nc.vector.reduce_sum(out=total[:], in_=sums_of[b][:], axis=mybir.AxisListType.X)
                total_of[b] = total

        def invert_sums(b):
            if 0 <= b < B:
                total_sums(b)
                column = small.tile([P, 1], F32)
                nc.vector.reciprocal(out=column[:], in_=total_of[b][:])
                column_of[b] = column

        def spread_inverse(b):
            if b == 0:
                inverse = psum_turn.tile([P, PAIR, Q], F32, tag="turned")
            else:
                inverse = psum_score.tile([P, PAIR, Q], F32, tag="scores")
            for g in range(PAIR):
                nc.tensor.transpose(inverse[:, g, :], column_of[b][:].to_broadcast([P, P]), identity[:])
            inverse_of[b] = inverse

        def normalise(k):
            b, half = divmod(k, GROUPS // PAIR)
            if half == 0:
                weights = weight_pool.tile([P, GROUPS // PAIR, PAIR, Q, PACK], BF16, align_bytes=64, bufs=2)
                weights_of[b] = weights
            nc.vector.tensor_tensor(
                out=weights_of[b][:, half].rearrange("p g (n k) j -> p (g n) j k", k=LINE),
                in0=pair_of[k][:].rearrange("p j g (n k) -> p (g n) j k", k=LINE),
                in1=inverse_of[b][:]
                .rearrange("p g (n k) -> p (g n) k", k=LINE)
                .unsqueeze(2)
                .to_broadcast([P, PAIR * Q // LINE, PACK, LINE]),
                op=ALU.mult,
            )

        def quantise_weights(b):
            w_codes = weight_pool.tile([P, GROUPS, Q], U32, align_bytes=64, bufs=3)
            w_scales = weight_pool.tile([P, GROUPS, Q], U8, align_bytes=64, bufs=3)
            nc.vector.quantize_mx(
                out=w_codes[:].rearrange("p g q -> p (g q)").bitcast(FP8X4),
                scales=w_scales[:].rearrange("p g q -> p (g q)"),
                in_=weights_of[b][:].rearrange("p h g q j -> p (h g q j)"),
            )
            weight_codes_of[b] = (w_codes, w_scales)

        def pieces(b):
            return LAST_PIECES if b == B - 1 else tuple((h * BANK, (h + 1) * BANK) for h in range(D_BANKS))

        def second_matmul(i, h):
            if not is_group(i):
                return
            b, g = divmod(i, GROUPS)
            w_codes, w_scales = weight_codes_of[b]
            c_codes, c_scales = context_codes_of[i]
            first, end = pieces(b)[h]
            if g == 0:
                if h < D_BANKS:
                    acc = psum_out.tile([P, BANK], F32, tag="acc")
                else:
                    acc = psum_score.tile([P, BANK], F32, tag="scores")
                acc_of[(b, h)] = acc
            nc.tensor.matmul_mx(
                out=acc_of[(b, h)][:, 0 : end - first],
                lhsT=w_codes[:, g, :].bitcast(FP8X4),
                lhsT_scale=w_scales[:, g, :],
                rhs=c_codes[:, first:end].bitcast(FP8X4),
                rhs_scale=c_scales[:, first:end],
                start=(g == 0),
                stop=(g == GROUPS - 1),
            )

        def store_piece(b, h):
            first, end = pieces(b)[h]
            result = results.tile([P, BANK], F32)
            copy = nc.vector.tensor_copy if b == B - 1 and h == 1 else nc.scalar.copy
            copy(out=result[:, 0 : end - first], in_=acc_of[(b, h)][:, 0 : end - first])
            nc.sync.dma_start(out=out[b, :, first:end], in_=result[:, 0 : end - first])

        def store(i):
            if not is_group(i) or i % GROUPS != GROUPS - 1:
                return
            b = i // GROUPS
            for h in range(len(pieces(b))):
                store_piece(b, h)

        def load_query(b):
            q_rows = query_pool.tile([P, D], BF16)
            nc.sync.dma_start(out=q_rows[:], in_=query[b])
            query_rows_of[b] = q_rows

        def quantise_query(b):
            nc.vector.quantize_mx(
                out=q_codes[:, b].rearrange("p c q -> p (c q)").bitcast(FP8X4),
                scales=q_scales[:, b].rearrange("p c q -> p (c q)"),
                in_=query_grouped_of[b][:].rearrange("p c q t -> p (c q t)"),
            )

        load(0)
        load_query(0)
        for i in range(1, PREFETCH):
            load(i)
        for count in range(TURN_LEAD):
            turn_next(count)

        done = {"regroup": 0, "quantise": 0, "scalar": 0}

        def next_regroup():
            i, h = divmod(done["regroup"], HALVES)
            if i < LATE and i < done["quantise"] // HALVES + 2:
                size = (D - EARLY_COLS if i in EARLY else D) // HALVES
                regroup(i, nc.vector.tensor_copy, h * size, (h + 1) * size)
                done["regroup"] += 1

        def next_quantise():
            i = done["quantise"] // HALVES
            if i < LATE and done["regroup"] >= HALVES * (i + 1):
                quantise_context(i, 0, D)
                done["quantise"] += HALVES

        def gpsimd_features(i):
            return GPSIMD_FEATURES.get(i, 0)

        def vector_features(i):
            return HALF if i >= WIDE_FROM else V_LATE

        def regroup_on_vector(i):
            regroup(i, nc.vector.tensor_copy, 0, vector_features(i))

        def regroup_on_scalar(i):
            regroup(i, nc.scalar.copy, vector_features(i) + gpsimd_features(i), D - woven_features(i))

        chain = []

        def tick():
            if chain:
                i, k = chain[0]
                norm_step(i, k)
                if k + 1 < CHAIN:
                    chain[0] = (i, k + 1)
                else:
                    chain.pop(0)

        next_regroup()
        for n in range(ALL_GROUPS):
            load(n + PREFETCH)
            if n % GROUPS == 1 and n // GROUPS + 1 < B:
                load_query(n // GROUPS + 1)
            late = n - 1 - SQUARE_LAG

            for i in EARLY:
                if n == EARLY[i]:
                    regroup(i, nc.scalar.copy, D - EARLY_COLS, D)
            copy_turned_tokens(n, 0)
            guess_root(late)
            if n == 1 or (n > 0 and n % GROUPS == 0):
                quantise_query(n // GROUPS)
                tick()
            quantise_tokens(n - 1)
            if n == 1:
                first_matmul(0, 0)
                first_matmul(0, 1)
            copy_turned_tokens(n, 1)
            square_guess(late)
            if n == WEIGHT_LAG:
                invert_sums(0)
            tick()
            next_regroup()
            if is_group(late) and late % GROUPS == GROUPS - 1:
                chain.append((late, 0))
            tick()
            damp(n - LEAKY_LAG)
            exponentials(n - EXP_LAG, 0)
            exponentials(n - EXP_LAG, 1)
            leaky_relu(n - LEAKY_LAG)
            tick()
            add_to_sums(PACK * (n - EXP_LAG - 1))
            add_to_sums(PACK * (n - EXP_LAG - 1) + 1)
            if n > 1:
                first_matmul(n - 1, 0)
                first_matmul(n - 1, 1)
            copy_turned_tokens(n, 2)
            exponentials(n - EXP_LAG, 2)
            exponentials(n - EXP_LAG, 3)
            copy_turned_tokens(n, 3)
            if n == 14:
                regroup_on_vector(LATE)
            if n > 0:
                next_quantise()
            tick()
            add_to_sums(PACK * (n - EXP_LAG - 1) + 2)
            add_to_sums(PACK * (n - EXP_LAG - 1) + 3)
            if PACE_FROM <= n < PACE:
                keep_pace(n - 1, 0)
                keep_pace(n - 1, 1)
            for j in range(PACK):
                sum_squares(n - SQUARE_LAG, j)
            if n in EXTRA_AT:
                next_regroup()
            shift_squares(n - SQUARE_LAG)

        n = ALL_GROUPS
        last = n - 1

        def all_exponentials(i):
            for j in range(PACK):
                exponentials(i, j)

        def all_sums(i):
            for j in range(PACK):
                add_to_sums(PACK * i + j)

        def all_squares(i):
            for j in range(PACK):
                sum_squares(i, j)

        def all_second(i):
            for h in range(len(pieces(i // GROUPS))):
                second_matmul(i, h)

        def hold_clock(passes):
            spare = psum_turn.tile([P, BANK], F32, tag="turned")
            unread_of[0] = spare
            for count in range(passes):
                keep_pace(last, count % 2)

        weave(LATE)
        spread_inverse(0)
        quantise_tokens(last)
        tick()
        damp(14)
        all_sums(6)
        first_matmul(last, 0)
        first_matmul(last, 1)
        all_squares(13)
        leaky_relu(14)
        gpsimd_after(leaky_of[14][:, 0, 0:1])
        regroup_on_gpsimd(9, 0, 192)
        regroup_on_gpsimd(10, 0, 192)
        tick()
        all_exponentials(7)
        all_sums(7)
        normalise(0)
        next_quantise()
        regroup_on_scalar(9)
        damp(last)
        normalise(1)
        tick()
        invert_sums(1)
        spread_inverse(1)
        hold_clock(3)
        all_squares(14)
        tick()
        leaky_relu(last)
        tick()
        quantise_weights(0)
        while chain:
            tick()
        gpsimd_after(weight_codes_of[0][0][:, 0, 0:1])
        regroup_on_gpsimd(10, 192, 384)
        copy_woven(9)
        weave(10)
        all_squares(last)
        shift_squares(last)
        normalise(2)
        exponentials(8, 0)
        exponentials(8, 1)
        guess_root(last)
        exponentials(8, 2)
        exponentials(8, 3)
        square_guess(last)
        for i in range(9, 12):
            all_exponentials(i)
        for i in range(8, 12):
            all_sums(i)
        chain.append((last, 0))
        tick()
        quantise_context(9, 0, D)
        regroup_on_gpsimd(11, 0, 192)
        tick()
        normalise(3)
        tick()
        for i in range(GROUPS):
            all_second(i)
        regroup_on_scalar(10)
        regroup_on_vector(10)
        tick()
        quantise_weights(1)
        tick()
        invert_sums(2)
        spread_inverse(2)
        tick()
        copy_woven(10)
        weave(11)
        regroup_on_vector(11)
        tick()
        quantise_context(10, 0, D)
        regroup_on_gpsimd(12, 0, 192)
        regroup_on_gpsimd(12, 192, 384)
        tick()
        normalise(4)
        normalise(5)
        while chain:
            tick()
        regroup_on_scalar(11)
        copy_woven(11)
        weave(12)
        store(3)
        all_second(4)
        all_second(5)
        quantise_context(11, 0, D)
        all_second(6)
        all_second(7)
        for i in range(12, 16):
            all_exponentials(i)
        for i in range(12, 16):
            all_sums(i)
        quantise_weights(2)
        regroup_on_vector(12)
        store(7)
        regroup_on_vector(13)
        invert_sums(3)
        gpsimd_after(column_of[3][:])
        regroup_on_gpsimd(13, 0, 192)
        regroup_on_gpsimd(13, 192, 384)
        spread_inverse(3)
        all_second(8)
        all_second(9)
        regroup_on_scalar(12)
        copy_woven(12)
        weave(13)
        normalise(6)
        normalise(7)
        all_second(10)
        quantise_context(12, 0, D)
        quantise_weights(3)
        all_second(11)
        regroup_on_scalar(13)
        copy_woven(13)
        weave(14)
        regroup_on_vector(14)
        store(11)
        all_second(12)
        quantise_context(13, 0, D)
        regroup_on_scalar(14)
        copy_woven(14)
        weave(15)
        regroup_on_vector(15)
        all_second(13)
        quantise_context(14, 0, HALF)
        quantise_context(15, 0, HALF)
        second_matmul(14, 0)
        second_matmul(15, 0)
        regroup_on_scalar(15)
        quantise_context(14, HALF, D)
        second_matmul(14, 1)
        second_matmul(14, 2)
        copy_woven(15)
        store_piece(B - 1, 0)
        quantise_context(15, 512, 768)
        second_matmul(15, 1)
        quantise_context(15, 768, 1024)
        second_matmul(15, 2)
        store_piece(B - 1, 1)
        store_piece(B - 1, 2)
        assert done["quantise"] == HALVES * LATE
